import numpy as np
import ml_dtypes


def mxq(x, axis, fmt="e4m3"):
    dtype, down = {"e4m3": (ml_dtypes.float8_e4m3fn, 7), "e5m2": (ml_dtypes.float8_e5m2, 14)}[fmt]
    v = np.moveaxis(np.asarray(x, np.float32).astype(ml_dtypes.bfloat16).astype(np.float64), axis, -1)
    blocks = v.reshape(v.shape[:-1] + (-1, 32))
    amax = np.abs(blocks).max(-1, keepdims=True)
    byte = np.maximum(np.where(amax > 0, np.frexp(amax)[1] - 1 + 127, 0) - down, 1)
    scale = np.exp2(byte - 127.0)
    codes = (blocks / scale).astype(np.float32).astype(dtype).astype(np.float64)
    return np.moveaxis((codes * scale).reshape(v.shape), -1, axis)


WIDE = False


def mx_kscale(k):
    if not WIDE:
        return np.ones(k)
    levels = np.array([10, -10, 5, -5, 0])
    a = np.random.permutation(np.resize(levels, k // 512 * 4)).reshape(k // 512, 4)
    idx = np.arange(k)
    return np.exp2(a[idx // 512, idx % 128 // 32])


BF16 = ml_dtypes.bfloat16


def bf(x):
    return np.asarray(x, np.float32).astype(BF16)


def f64(x):
    return np.asarray(x).astype(np.float64)


B, S, D, K, R = 4, 128, 512, 8192, 16
C = 1.0


def _artanh(x):
    return np.arctanh(np.clip(x, -1 + 1e-5, 1 - 1e-5))


def _expmap0(u, c=C):
    sc = np.sqrt(c)
    n = np.maximum(np.linalg.norm(u, axis=-1, keepdims=True), 1e-15)
    return np.tanh(sc * n) * u / (sc * n)


def _logmap0(x, c=C):
    sc = np.sqrt(c)
    n = np.maximum(np.linalg.norm(x, axis=-1, keepdims=True), 1e-15)
    return _artanh(sc * n) * x / (sc * n)


def _mobius_add(x, y, c=C):
    x2 = np.sum(x * x, -1, keepdims=True)
    y2 = np.sum(y * y, -1, keepdims=True)
    xy = np.sum(x * y, -1, keepdims=True)
    num = (1 + 2 * c * xy + c * y2) * x + (1 - c * x2) * y
    den = 1 + 2 * c * xy + c * c * x2 * y2
    return num / np.maximum(den, 1e-15)


def _mobius_matvec(M, x, c=C):
    sc = np.sqrt(c)
    xn = np.maximum(np.linalg.norm(x, axis=-1, keepdims=True), 1e-15)
    Mx = mxq(x, 1, "e4m3") @ mxq(M, 1, "e4m3").T
    Mxn = np.maximum(np.linalg.norm(Mx, axis=-1, keepdims=True), 1e-15)
    return np.tanh(Mxn / xn * _artanh(sc * xn)) * Mx / (sc * Mxn)


def _dist2_all(x, y, c=C):
    x2 = np.sum(x * x, -1)[:, None]
    y2 = np.sum(y * y, -1)[None, :]
    xy = mxq(x, 1, "e4m3") @ mxq(y, 1, "e4m3").T
    a = 1 - 2 * c * xy + c * y2
    b = 1 - c * x2
    den = 1 - 2 * c * xy + c * c * x2 * y2
    num2 = a * a * x2 - 2 * a * b * xy + b * b * y2
    norm = np.sqrt(np.maximum(num2, 0.0)) / np.maximum(den, 1e-15)
    d = (2.0 / np.sqrt(c)) * _artanh(np.sqrt(c) * norm)
    return d * d


def setup_inputs():
    s = mx_kscale(D)
    g = 1.0 / np.sqrt(np.mean(s * s))
    w0 = np.random.standard_normal((D, D)) / np.sqrt(D)
    lat = np.random.standard_normal((R, D))
    v0 = (np.random.standard_normal((B, S, R)) @ lat / np.sqrt(R) + np.random.standard_normal((B, S, D))) * np.sqrt(0.5)
    c0 = (np.random.standard_normal((K, R)) @ (lat @ w0.T) / np.sqrt(R) + np.random.standard_normal((K, D))) * np.sqrt(0.5)
    fb = np.log(np.random.uniform(size=K) * 1000.0 + 1.0)
    return {"v_tangent": bf(v0 * (0.6 / np.sqrt(D)) * s * g),
            "code_points": bf(_expmap0(c0 * (0.6 / np.sqrt(D)))),
            "W": bf(w0 / (s * g)[None, :]),
            "b": bf(np.random.standard_normal(D) * (0.3 / np.sqrt(D))),
            "freq_bias": bf((fb - fb.mean()) * 0.5),
            "temperature": bf(1.25 + 0.05 * np.random.standard_normal(1))}


def reference(v_tangent, code_points, W, b, freq_bias, temperature):
    v_tangent, code_points, W = f64(v_tangent), f64(code_points), f64(W)
    b, freq_bias, temperature = f64(b), f64(freq_bias), f64(temperature)
    batch_shape = v_tangent.shape[:-1]
    v = v_tangent.reshape(-1, v_tangent.shape[-1])
    p = _expmap0(v)
    p = _mobius_add(_mobius_matvec(W, p), _expmap0(b[None, :]))
    v = _logmap0(p)
    p = _expmap0(v)
    logits = -_dist2_all(p, code_points) / (temperature * temperature)
    logits = logits + freq_bias[None, :]
    return logits.reshape(*batch_shape, -1)

@@ -1,0 +1,477 @@
+from contextlib import ExitStack
+import math
+
+import concourse.mybir as mybir
+from concourse.masks import make_identity
+
+F32 = mybir.dt.float32
+BF16 = mybir.dt.bfloat16
+U32 = mybir.dt.uint32
+U8 = mybir.dt.uint8
+FP8X4 = mybir.dt.float8_e4m3fn_x4
+ALU = mybir.AluOpType
+AF = mybir.ActivationFunctionType
+
+P = 128
+D = 512
+ROWS = 512
+CODES = 8192
+UNIT = 512
+N_UNITS = CODES // UNIT
+TILES = 4
+GROUP = 4
+FLOPS = 2 * ROWS * D * D + 2 * ROWS * CODES * D
+
+CLIP = 1.0 - 1e-5
+ATANH_CLIP = 0.5 * math.log((1.0 + CLIP) / (1.0 - CLIP))
+T_MAX = CLIP * CLIP / (1.0 - CLIP * CLIP)
+TINY = 1e-15
+GAP_MIN = 1e-8
+COL = (0, 1, 8, 9)
+BCOL = 2
+
+RAW_BUFS = 6
+GRP_BUFS = 2
+ZB_BUFS = 6
+HEAD_UNITS = 6
+LOOKAHEAD = 2
+YS_ACT = (4, 4, 4, 4, 1, 1, 1, 1, 1, 1, 1, 1, 1, 1, 1, 1)
+EV_ENG = ("vv",) * 16
+HOOK_A = (0, 2, 1, 1, 1, 3, 3, 0, 0, 0, 0, 0)
+HOOK_V = (2, 2, 1, 1, 1, 3, 4, 1, 0, 0, 0, 0)
+PREFILL_AT = 2
+SLOT_A = (1, 0)
+SLOT_V = (3, 3)
+FB_ENG = "gggggggggggggvgv"
+
+
+def tile_hyperbolicdistancedecoder_kernel(tc, v_tangent, code_points, W, b, freq_bias, temperature, out):
+    nc = tc.nc
+    with ExitStack() as ctx:
+        const = ctx.enter_context(tc.tile_pool(name="const", bufs=1))
+        work = ctx.enter_context(tc.tile_pool(name="work", bufs=1))
+        psum = ctx.enter_context(tc.psum_pool(name="psum", bufs=1))
+        ctx.enter_context(tc.manual_schedule())
+
+        v_view = v_tangent.flatten_outer_dims().rearrange("(r p) d -> p r d", p=P)
+        w_view = W.rearrange("(t p) d -> p t d", p=P)
+        code_view = code_points.rearrange("(u t p) d -> u p t d", t=TILES, p=P)
+        out_view = out.flatten_outer_dims().rearrange("(r p) (u j) -> u p r j", p=P, j=UNIT)
+
+        def small(name, cols=16):
+            return const.tile([P, cols], F32, name=name)
+
+        ident = const.tile([P, P], F32, name="ident")
+        a2 = const.tile([P, ROWS], F32, name="a2")
+        b_bc = const.tile([P, D], BF16, name="b_bc")
+        t_bc = const.tile([P, 1], BF16, name="t_bc")
+        fb = const.tile([P, CODES], BF16, name="fb")
+        cw = const.tile([P, N_UNITS, UNIT], U32, name="cw", align_bytes=64)
+        cs = const.tile([P, N_UNITS, UNIT], U8, name="cs", align_bytes=64)
+        xw = const.tile([P, ROWS], U32, name="xw", align_bytes=64)
+        xs = const.tile([P, ROWS], U8, name="xs", align_bytes=64)
+        ww = const.tile([P, D], U32, name="ww", align_bytes=64)
+        ws = const.tile([P, D], U8, name="ws", align_bytes=64)
+        pw = const.tile([P, ROWS], U32, name="pw", align_bytes=64)
+        ps = const.tile([P, ROWS], U8, name="ps", align_bytes=64)
+        junk_a = const.tile([P, D], BF16, name="junk_a")
+        junk_v = const.tile([P, D], F32, name="junk_v")
+        ysum = const.tile([P, N_UNITS, 16], F32, name="ysum")
+        yh = const.tile([P, N_UNITS, 16], F32, name="yh")
+        gap = const.tile([P, N_UNITS, 16], F32, name="gap")
+        beta = const.tile([P, N_UNITS, 16], F32, name="beta")
+        nbeta = const.tile([P, N_UNITS, 16], F32, name="nbeta")
+        ombeta = const.tile([P, N_UNITS, 16], F32, name="ombeta")
+        zmax = const.tile([P, N_UNITS, 16], F32, name="zmax")
+
+        def ts(o, i, s1, s2, op0, op1):
+            nc.vector.tensor_scalar(out=o, in0=i, scalar1=s1, scalar2=s2, op0=op0, op1=op1)
+
+        def ts1(o, i, s1, op0):
+            nc.vector.tensor_scalar(out=o, in0=i, scalar1=s1, scalar2=None, op0=op0)
+
+        def stt(o, i0, s, i1, op0, op1):
+            nc.vector.scalar_tensor_tensor(out=o, in0=i0, scalar=s, in1=i1, op0=op0, op1=op1)
+
+        def tt(o, i0, i1, op):
+            nc.vector.tensor_tensor(out=o, in0=i0, in1=i1, op=op)
+
+        def sumsq(eng, src, acc):
+            if eng == "a":
+                nc.scalar.activation(out=junk_a[:], in_=src, func=AF.Square, accum_out=acc)
+            else:
+                nc.vector.scalar_tensor_tensor(out=junk_v[:], in0=src, scalar=1.0, in1=src, op0=ALU.mult, op1=ALU.mult, accum_out=acc)
+
+        def copy(eng, o, i):
+            if eng == "a":
+                nc.scalar.copy(out=o, in_=i)
+            else:
+                nc.vector.tensor_copy(out=o, in_=i)
+
+        def word_transposes(raw, half):
+            ct = psum.tile([P, 2, 2, P], F32, tag="ct", bufs=2, name="ct")
+            rawf = raw[:].rearrange("p t d -> p (t d)").bitcast(F32)
+            for i in range(2):
+                for uu in range(2):
+                    col = (2 * half + i) * (D // 2) + uu * P
+                    nc.tensor.transpose(ct[:, i, uu, :], rawf[:, col : col + P], ident[:])
+            return ct
+
+        def word_evac(eng, ct, grp, half):
+            dst = grp[:].bitcast(F32).rearrange("p (c u) -> p c u", u=2)[:, half * 2 * P : (half + 1) * 2 * P, :]
+            copy(eng, dst.rearrange("p (i c) u -> p i c u", i=2), ct[:].rearrange("p i u c -> p i c u"))
+
+        def new_grp():
+            return work.tile([P, 4 * UNIT], BF16, tag="grp", bufs=GRP_BUFS, name="grp", align_bytes=64)
+
+        def head_grp():
+            return work.tile([P, 4 * UNIT], BF16, tag="lq", bufs=GROUP, name="hgrp", align_bytes=64)
+
+        def quantise(grp, words, scales):
+            nc.vector.quantize_mx(out=words.bitcast(FP8X4), scales=scales, in_=grp[:])
+
+        def f32_transposes(src, r):
+            tp = psum.tile([P, 4, P], F32, tag="e", bufs=4, name="tp")
+            view = src[:, r, :].rearrange("p (u q e) -> p u e q", u=2, e=2)
+            for uu in range(2):
+                for ee in range(2):
+                    nc.tensor.transpose(tp[:, 2 * uu + ee, :], view[:, uu, ee, :], ident[:])
+            return tp
+
+        def f32_evac(eng, tp, grp, r):
+            dst = grp[:].rearrange("p (c k) -> p c k", k=4)[:, r * P : (r + 1) * P, :]
+            copy(eng, dst, tp[:].rearrange("p t c -> p c t"))
+
+        raws = {}
+        state = {"next_load": 0}
+
+        def load_next():
+            u = state["next_load"]
+            if u < N_UNITS:
+                raw = work.tile([P, TILES, D], BF16, tag="raw", bufs=RAW_BUFS, name="raw")
+                nc.sync.dma_start(out=raw[:], in_=code_view[u])
+                raws[u] = raw
+                state["next_load"] = u + 1
+
+        def ycol(u, t):
+            return t if t < YS_ACT[u] else 8 + t
+
+        def prep_pieces(u):
+            box = {}
+
+            def tr(half):
+                box[half] = word_transposes(raws[u], half)
+
+            def ev(half):
+                if half == 0:
+                    box["grp"] = new_grp()
+                word_evac(EV_ENG[u][half], box[half], box["grp"], half)
+
+            def ys(t):
+                c = ycol(u, t)
+                sumsq("a" if t < YS_ACT[u] else "v", raws[u][:, t, :], ysum[:, u, c : c + 1])
+
+            def qz():
+                quantise(box["grp"], cw[:, u, :], cs[:, u, :])
+
+            def sc():
+                while fifo_a and fifo_a[0][0] <= u:
+                    fifo_a.pop(0)[1]()
+                load_next()
+                y = ysum[:, u, :]
+                ts(yh[:, u, :], y, -0.5, -0.5, ALU.mult, ALU.add)
+                ts(gap[:, u, :], y, -1.0, 1.0, ALU.mult, ALU.add)
+                ts1(gap[:, u, :], gap[:, u, :], GAP_MIN, ALU.max)
+                nc.vector.reciprocal(out=beta[:, u, :], in_=gap[:, u, :])
+                ts1(nbeta[:, u, :], beta[:, u, :], -1.0, ALU.mult)
+                ts(ombeta[:, u, :], beta[:, u, :], -1.0, 1.0, ALU.mult, ALU.add)
+                ts(zmax[:, u, :], gap[:, u, :], T_MAX, 1.0, ALU.mult, ALU.add)
+
+            for t in range(TILES):
+                if t < YS_ACT[u]:
+                    fifo_a.append((u, lambda t=t: ys(t)))
+            seq = [lambda: tr(0), lambda: tr(1), lambda: ev(0), lambda: ev(1)]
+            for t in range(YS_ACT[u], TILES):
+                seq.append(lambda t=t: ys(t))
+            seq.extend([lambda: qz(), lambda: sc()])
+            for fn in seq:
+                fifo_v.append((u, fn))
+
+        fifo_a = []
+        fifo_v = []
+        for u in range(N_UNITS):
+            prep_pieces(u)
+
+        def fill_a(k):
+            for i in range(k):
+                if fifo_a:
+                    fifo_a.pop(0)[1]()
+
+        def fill_v(k):
+            for i in range(k):
+                if fifo_v:
+                    fifo_v.pop(0)[1]()
+
+        def hook(i):
+            fill_a(HOOK_A[i])
+            fill_v(HOOK_V[i])
+
+        def fill_to(u):
+            while fifo_v and fifo_v[0][0] <= u:
+                fifo_v.pop(0)[1]()
+
+        dummy = small("dummy", 1)
+        n2 = small("n2")
+        mx2 = small("mx2")
+        mb = small("mb")
+        nc.vector.memset(dummy[:], 1.0)
+        nc.vector.memset(n2[:], 1.0)
+        nc.vector.memset(mx2[:], 1.0)
+        nc.vector.memset(mb[:], 0.0)
+        nc.vector.memset(ysum[:].rearrange("p u c -> p (u c)"), 0.0)
+        rv = work.tile([P, TILES, D], BF16, tag="raw", bufs=RAW_BUFS, name="rv")
+        nc.sync.dma_start(out=rv[:], in_=v_view)
+        rw = work.tile([P, TILES, D], BF16, tag="raw", bufs=RAW_BUFS, name="rw")
+        nc.sync.dma_start(out=rw[:], in_=w_view)
+        nc.scalar.dma_start(out=b_bc[:], in_=b.partition_broadcast(P))
+        nc.scalar.dma_start(out=t_bc[:], in_=temperature.partition_broadcast(P))
+        for i in range(RAW_BUFS - 2):
+            load_next()
+        make_identity(nc, ident[:])
+        nc.gpsimd.dma_start(out=fb[:], in_=freq_bias.partition_broadcast(P))
+        nc.scalar.activation(out=dummy[:], in_=dummy[:], func=AF.Sqrt)
+
+        c2 = small("c2", 1)
+        tt(c2[:], t_bc[:], t_bc[:], ALU.mult)
+        nc.vector.reciprocal(out=c2[:], in_=c2[:])
+        ts1(c2[:], c2[:], 4.0, ALU.mult)
+
+        sumsq("a", b_bc[:], n2[:, BCOL : BCOL + 1])
+        sumsq("a", rv[:, 0, :], n2[:, COL[0] : COL[0] + 1])
+        sumsq("v", rv[:, 2, :], n2[:, COL[2] : COL[2] + 1])
+        sumsq("a", rv[:, 1, :], n2[:, COL[1] : COL[1] + 1])
+        sumsq("v", rv[:, 3, :], n2[:, COL[3] : COL[3] + 1])
+        nr = small("nr")
+        nn = small("nn")
+        th = small("th")
+        rn = small("rn")
+        sx = small("sx")
+        nc.scalar.activation(out=nr[:], in_=n2[:], func=AF.Sqrt)
+        ts1(nn[:], nr[:], TINY, ALU.max)
+        nc.scalar.activation(out=th[:], in_=nn[:], func=AF.Tanh)
+        nc.vector.reciprocal(out=rn[:], in_=nn[:])
+        wct0 = word_transposes(rw, 0)
+        wct1 = word_transposes(rw, 1)
+        wgrp = head_grp()
+        word_evac("v", wct0, wgrp, 0)
+        word_evac("v", wct1, wgrp, 1)
+        hook(0)
+        tt(sx[:], th[:], rn[:], ALU.mult)
+        x_all = work.tile([P, TILES, D], F32, tag="zb", bufs=ZB_BUFS, name="x_all")
+        for r, eng in ((0, "v"), (2, "a"), (1, "v"), (3, "a")):
+            c = COL[r]
+            if eng == "v":
+                ts1(x_all[:, r, :], rv[:, r, :], sx[:, c : c + 1], ALU.mult)
+            else:
+                nc.scalar.activation(out=x_all[:, r, :], in_=rv[:, r, :], func=AF.Copy, scale=sx[:, c : c + 1])
+        load_next()
+        load_next()
+        quantise(wgrp, ww[:], ws[:])
+        xgrp = head_grp()
+        tps = {}
+        for r in (0, 2, 1, 3):
+            tps[r] = f32_transposes(x_all, r)
+        at = small("at")
+        rho = small("rho")
+        y2 = small("y2", 1)
+        y2p1 = small("y2p1", 1)
+        ts1(at[:], nn[:], ATANH_CLIP, ALU.min)
+        ts1(rho[:], th[:], TINY, ALU.max)
+        nc.vector.reciprocal(out=rho[:], in_=rho[:])
+        tt(rho[:], rho[:], at[:], ALU.mult)
+        tt(y2[:], th[:, BCOL : BCOL + 1], th[:, BCOL : BCOL + 1], ALU.mult)
+        ts1(y2p1[:], y2[:], 1.0, ALU.add)
+        sb = sx[:, BCOL : BCOL + 1]
+        hook(1)
+        f32_evac("v", tps[0], xgrp, 0)
+        hook(2)
+        f32_evac("a", tps[2], xgrp, 2)
+        hook(3)
+        f32_evac("v", tps[1], xgrp, 1)
+        hook(4)
+        f32_evac("a", tps[3], xgrp, 3)
+        nc.scalar.activation(out=dummy[:], in_=dummy[:], func=AF.Sqrt)
+        hook(5)
+        quantise(xgrp, xw[:], xs[:])
+        mxs = {}
+        for r in range(TILES):
+            mx = psum.tile([P, D], F32, tag="e", bufs=4, name="mx")
+            nc.tensor.matmul_mx(
+                out=mx[:], lhsT=xw[:, r * P : (r + 1) * P].bitcast(FP8X4), lhsT_scale=xs[:, r * P : (r + 1) * P],
+                rhs=ww[:].bitcast(FP8X4), rhs_scale=ws[:], start=True, stop=True,
+            )
+            mxs[r] = mx
+        for r in range(TILES):
+            c = COL[r]
+            nc.scalar.activation(out=junk_a[:], in_=mxs[r][:], func=AF.Square, accum_out=mx2[:, c : c + 1])
+            mx_v = psum.tile([P, D], F32, tag="s", bufs=2, name="mx_v")
+            nc.tensor.matmul_mx(
+                out=mx_v[:], lhsT=xw[:, r * P : (r + 1) * P].bitcast(FP8X4), lhsT_scale=xs[:, r * P : (r + 1) * P],
+                rhs=ww[:].bitcast(FP8X4), rhs_scale=ws[:], start=True, stop=True,
+            )
+            nc.vector.scalar_tensor_tensor(
+                out=junk_v[:], in0=mx_v[:], scalar=1.0, in1=b_bc[:], op0=ALU.mult, op1=ALU.mult, accum_out=mb[:, c : c + 1]
+            )
+        mxn = small("mxn")
+        arg = small("arg")
+        tm = small("tm")
+        rm = small("rm")
+        w2 = small("w2")
+        nc.scalar.activation(out=mxn[:], in_=mx2[:], func=AF.Sqrt)
+        ts1(mxn[:], mxn[:], TINY, ALU.max)
+        tt(arg[:], mxn[:], rho[:], ALU.mult)
+        nc.scalar.activation(out=tm[:], in_=arg[:], func=AF.Tanh)
+        nc.scalar.activation(out=dummy[:], in_=dummy[:], func=AF.Sqrt)
+        nc.vector.reciprocal(out=rm[:], in_=mxn[:])
+        stt(w2[:], mb[:], sb, rm[:], ALU.mult, ALU.mult)
+        hook(6)
+        x2 = small("x2")
+        xy2 = small("xy2")
+        den = small("den")
+        num = small("num")
+        qn2 = small("qn2")
+        qn = small("qn")
+        tt(x2[:], tm[:], tm[:], ALU.mult)
+        stt(xy2[:], tm[:], 2.0, w2[:], ALU.mult, ALU.mult)
+        stt(den[:], x2[:], y2[:], xy2[:], ALU.mult, ALU.add)
+        ts(den[:], den[:], 1.0, TINY, ALU.add, ALU.max)
+        nc.vector.reciprocal(out=den[:], in_=den[:])
+        stt(num[:], x2[:], y2[:], xy2[:], ALU.add, ALU.add)
+        stt(qn2[:], num[:], 0.0, den[:], ALU.max, ALU.mult)
+        nc.scalar.activation(out=qn[:], in_=qn2[:], func=AF.Sqrt)
+        g1 = small("g1")
+        g2 = small("g2")
+        aa = small("aa")
+        tt(g1[:], tm[:], rm[:], ALU.mult)
+        tt(g1[:], g1[:], den[:], ALU.mult)
+        ts1(aa[:], xy2[:], y2p1[:], ALU.add)
+        tt(g1[:], g1[:], aa[:], ALU.mult)
+        ts(g2[:], x2[:], -1.0, 1.0, ALU.mult, ALU.add)
+        stt(g2[:], g2[:], sb, den[:], ALU.mult, ALU.mult)
+        ff = small("ff")
+        ts1(ff[:], qn[:], TINY, ALU.max)
+        nc.vector.reciprocal(out=ff[:], in_=ff[:])
+        ts(ff[:], ff[:], CLIP, 1.0, ALU.mult, ALU.min)
+        p1 = small("p1")
+        p2 = small("p2")
+        tt(p2[:], g2[:], ff[:], ALU.mult)
+        tt(p1[:], g1[:], ff[:], ALU.mult)
+        tmp = work.tile([P, TILES, D], F32, tag="a", bufs=GROUP, name="tmp")
+        p_all = work.tile([P, TILES, D], F32, tag="zb", bufs=ZB_BUFS, name="p_all")
+        pgrp = head_grp()
+        for r in range(TILES):
+            c = COL[r]
+            nc.scalar.activation(out=tmp[:, r, :], in_=b_bc[:], func=AF.Copy, scale=p2[:, c : c + 1])
+            stt(p_all[:, r, :], mxs[r][:], p1[:, c : c + 1], tmp[:, r, :], ALU.mult, ALU.add)
+            tps[r] = f32_transposes(p_all, r)
+        a2c = small("a2c")
+        ts(a2c[:], qn2[:], CLIP * CLIP, -1.0, ALU.min, ALU.mult)
+        ts1(a2c[:], a2c[:], 1.0, ALU.add)
+        nc.vector.reciprocal(out=a2c[:], in_=a2c[:])
+        ts1(a2c[:], a2c[:], -2.0, ALU.mult)
+        a2p = psum.tile([P, ROWS], F32, tag="s", bufs=2, name="a2p")
+        for r in range(TILES):
+            c = COL[r]
+            nc.tensor.matmul(out=a2p[:, r * P : (r + 1) * P], lhsT=a2c[:, c : c + 1].to_broadcast([P, P]), rhs=ident[:], start=True, stop=True)
+        f32_evac("v", tps[0], pgrp, 0)
+        f32_evac("a", tps[1], pgrp, 1)
+        f32_evac("v", tps[2], pgrp, 2)
+        f32_evac("a", tps[3], pgrp, 3)
+        copy("a", a2[:], a2p[:])
+        hook(7)
+        quantise(pgrp, pw[:], ps[:])
+
+        zbs = {}
+        aas = {}
+        lqs = {}
+        es = {}
+
+        def front(u):
+            fill_to(u)
+            zb = work.tile([P, TILES, ROWS], F32, tag="zb", bufs=ZB_BUFS, name="zb")
+            zbs[u] = zb
+            for t in range(TILES):
+                c = ycol(u, t)
+                s = psum.tile([P, ROWS], F32, tag="s", bufs=2, name="s")
+                nc.tensor.matmul_mx(
+                    out=s[:], lhsT=cw[:, u, t * P : (t + 1) * P].bitcast(FP8X4), lhsT_scale=cs[:, u, t * P : (t + 1) * P],
+                    rhs=pw[:].bitcast(FP8X4), rhs_scale=ps[:], start=True, stop=True,
+                )
+                stt(zb[:, t, :], s[:], yh[:, u, c : c + 1], a2[:], ALU.add, ALU.mult)
+                nc.gpsimd.tensor_scalar(out=zb[:, t, :], in0=zb[:, t, :], scalar1=zmax[:, u, c : c + 1], scalar2=1.0, op0=ALU.min, op1=ALU.max)
+
+        def roots(u):
+            a = work.tile([P, TILES, ROWS], F32, tag="a", bufs=GROUP, name="a")
+            aas[u] = a
+            zb = zbs[u]
+            for t in range(TILES):
+                c = ycol(u, t)
+                nc.scalar.activation(out=a[:, t, :], in_=zb[:, t, :], func=AF.Sqrt, scale=beta[:, u, c : c + 1], bias=nbeta[:, u, c : c + 1])
+                nc.scalar.activation(out=zb[:, t, :], in_=zb[:, t, :], func=AF.Sqrt, scale=beta[:, u, c : c + 1], bias=ombeta[:, u, c : c + 1])
+
+        def add_t(u, r):
+            e = psum.tile([P, UNIT], F32, tag="e", bufs=4, name="e")
+            es[(u, r)] = e
+            for t in range(TILES):
+                o = e[:, t * P : (t + 1) * P]
+                nc.tensor.matmul(out=o, lhsT=aas[u][:, t, r * P : (r + 1) * P], rhs=ident[:], start=True, stop=False, is_transpose=True)
+                nc.tensor.matmul(out=o, lhsT=zbs[u][:, t, r * P : (r + 1) * P], rhs=ident[:], start=False, stop=True, is_transpose=True)
+
+        def log_r(u, r):
+            if r == 0:
+                lqs[u] = work.tile([P, TILES, UNIT], F32, tag="lq", bufs=GROUP, name="lq", align_bytes=64)
+            nc.scalar.activation(out=lqs[u][:, r, :], in_=es[(u, r)][:], func=AF.Ln)
+
+        def finish(u):
+            lq = lqs[u]
+            flat = lq[:].rearrange("p r j -> p (r j)")
+            stt(flat, flat, c2[:], flat, ALU.mult, ALU.mult)
+            fbu = fb[:, u * UNIT : (u + 1) * UNIT].unsqueeze(1).to_broadcast([P, TILES, UNIT])
+            if FB_ENG[u] == "g":
+                nc.gpsimd.tensor_tensor(out=lq[:], in0=fbu, in1=lq[:], op=ALU.subtract)
+            else:
+                tt(lq[:], fbu, lq[:], ALU.subtract)
+            nc.sync.dma_start(out=out_view[u], in_=lq[:])
+
+        def finish_r(u, r):
+            part = lqs[u][:, r, :]
+            stt(part, part, c2[:], part, ALU.mult, ALU.mult)
+            tt(part, fb[:, u * UNIT : (u + 1) * UNIT], part, ALU.subtract)
+            nc.sync.dma_start(out=out_view[u][:, r, :], in_=part)
+
+        for u in range(LOOKAHEAD):
+            front(u)
+        for g in range(N_UNITS // GROUP):
+            first = g * GROUP
+            for i in range(GROUP):
+                u = first + i
+                if i == PREFILL_AT:
+                    for r in range(TILES):
+                        add_t(first, r)
+                if u + LOOKAHEAD < N_UNITS:
+                    front(u + LOOKAHEAD)
+                roots(u)
+                fill_a(SLOT_A[0])
+                fill_v(SLOT_V[0])
+            for i in range(GROUP):
+                u = first + i
+                for r in range(TILES):
+                    log_r(u, r)
+                    if i + 1 < GROUP:
+                        add_t(u + 1, r)
+                    if u == N_UNITS - 1:
+                        finish_r(u, r)
+                if u < N_UNITS - 1:
+                    finish(u)
+                fill_a(SLOT_A[1])
+                fill_v(SLOT_V[1])

@@ -35,14 +35,17 @@ GRP_BUFS = 2
 ZB_BUFS = 6
 HEAD_UNITS = 6
 LOOKAHEAD = 2
-YS_ACT = (4, 4, 4, 4, 1, 1, 1, 1, 1, 1, 1, 1, 1, 1, 1, 1)
+YS_ACT = (4, 4, 4, 4, 2, 2, 2, 2, 2, 2, 2, 2, 2, 2, 2, 2)
 EV_ENG = ("vv",) * 16
 HOOK_A = (0, 2, 1, 1, 1, 3, 3, 0, 0, 0, 0, 0)
 HOOK_V = (2, 2, 1, 1, 1, 3, 4, 1, 0, 0, 0, 0)
 PREFILL_AT = 2
-SLOT_A = (1, 0)
+SLOT_A = (1, 1)
 SLOT_V = (3, 3)
-FB_ENG = "gggggggggggggvgv"
+FORM = "tttttttttttttttt"
+FB_ENG = "ggggggggggggvgvv"
+CL_ENG = "vvvvvvvvvvvvvvvv"
+SQ_ENG = "vvvvvvvvvvvvvvvv"
 
 
 def tile_hyperbolicdistancedecoder_kernel(tc, v_tangent, code_points, W, b, freq_bias, temperature, out):
@@ -183,8 +186,12 @@ def tile_hyperbolicdistancedecoder_kernel(tc, v_tangent, code_points, W, b, freq
                 ts(gap[:, u, :], y, -1.0, 1.0, ALU.mult, ALU.add)
                 ts1(gap[:, u, :], gap[:, u, :], GAP_MIN, ALU.max)
                 nc.vector.reciprocal(out=beta[:, u, :], in_=gap[:, u, :])
-                ts1(nbeta[:, u, :], beta[:, u, :], -1.0, ALU.mult)
-                ts(ombeta[:, u, :], beta[:, u, :], -1.0, 1.0, ALU.mult, ALU.add)
+                if FORM[u] == "t":
+                    ts1(nbeta[:, u, :], beta[:, u, :], -1.0, ALU.mult)
+                    ts(ombeta[:, u, :], beta[:, u, :], -1.0, 1.0, ALU.mult, ALU.add)
+                else:
+                    ts1(nbeta[:, u, :], beta[:, u, :], 2.0, ALU.mult)
+                    ts(ombeta[:, u, :], beta[:, u, :], -2.0, 1.0, ALU.mult, ALU.add)
                 ts(zmax[:, u, :], gap[:, u, :], T_MAX, 1.0, ALU.mult, ALU.add)
 
             for t in range(TILES):
@@ -245,6 +252,16 @@ def tile_hyperbolicdistancedecoder_kernel(tc, v_tangent, code_points, W, b, freq
         tt(c2[:], t_bc[:], t_bc[:], ALU.mult)
         nc.vector.reciprocal(out=c2[:], in_=c2[:])
         ts1(c2[:], c2[:], 4.0, ALU.mult)
+        c2m = small("c2m", 1)
+        ts1(c2m[:], c2[:], 0.25, ALU.mult)
+        neg1 = small("neg1", 1)
+        nc.vector.memset(neg1[:], -1.0)
+        c1 = small("c1", 1)
+        nc.vector.tensor_copy(out=c1[:], in_=t_bc[:])
+        nc.vector.reciprocal(out=c1[:], in_=c1[:])
+        c1m = small("c1m", 1)
+        nc.vector.tensor_copy(out=c1m[:], in_=c1[:])
+        ts1(c1[:], c1[:], 2.0, ALU.mult)
 
         sumsq("a", b_bc[:], n2[:, BCOL : BCOL + 1])
         sumsq("a", rv[:, 0, :], n2[:, COL[0] : COL[0] + 1])
@@ -396,6 +413,14 @@ def tile_hyperbolicdistancedecoder_kernel(tc, v_tangent, code_points, W, b, freq
         lqs = {}
         es = {}
 
+        def clip(u, t):
+            c = ycol(u, t)
+            part = zbs[u][:, t, :]
+            if CL_ENG[u] == "g":
+                nc.gpsimd.tensor_scalar(out=part, in0=part, scalar1=zmax[:, u, c : c + 1], scalar2=1.0, op0=ALU.min, op1=ALU.max)
+            else:
+                ts(part, part, zmax[:, u, c : c + 1], 1.0, ALU.min, ALU.max)
+
         def front(u):
             fill_to(u)
             zb = work.tile([P, TILES, ROWS], F32, tag="zb", bufs=ZB_BUFS, name="zb")
@@ -408,16 +433,32 @@ def tile_hyperbolicdistancedecoder_kernel(tc, v_tangent, code_points, W, b, freq
                     rhs=pw[:].bitcast(FP8X4), rhs_scale=ps[:], start=True, stop=True,
                 )
                 stt(zb[:, t, :], s[:], yh[:, u, c : c + 1], a2[:], ALU.add, ALU.mult)
-                nc.gpsimd.tensor_scalar(out=zb[:, t, :], in0=zb[:, t, :], scalar1=zmax[:, u, c : c + 1], scalar2=1.0, op0=ALU.min, op1=ALU.max)
+                if t > 0:
+                    clip(u, t - 1)
+            clip(u, TILES - 1)
 
         def roots(u):
+            zb = zbs[u]
+            if FORM[u] == "t":
+                a = work.tile([P, TILES, ROWS], F32, tag="a", bufs=GROUP, name="a")
+                aas[u] = a
+                for t in range(TILES):
+                    c = ycol(u, t)
+                    nc.scalar.activation(out=a[:, t, :], in_=zb[:, t, :], func=AF.Sqrt, scale=beta[:, u, c : c + 1], bias=nbeta[:, u, c : c + 1])
+                    nc.scalar.activation(out=zb[:, t, :], in_=zb[:, t, :], func=AF.Sqrt, scale=beta[:, u, c : c + 1], bias=ombeta[:, u, c : c + 1])
+            else:
+                af = aas[u][:].rearrange("p t i -> p (t i)")
+                nc.scalar.activation(out=af, in_=af, func=AF.Sqrt, bias=neg1[:])
+
+        def cosh_form(u):
+            zb = zbs[u]
             a = work.tile([P, TILES, ROWS], F32, tag="a", bufs=GROUP, name="a")
             aas[u] = a
-            zb = zbs[u]
             for t in range(TILES):
                 c = ycol(u, t)
-                nc.scalar.activation(out=a[:, t, :], in_=zb[:, t, :], func=AF.Sqrt, scale=beta[:, u, c : c + 1], bias=nbeta[:, u, c : c + 1])
-                nc.scalar.activation(out=zb[:, t, :], in_=zb[:, t, :], func=AF.Sqrt, scale=beta[:, u, c : c + 1], bias=ombeta[:, u, c : c + 1])
+                ts(zb[:, t, :], zb[:, t, :], nbeta[:, u, c : c + 1], ombeta[:, u, c : c + 1], ALU.mult, ALU.add)
+            zf = zb[:].rearrange("p t i -> p (t i)")
+            stt(a[:].rearrange("p t i -> p (t i)"), zf, 1.0, zf, ALU.mult, ALU.mult)
 
         def add_t(u, r):
             e = psum.tile([P, UNIT], F32, tag="e", bufs=4, name="e")
@@ -435,7 +476,10 @@ def tile_hyperbolicdistancedecoder_kernel(tc, v_tangent, code_points, W, b, freq
         def finish(u):
             lq = lqs[u]
             flat = lq[:].rearrange("p r j -> p (r j)")
-            stt(flat, flat, c2[:], flat, ALU.mult, ALU.mult)
+            if SQ_ENG[u] == "a":
+                nc.scalar.activation(out=flat, in_=flat, func=AF.Square, scale=(c1 if FORM[u] == "t" else c1m)[:])
+            else:
+                stt(flat, flat, (c2 if FORM[u] == "t" else c2m)[:], flat, ALU.mult, ALU.mult)
             fbu = fb[:, u * UNIT : (u + 1) * UNIT].unsqueeze(1).to_broadcast([P, TILES, UNIT])
             if FB_ENG[u] == "g":
                 nc.gpsimd.tensor_tensor(out=lq[:], in0=fbu, in1=lq[:], op=ALU.subtract)
@@ -445,7 +489,7 @@ def tile_hyperbolicdistancedecoder_kernel(tc, v_tangent, code_points, W, b, freq
 
         def finish_r(u, r):
             part = lqs[u][:, r, :]
-            stt(part, part, c2[:], part, ALU.mult, ALU.mult)
+            stt(part, part, (c2 if FORM[u] == "t" else c2m)[:], part, ALU.mult, ALU.mult)
             tt(part, fb[:, u * UNIT : (u + 1) * UNIT], part, ALU.subtract)
             nc.sync.dma_start(out=out_view[u][:, r, :], in_=part)
 
@@ -461,6 +505,8 @@ def tile_hyperbolicdistancedecoder_kernel(tc, v_tangent, code_points, W, b, freq
                 if u + LOOKAHEAD < N_UNITS:
                     front(u + LOOKAHEAD)
                 roots(u)
+                if u + 1 < N_UNITS and FORM[u + 1] == "m":
+                    cosh_form(u + 1)
                 fill_a(SLOT_A[0])
                 fill_v(SLOT_V[0])
             for i in range(GROUP):

@@ -43,7 +43,7 @@ PREFILL_AT = 2
 SLOT_A = (1, 1)
 SLOT_V = (3, 3)
 FORM = "tttttttttttttttt"
-FB_ENG = "ggggggggggggvgvv"
+FB_ENG = "vvvvvvvvvvvvvvvv"
 CL_ENG = "vvvvvvvvvvvvvvvv"
 SQ_ENG = "vvvvvvvvvvvvvvvv"
 

@@ -31,21 +31,22 @@ COL = (0, 1, 8, 9)
 BCOL = 2
 
 RAW_BUFS = 6
+CW_BUFS = 6
 GRP_BUFS = 2
 ZB_BUFS = 6
-HEAD_UNITS = 6
+HEAD_UNITS = 4
 LOOKAHEAD = 2
-YS_ACT = (4, 4, 4, 4, 2, 2, 2, 2, 2, 2, 2, 2, 2, 2, 2, 2)
+YS_ACT = (4, 4, 4, 4, 4, 4, 4, 4, 4, 4, 4, 4, 4, 4, 4, 4)
 EV_ENG = ("vv",) * 16
-HOOK_A = (0, 2, 1, 1, 1, 3, 3, 0, 0, 0, 0, 0)
-HOOK_V = (2, 2, 1, 1, 1, 3, 4, 1, 0, 0, 0, 0)
-PREFILL_AT = 2
-SLOT_A = (1, 1)
-SLOT_V = (3, 3)
+PREFILL_AT = 1
+LN_FILL = 0
+SLOT_A = (1, 0)
+SLOT_V = (3, 2)
 FORM = "tttttttttttttttt"
+ADD_ENG = "pppppppppvvvpvvv"
 FB_ENG = "vvvvvvvvvvvvvvvv"
 CL_ENG = "vvvvvvvvvvvvvvvv"
-SQ_ENG = "vvvvvvvvvvvvvvvv"
+SQ_ENG = "vvvvvvvvvvvvvava"
 
 
 def tile_hyperbolicdistancedecoder_kernel(tc, v_tangent, code_points, W, b, freq_bias, temperature, out):
@@ -54,7 +55,6 @@ def tile_hyperbolicdistancedecoder_kernel(tc, v_tangent, code_points, W, b, freq
         const = ctx.enter_context(tc.tile_pool(name="const", bufs=1))
         work = ctx.enter_context(tc.tile_pool(name="work", bufs=1))
         psum = ctx.enter_context(tc.psum_pool(name="psum", bufs=1))
-        ctx.enter_context(tc.manual_schedule())
 
         v_view = v_tangent.flatten_outer_dims().rearrange("(r p) d -> p r d", p=P)
         w_view = W.rearrange("(t p) d -> p t d", p=P)
@@ -69,8 +69,8 @@ def tile_hyperbolicdistancedecoder_kernel(tc, v_tangent, code_points, W, b, freq
         b_bc = const.tile([P, D], BF16, name="b_bc")
         t_bc = const.tile([P, 1], BF16, name="t_bc")
         fb = const.tile([P, CODES], BF16, name="fb")
-        cw = const.tile([P, N_UNITS, UNIT], U32, name="cw", align_bytes=64)
-        cs = const.tile([P, N_UNITS, UNIT], U8, name="cs", align_bytes=64)
+        cws = {}
+        css = {}
         xw = const.tile([P, ROWS], U32, name="xw", align_bytes=64)
         xs = const.tile([P, ROWS], U8, name="xs", align_bytes=64)
         ww = const.tile([P, D], U32, name="ww", align_bytes=64)
@@ -175,7 +175,9 @@ def tile_hyperbolicdistancedecoder_kernel(tc, v_tangent, code_points, W, b, freq
                 sumsq("a" if t < YS_ACT[u] else "v", raws[u][:, t, :], ysum[:, u, c : c + 1])
 
             def qz():
-                quantise(box["grp"], cw[:, u, :], cs[:, u, :])
+                cws[u] = work.tile([P, UNIT], U32, tag="cw", bufs=CW_BUFS, name="cw", align_bytes=64)
+                css[u] = work.tile([P, UNIT], U8, tag="cs", bufs=CW_BUFS, name="cs", align_bytes=64)
+                quantise(box["grp"], cws[u][:], css[u][:])
 
             def sc():
                 while fifo_a and fifo_a[0][0] <= u:
@@ -211,7 +213,7 @@ def tile_hyperbolicdistancedecoder_kernel(tc, v_tangent, code_points, W, b, freq
 
         def fill_a(k):
             for i in range(k):
-                if fifo_a:
+                if fifo_a and fifo_a[0][0] < state["next_load"]:
                     fifo_a.pop(0)[1]()
 
         def fill_v(k):
@@ -219,22 +221,20 @@ def tile_hyperbolicdistancedecoder_kernel(tc, v_tangent, code_points, W, b, freq
                 if fifo_v:
                     fifo_v.pop(0)[1]()
 
-        def hook(i):
-            fill_a(HOOK_A[i])
-            fill_v(HOOK_V[i])
-
         def fill_to(u):
             while fifo_v and fifo_v[0][0] <= u:
                 fifo_v.pop(0)[1]()
 
-        dummy = small("dummy", 1)
         n2 = small("n2")
         mx2 = small("mx2")
         mb = small("mb")
-        nc.vector.memset(dummy[:], 1.0)
+        tm = small("tm")
+        warm = small("warm", 1)
+        nc.vector.memset(warm[:], 1.0)
         nc.vector.memset(n2[:], 1.0)
         nc.vector.memset(mx2[:], 1.0)
         nc.vector.memset(mb[:], 0.0)
+        nc.vector.memset(tm[:], 0.0)
         nc.vector.memset(ysum[:].rearrange("p u c -> p (u c)"), 0.0)
         rv = work.tile([P, TILES, D], BF16, tag="raw", bufs=RAW_BUFS, name="rv")
         nc.sync.dma_start(out=rv[:], in_=v_view)
@@ -246,7 +246,137 @@ def tile_hyperbolicdistancedecoder_kernel(tc, v_tangent, code_points, W, b, freq
             load_next()
         make_identity(nc, ident[:])
         nc.gpsimd.dma_start(out=fb[:], in_=freq_bias.partition_broadcast(P))
-        nc.scalar.activation(out=dummy[:], in_=dummy[:], func=AF.Sqrt)
+        nc.scalar.activation(out=warm[:], in_=warm[:], func=AF.Sqrt)
+
+        sumsq("a", b_bc[:], n2[:, BCOL : BCOL + 1])
+        sumsq("a", rv[:, 0, :], n2[:, COL[0] : COL[0] + 1])
+        sumsq("v", rv[:, 2, :], n2[:, COL[2] : COL[2] + 1])
+        sumsq("a", rv[:, 1, :], n2[:, COL[1] : COL[1] + 1])
+        sumsq("v", rv[:, 3, :], n2[:, COL[3] : COL[3] + 1])
+        nr = small("nr")
+        nn = small("nn")
+        th = small("th")
+        rn = small("rn")
+        sx = small("sx")
+        nc.scalar.activation(out=nr[:], in_=n2[:], func=AF.Sqrt)
+        nc.scalar.activation(out=th[:], in_=nr[:], func=AF.Tanh)
+        warm2 = small("warm2", 1)
+        nc.scalar.activation(out=warm2[:], in_=th[:, 0:1], func=AF.Sqrt)
+        ts1(nn[:], nr[:], TINY, ALU.max)
+        nc.vector.reciprocal(out=rn[:], in_=nn[:])
+        tt(sx[:], th[:], rn[:], ALU.mult)
+        x_all = work.tile([P, TILES, D], F32, tag="zb", bufs=ZB_BUFS, name="x_all")
+        tps = {}
+        for r in range(TILES):
+            c = COL[r]
+            ts1(x_all[:, r, :], rv[:, r, :], sx[:, c : c + 1], ALU.mult)
+            tps[r] = f32_transposes(x_all, r)
+        xgrp = head_grp()
+        for r in range(TILES):
+            f32_evac("av"[r % 2], tps[r], xgrp, r)
+        wct0 = word_transposes(rw, 0)
+        wct1 = word_transposes(rw, 1)
+        wgrp = head_grp()
+        word_evac("v", wct0, wgrp, 0)
+        word_evac("a", wct1, wgrp, 1)
+        load_next()
+        load_next()
+        quantise(wgrp, ww[:], ws[:])
+        quantise(xgrp, xw[:], xs[:])
+        mxs = {}
+        for r in range(TILES):
+            c = COL[r]
+            mx = psum.tile([P, D], F32, tag="e", bufs=4, name="mx")
+            nc.tensor.matmul_mx(
+                out=mx[:], lhsT=xw[:, r * P : (r + 1) * P].bitcast(FP8X4), lhsT_scale=xs[:, r * P : (r + 1) * P],
+                rhs=ww[:].bitcast(FP8X4), rhs_scale=ws[:], start=True, stop=True,
+            )
+            mxs[r] = mx
+            nc.scalar.activation(out=junk_a[:], in_=mx[:], func=AF.Square, accum_out=mx2[:, c : c + 1])
+            mx_v = psum.tile([P, D], F32, tag="s", bufs=2, name="mx_v")
+            nc.tensor.matmul_mx(
+                out=mx_v[:], lhsT=xw[:, r * P : (r + 1) * P].bitcast(FP8X4), lhsT_scale=xs[:, r * P : (r + 1) * P],
+                rhs=ww[:].bitcast(FP8X4), rhs_scale=ws[:], start=True, stop=True,
+            )
+            nc.vector.scalar_tensor_tensor(
+                out=junk_v[:], in0=mx_v[:], scalar=1.0, in1=b_bc[:], op0=ALU.mult, op1=ALU.mult, accum_out=mb[:, c : c + 1]
+            )
+        at = small("at")
+        rho = small("rho")
+        y2 = small("y2", 1)
+        y2p1 = small("y2p1", 1)
+        ts1(at[:], nn[:], ATANH_CLIP, ALU.min)
+        ts1(rho[:], th[:], TINY, ALU.max)
+        nc.vector.reciprocal(out=rho[:], in_=rho[:])
+        tt(rho[:], rho[:], at[:], ALU.mult)
+        tt(y2[:], th[:, BCOL : BCOL + 1], th[:, BCOL : BCOL + 1], ALU.mult)
+        ts1(y2p1[:], y2[:], 1.0, ALU.add)
+        sb = sx[:, BCOL : BCOL + 1]
+        mr = small("mr")
+        rm = small("rm")
+        w2 = small("w2")
+        nc.scalar.activation(out=mr[:], in_=mx2[:], func=AF.Sqrt)
+        for r in range(TILES):
+            c = COL[r]
+            nc.scalar.activation(out=tm[:, c : c + 1], in_=mr[:, c : c + 1], func=AF.Tanh, scale=rho[:, c : c + 1])
+        warm3 = small("warm3", 1)
+        nc.scalar.activation(out=warm3[:], in_=tm[:, COL[3] : COL[3] + 1], func=AF.Sqrt)
+        ts1(rm[:], mr[:], TINY, ALU.max)
+        nc.vector.reciprocal(out=rm[:], in_=rm[:])
+        stt(w2[:], mb[:], sb, rm[:], ALU.mult, ALU.mult)
+        x2 = small("x2")
+        xy2 = small("xy2")
+        den = small("den")
+        num = small("num")
+        qn2 = small("qn2")
+        tt(x2[:], tm[:], tm[:], ALU.mult)
+        stt(xy2[:], tm[:], 2.0, w2[:], ALU.mult, ALU.mult)
+        stt(den[:], x2[:], y2[:], xy2[:], ALU.mult, ALU.add)
+        ts(den[:], den[:], 1.0, TINY, ALU.add, ALU.max)
+        nc.vector.reciprocal(out=den[:], in_=den[:])
+        stt(num[:], x2[:], y2[:], xy2[:], ALU.add, ALU.add)
+        stt(qn2[:], num[:], 0.0, den[:], ALU.max, ALU.mult)
+        dd = small("dd")
+        ff = small("ff")
+        ts1(dd[:], qn2[:], -1.0, ALU.add)
+        ts(ff[:], dd[:], 0.375, -0.5, ALU.mult, ALU.add)
+        tt(ff[:], ff[:], dd[:], ALU.mult)
+        ts(ff[:], ff[:], 1.0, CLIP, ALU.add, ALU.mult)
+        ts1(ff[:], ff[:], 1.0, ALU.min)
+        g1 = small("g1")
+        g2 = small("g2")
+        aa = small("aa")
+        p1 = small("p1")
+        p2 = small("p2")
+        ts(g2[:], x2[:], -1.0, 1.0, ALU.mult, ALU.add)
+        stt(g2[:], g2[:], sb, den[:], ALU.mult, ALU.mult)
+        tt(p2[:], g2[:], ff[:], ALU.mult)
+        tt(g1[:], tm[:], rm[:], ALU.mult)
+        tt(g1[:], g1[:], den[:], ALU.mult)
+        ts1(aa[:], xy2[:], y2p1[:], ALU.add)
+        tt(g1[:], g1[:], aa[:], ALU.mult)
+        tt(p1[:], g1[:], ff[:], ALU.mult)
+        tmp = work.tile([P, TILES, D], F32, tag="a", bufs=GROUP, name="tmp")
+        p_all = work.tile([P, TILES, D], F32, tag="zb", bufs=ZB_BUFS, name="p_all")
+        pgrp = head_grp()
+        for r in range(TILES):
+            c = COL[r]
+            nc.scalar.activation(out=tmp[:, r, :], in_=b_bc[:], func=AF.Copy, scale=p2[:, c : c + 1])
+            stt(p_all[:, r, :], mxs[r][:], p1[:, c : c + 1], tmp[:, r, :], ALU.mult, ALU.add)
+            tps[r] = f32_transposes(p_all, r)
+        for r in range(TILES):
+            f32_evac("av"[r % 2], tps[r], pgrp, r)
+        quantise(pgrp, pw[:], ps[:])
+        a2c = small("a2c")
+        ts(a2c[:], qn2[:], CLIP * CLIP, -1.0, ALU.min, ALU.mult)
+        ts1(a2c[:], a2c[:], 1.0, ALU.add)
+        nc.vector.reciprocal(out=a2c[:], in_=a2c[:])
+        ts1(a2c[:], a2c[:], -2.0, ALU.mult)
+        a2p = psum.tile([P, ROWS], F32, tag="s", bufs=2, name="a2p")
+        for r in range(TILES):
+            c = COL[r]
+            nc.tensor.matmul(out=a2p[:, r * P : (r + 1) * P], lhsT=a2c[:, c : c + 1].to_broadcast([P, P]), rhs=ident[:], start=True, stop=True)
+        copy("a", a2[:], a2p[:])
 
         c2 = small("c2", 1)
         tt(c2[:], t_bc[:], t_bc[:], ALU.mult)
@@ -263,152 +393,10 @@ def tile_hyperbolicdistancedecoder_kernel(tc, v_tangent, code_points, W, b, freq
         nc.vector.tensor_copy(out=c1m[:], in_=c1[:])
         ts1(c1[:], c1[:], 2.0, ALU.mult)
 
-        sumsq("a", b_bc[:], n2[:, BCOL : BCOL + 1])
-        sumsq("a", rv[:, 0, :], n2[:, COL[0] : COL[0] + 1])
-        sumsq("v", rv[:, 2, :], n2[:, COL[2] : COL[2] + 1])
-        sumsq("a", rv[:, 1, :], n2[:, COL[1] : COL[1] + 1])
-        sumsq("v", rv[:, 3, :], n2[:, COL[3] : COL[3] + 1])
-        nr = small("nr")
-        nn = small("nn")
-        th = small("th")
-        rn = small("rn")
-        sx = small("sx")
-        nc.scalar.activation(out=nr[:], in_=n2[:], func=AF.Sqrt)
-        ts1(nn[:], nr[:], TINY, ALU.max)
-        nc.scalar.activation(out=th[:], in_=nn[:], func=AF.Tanh)
-        nc.vector.reciprocal(out=rn[:], in_=nn[:])
-        wct0 = word_transposes(rw, 0)
-        wct1 = word_transposes(rw, 1)
-        wgrp = head_grp()
-        word_evac("v", wct0, wgrp, 0)
-        word_evac("v", wct1, wgrp, 1)
-        hook(0)
-        tt(sx[:], th[:], rn[:], ALU.mult)
-        x_all = work.tile([P, TILES, D], F32, tag="zb", bufs=ZB_BUFS, name="x_all")
-        for r, eng in ((0, "v"), (2, "a"), (1, "v"), (3, "a")):
-            c = COL[r]
-            if eng == "v":
-                ts1(x_all[:, r, :], rv[:, r, :], sx[:, c : c + 1], ALU.mult)
-            else:
-                nc.scalar.activation(out=x_all[:, r, :], in_=rv[:, r, :], func=AF.Copy, scale=sx[:, c : c + 1])
-        load_next()
-        load_next()
-        quantise(wgrp, ww[:], ws[:])
-        xgrp = head_grp()
-        tps = {}
-        for r in (0, 2, 1, 3):
-            tps[r] = f32_transposes(x_all, r)
-        at = small("at")
-        rho = small("rho")
-        y2 = small("y2", 1)
-        y2p1 = small("y2p1", 1)
-        ts1(at[:], nn[:], ATANH_CLIP, ALU.min)
-        ts1(rho[:], th[:], TINY, ALU.max)
-        nc.vector.reciprocal(out=rho[:], in_=rho[:])
-        tt(rho[:], rho[:], at[:], ALU.mult)
-        tt(y2[:], th[:, BCOL : BCOL + 1], th[:, BCOL : BCOL + 1], ALU.mult)
-        ts1(y2p1[:], y2[:], 1.0, ALU.add)
-        sb = sx[:, BCOL : BCOL + 1]
-        hook(1)
-        f32_evac("v", tps[0], xgrp, 0)
-        hook(2)
-        f32_evac("a", tps[2], xgrp, 2)
-        hook(3)
-        f32_evac("v", tps[1], xgrp, 1)
-        hook(4)
-        f32_evac("a", tps[3], xgrp, 3)
-        nc.scalar.activation(out=dummy[:], in_=dummy[:], func=AF.Sqrt)
-        hook(5)
-        quantise(xgrp, xw[:], xs[:])
-        mxs = {}
-        for r in range(TILES):
-            mx = psum.tile([P, D], F32, tag="e", bufs=4, name="mx")
-            nc.tensor.matmul_mx(
-                out=mx[:], lhsT=xw[:, r * P : (r + 1) * P].bitcast(FP8X4), lhsT_scale=xs[:, r * P : (r + 1) * P],
-                rhs=ww[:].bitcast(FP8X4), rhs_scale=ws[:], start=True, stop=True,
-            )
-            mxs[r] = mx
-        for r in range(TILES):
-            c = COL[r]
-            nc.scalar.activation(out=junk_a[:], in_=mxs[r][:], func=AF.Square, accum_out=mx2[:, c : c + 1])
-            mx_v = psum.tile([P, D], F32, tag="s", bufs=2, name="mx_v")
-            nc.tensor.matmul_mx(
-                out=mx_v[:], lhsT=xw[:, r * P : (r + 1) * P].bitcast(FP8X4), lhsT_scale=xs[:, r * P : (r + 1) * P],
-                rhs=ww[:].bitcast(FP8X4), rhs_scale=ws[:], start=True, stop=True,
-            )
-            nc.vector.scalar_tensor_tensor(
-                out=junk_v[:], in0=mx_v[:], scalar=1.0, in1=b_bc[:], op0=ALU.mult, op1=ALU.mult, accum_out=mb[:, c : c + 1]
-            )
-        mxn = small("mxn")
-        arg = small("arg")
-        tm = small("tm")
-        rm = small("rm")
-        w2 = small("w2")
-        nc.scalar.activation(out=mxn[:], in_=mx2[:], func=AF.Sqrt)
-        ts1(mxn[:], mxn[:], TINY, ALU.max)
-        tt(arg[:], mxn[:], rho[:], ALU.mult)
-        nc.scalar.activation(out=tm[:], in_=arg[:], func=AF.Tanh)
-        nc.scalar.activation(out=dummy[:], in_=dummy[:], func=AF.Sqrt)
-        nc.vector.reciprocal(out=rm[:], in_=mxn[:])
-        stt(w2[:], mb[:], sb, rm[:], ALU.mult, ALU.mult)
-        hook(6)
-        x2 = small("x2")
-        xy2 = small("xy2")
-        den = small("den")
-        num = small("num")
-        qn2 = small("qn2")
-        qn = small("qn")
-        tt(x2[:], tm[:], tm[:], ALU.mult)
-        stt(xy2[:], tm[:], 2.0, w2[:], ALU.mult, ALU.mult)
-        stt(den[:], x2[:], y2[:], xy2[:], ALU.mult, ALU.add)
-        ts(den[:], den[:], 1.0, TINY, ALU.add, ALU.max)
-        nc.vector.reciprocal(out=den[:], in_=den[:])
-        stt(num[:], x2[:], y2[:], xy2[:], ALU.add, ALU.add)
-        stt(qn2[:], num[:], 0.0, den[:], ALU.max, ALU.mult)
-        nc.scalar.activation(out=qn[:], in_=qn2[:], func=AF.Sqrt)
-        g1 = small("g1")
-        g2 = small("g2")
-        aa = small("aa")
-        tt(g1[:], tm[:], rm[:], ALU.mult)
-        tt(g1[:], g1[:], den[:], ALU.mult)
-        ts1(aa[:], xy2[:], y2p1[:], ALU.add)
-        tt(g1[:], g1[:], aa[:], ALU.mult)
-        ts(g2[:], x2[:], -1.0, 1.0, ALU.mult, ALU.add)
-        stt(g2[:], g2[:], sb, den[:], ALU.mult, ALU.mult)
-        ff = small("ff")
-        ts1(ff[:], qn[:], TINY, ALU.max)
-        nc.vector.reciprocal(out=ff[:], in_=ff[:])
-        ts(ff[:], ff[:], CLIP, 1.0, ALU.mult, ALU.min)
-        p1 = small("p1")
-        p2 = small("p2")
-        tt(p2[:], g2[:], ff[:], ALU.mult)
-        tt(p1[:], g1[:], ff[:], ALU.mult)
-        tmp = work.tile([P, TILES, D], F32, tag="a", bufs=GROUP, name="tmp")
-        p_all = work.tile([P, TILES, D], F32, tag="zb", bufs=ZB_BUFS, name="p_all")
-        pgrp = head_grp()
-        for r in range(TILES):
-            c = COL[r]
-            nc.scalar.activation(out=tmp[:, r, :], in_=b_bc[:], func=AF.Copy, scale=p2[:, c : c + 1])
-            stt(p_all[:, r, :], mxs[r][:], p1[:, c : c + 1], tmp[:, r, :], ALU.mult, ALU.add)
-            tps[r] = f32_transposes(p_all, r)
-        a2c = small("a2c")
-        ts(a2c[:], qn2[:], CLIP * CLIP, -1.0, ALU.min, ALU.mult)
-        ts1(a2c[:], a2c[:], 1.0, ALU.add)
-        nc.vector.reciprocal(out=a2c[:], in_=a2c[:])
-        ts1(a2c[:], a2c[:], -2.0, ALU.mult)
-        a2p = psum.tile([P, ROWS], F32, tag="s", bufs=2, name="a2p")
-        for r in range(TILES):
-            c = COL[r]
-            nc.tensor.matmul(out=a2p[:, r * P : (r + 1) * P], lhsT=a2c[:, c : c + 1].to_broadcast([P, P]), rhs=ident[:], start=True, stop=True)
-        f32_evac("v", tps[0], pgrp, 0)
-        f32_evac("a", tps[1], pgrp, 1)
-        f32_evac("v", tps[2], pgrp, 2)
-        f32_evac("a", tps[3], pgrp, 3)
-        copy("a", a2[:], a2p[:])
-        hook(7)
-        quantise(pgrp, pw[:], ps[:])
-
         zbs = {}
+        betat = const.tile([P, N_UNITS, 16], F32, name="betat")
+        tok_a = [small("tok_a%d" % g, 1) for g in range(N_UNITS // GROUP)]
+        tok_b = [small("tok_b%d" % g, 1) for g in range(N_UNITS // GROUP)]
         aas = {}
         lqs = {}
         es = {}
@@ -429,7 +417,7 @@ def tile_hyperbolicdistancedecoder_kernel(tc, v_tangent, code_points, W, b, freq
                 c = ycol(u, t)
                 s = psum.tile([P, ROWS], F32, tag="s", bufs=2, name="s")
                 nc.tensor.matmul_mx(
-                    out=s[:], lhsT=cw[:, u, t * P : (t + 1) * P].bitcast(FP8X4), lhsT_scale=cs[:, u, t * P : (t + 1) * P],
+                    out=s[:], lhsT=cws[u][:, t * P : (t + 1) * P].bitcast(FP8X4), lhsT_scale=css[u][:, t * P : (t + 1) * P],
                     rhs=pw[:].bitcast(FP8X4), rhs_scale=ps[:], start=True, stop=True,
                 )
                 stt(zb[:, t, :], s[:], yh[:, u, c : c + 1], a2[:], ALU.add, ALU.mult)
@@ -439,13 +427,18 @@ def tile_hyperbolicdistancedecoder_kernel(tc, v_tangent, code_points, W, b, freq
 
         def roots(u):
             zb = zbs[u]
+            g = u // GROUP
+            if g > 0:
+                nc.scalar.activation(out=betat[:, u, :], in_=beta[:, u, :], func=AF.Identity, bias=tok_b[g - 1][:])
+            else:
+                nc.scalar.copy(out=betat[:, u, :], in_=beta[:, u, :])
             if FORM[u] == "t":
                 a = work.tile([P, TILES, ROWS], F32, tag="a", bufs=GROUP, name="a")
                 aas[u] = a
                 for t in range(TILES):
                     c = ycol(u, t)
-                    nc.scalar.activation(out=a[:, t, :], in_=zb[:, t, :], func=AF.Sqrt, scale=beta[:, u, c : c + 1], bias=nbeta[:, u, c : c + 1])
-                    nc.scalar.activation(out=zb[:, t, :], in_=zb[:, t, :], func=AF.Sqrt, scale=beta[:, u, c : c + 1], bias=ombeta[:, u, c : c + 1])
+                    nc.scalar.activation(out=a[:, t, :], in_=zb[:, t, :], func=AF.Sqrt, scale=betat[:, u, c : c + 1], bias=nbeta[:, u, c : c + 1])
+                    nc.scalar.activation(out=zb[:, t, :], in_=zb[:, t, :], func=AF.Sqrt, scale=betat[:, u, c : c + 1], bias=ombeta[:, u, c : c + 1])
             else:
                 af = aas[u][:].rearrange("p t i -> p (t i)")
                 nc.scalar.activation(out=af, in_=af, func=AF.Sqrt, bias=neg1[:])
@@ -465,20 +458,25 @@ def tile_hyperbolicdistancedecoder_kernel(tc, v_tangent, code_points, W, b, freq
             es[(u, r)] = e
             for t in range(TILES):
                 o = e[:, t * P : (t + 1) * P]
-                nc.tensor.matmul(out=o, lhsT=aas[u][:, t, r * P : (r + 1) * P], rhs=ident[:], start=True, stop=False, is_transpose=True)
-                nc.tensor.matmul(out=o, lhsT=zbs[u][:, t, r * P : (r + 1) * P], rhs=ident[:], start=False, stop=True, is_transpose=True)
+                if ADD_ENG[u] == "p":
+                    nc.tensor.matmul(out=o, lhsT=aas[u][:, t, r * P : (r + 1) * P], rhs=ident[:], start=True, stop=False, is_transpose=True)
+                    nc.tensor.matmul(out=o, lhsT=zbs[u][:, t, r * P : (r + 1) * P], rhs=ident[:], start=False, stop=True, is_transpose=True)
+                else:
+                    nc.tensor.transpose(o, aas[u][:, t, r * P : (r + 1) * P], ident[:])
 
         def log_r(u, r):
             if r == 0:
                 lqs[u] = work.tile([P, TILES, UNIT], F32, tag="lq", bufs=GROUP, name="lq", align_bytes=64)
-            nc.scalar.activation(out=lqs[u][:, r, :], in_=es[(u, r)][:], func=AF.Ln)
+            nc.scalar.activation(out=lqs[u][:, r, :], in_=es[(u, r)][:], func=AF.Ln, bias=tok_a[u // GROUP][:])
+            if SQ_ENG[u] == "a":
+                nc.scalar.activation(out=lqs[u][:, r, :], in_=lqs[u][:, r, :], func=AF.Square, scale=(c1 if FORM[u] == "t" else c1m)[:])
+            else:
+                fill_a(LN_FILL)
 
         def finish(u):
             lq = lqs[u]
             flat = lq[:].rearrange("p r j -> p (r j)")
-            if SQ_ENG[u] == "a":
-                nc.scalar.activation(out=flat, in_=flat, func=AF.Square, scale=(c1 if FORM[u] == "t" else c1m)[:])
-            else:
+            if SQ_ENG[u] == "v":
                 stt(flat, flat, (c2 if FORM[u] == "t" else c2m)[:], flat, ALU.mult, ALU.mult)
             fbu = fb[:, u * UNIT : (u + 1) * UNIT].unsqueeze(1).to_broadcast([P, TILES, UNIT])
             if FB_ENG[u] == "g":
@@ -489,10 +487,12 @@ def tile_hyperbolicdistancedecoder_kernel(tc, v_tangent, code_points, W, b, freq
 
         def finish_r(u, r):
             part = lqs[u][:, r, :]
-            stt(part, part, (c2 if FORM[u] == "t" else c2m)[:], part, ALU.mult, ALU.mult)
+            if SQ_ENG[u] == "v":
+                stt(part, part, (c2 if FORM[u] == "t" else c2m)[:], part, ALU.mult, ALU.mult)
             tt(part, fb[:, u * UNIT : (u + 1) * UNIT], part, ALU.subtract)
             nc.sync.dma_start(out=out_view[u][:, r, :], in_=part)
 
+        fill_to(HEAD_UNITS - 1)
         for u in range(LOOKAHEAD):
             front(u)
         for g in range(N_UNITS // GROUP):
@@ -505,16 +505,21 @@ def tile_hyperbolicdistancedecoder_kernel(tc, v_tangent, code_points, W, b, freq
                 if u + LOOKAHEAD < N_UNITS:
                     front(u + LOOKAHEAD)
                 roots(u)
+                if ADD_ENG[u] == "v":
+                    tt(aas[u][:], aas[u][:], zbs[u][:], ALU.add)
                 if u + 1 < N_UNITS and FORM[u + 1] == "m":
                     cosh_form(u + 1)
                 fill_a(SLOT_A[0])
                 fill_v(SLOT_V[0])
+            nc.scalar.activation(out=tok_a[g][:], in_=zbs[first + GROUP - 1][:, TILES - 1, 0:1], func=AF.Copy, scale=0.0)
             for i in range(GROUP):
                 u = first + i
                 for r in range(TILES):
                     log_r(u, r)
                     if i + 1 < GROUP:
                         add_t(u + 1, r)
+                    if i == GROUP - 1 and r == TILES - 1:
+                        nc.scalar.activation(out=tok_b[g][:], in_=lqs[u][:, r, 0:1], func=AF.Copy, scale=0.0)
                     if u == N_UNITS - 1:
                         finish_r(u, r)
                 if u < N_UNITS - 1:

@@ -16,10 +16,11 @@ P = 128
 D = 512
 ROWS = 512
 CODES = 8192
-UNIT = 512
-N_UNITS = CODES // UNIT
 TILES = 4
+UNIT = TILES * P
+N_UNITS = CODES // UNIT
 GROUP = 4
+N_GROUPS = N_UNITS // GROUP
 FLOPS = 2 * ROWS * D * D + 2 * ROWS * CODES * D
 
 CLIP = 1.0 - 1e-5
@@ -27,26 +28,16 @@ ATANH_CLIP = 0.5 * math.log((1.0 + CLIP) / (1.0 - CLIP))
 T_MAX = CLIP * CLIP / (1.0 - CLIP * CLIP)
 TINY = 1e-15
 GAP_MIN = 1e-8
+
 COL = (0, 1, 8, 9)
 BCOL = 2
 
 RAW_BUFS = 6
-CW_BUFS = 6
-GRP_BUFS = 2
-ZB_BUFS = 6
-HEAD_UNITS = 4
-LOOKAHEAD = 2
-YS_ACT = (4, 4, 4, 4, 4, 4, 4, 4, 4, 4, 4, 4, 4, 4, 4, 4)
-EV_ENG = ("vv",) * 16
-PREFILL_AT = 1
-LN_FILL = 0
-SLOT_A = (1, 0)
-SLOT_V = (3, 2)
-FORM = "tttttttttttttttt"
-ADD_ENG = "pppppppppvvvpvvv"
-FB_ENG = "vvvvvvvvvvvvvvvv"
-CL_ENG = "vvvvvvvvvvvvvvvv"
-SQ_ENG = "vvvvvvvvvvvvvava"
+WORD_BUFS = 6
+Z_BUFS = GROUP + 2
+AHEAD = 2
+PREPARE_AHEAD = 4
+FIRST_VECTOR_ADD_GROUP = 2
 
 
 def tile_hyperbolicdistancedecoder_kernel(tc, v_tangent, code_points, W, b, freq_bias, temperature, out):
@@ -64,28 +55,30 @@ def tile_hyperbolicdistancedecoder_kernel(tc, v_tangent, code_points, W, b, freq
         def small(name, cols=16):
             return const.tile([P, cols], F32, name=name)
 
+        def per_code(name):
+            return const.tile([P, N_UNITS, TILES], F32, name=name)
+
         ident = const.tile([P, P], F32, name="ident")
-        a2 = const.tile([P, ROWS], F32, name="a2")
+        neg2alpha = const.tile([P, ROWS], F32, name="neg2alpha")
         b_bc = const.tile([P, D], BF16, name="b_bc")
         t_bc = const.tile([P, 1], BF16, name="t_bc")
         fb = const.tile([P, CODES], BF16, name="fb")
-        cws = {}
-        css = {}
-        xw = const.tile([P, ROWS], U32, name="xw", align_bytes=64)
-        xs = const.tile([P, ROWS], U8, name="xs", align_bytes=64)
-        ww = const.tile([P, D], U32, name="ww", align_bytes=64)
-        ws = const.tile([P, D], U8, name="ws", align_bytes=64)
-        pw = const.tile([P, ROWS], U32, name="pw", align_bytes=64)
-        ps = const.tile([P, ROWS], U8, name="ps", align_bytes=64)
-        junk_a = const.tile([P, D], BF16, name="junk_a")
-        junk_v = const.tile([P, D], F32, name="junk_v")
-        ysum = const.tile([P, N_UNITS, 16], F32, name="ysum")
-        yh = const.tile([P, N_UNITS, 16], F32, name="yh")
-        gap = const.tile([P, N_UNITS, 16], F32, name="gap")
-        beta = const.tile([P, N_UNITS, 16], F32, name="beta")
-        nbeta = const.tile([P, N_UNITS, 16], F32, name="nbeta")
-        ombeta = const.tile([P, N_UNITS, 16], F32, name="ombeta")
-        zmax = const.tile([P, N_UNITS, 16], F32, name="zmax")
+        x_words = const.tile([P, ROWS], U32, name="x_words", align_bytes=64)
+        x_scales = const.tile([P, ROWS], U8, name="x_scales", align_bytes=64)
+        w_words = const.tile([P, D], U32, name="w_words", align_bytes=64)
+        w_scales = const.tile([P, D], U8, name="w_scales", align_bytes=64)
+        p_words = const.tile([P, ROWS], U32, name="p_words", align_bytes=64)
+        p_scales = const.tile([P, ROWS], U8, name="p_scales", align_bytes=64)
+        unread_a = const.tile([P, D], BF16, name="unread_a")
+        unread_v = const.tile([P, D], F32, name="unread_v")
+        y2 = per_code("y2")
+        shift = per_code("shift")
+        gap = per_code("gap")
+        beta = per_code("beta")
+        beta_gated = per_code("beta_gated")
+        neg_beta = per_code("neg_beta")
+        one_minus_beta = per_code("one_minus_beta")
+        z_max = per_code("z_max")
 
         def ts(o, i, s1, s2, op0, op1):
             nc.vector.tensor_scalar(out=o, in0=i, scalar1=s1, scalar2=s2, op0=op0, op1=op1)
@@ -99,430 +92,341 @@ def tile_hyperbolicdistancedecoder_kernel(tc, v_tangent, code_points, W, b, freq
         def tt(o, i0, i1, op):
             nc.vector.tensor_tensor(out=o, in0=i0, in1=i1, op=op)
 
-        def sumsq(eng, src, acc):
-            if eng == "a":
-                nc.scalar.activation(out=junk_a[:], in_=src, func=AF.Square, accum_out=acc)
-            else:
-                nc.vector.scalar_tensor_tensor(out=junk_v[:], in0=src, scalar=1.0, in1=src, op0=ALU.mult, op1=ALU.mult, accum_out=acc)
+        def sum_of_squares_scalar(src, acc):
+            nc.scalar.activation(out=unread_a[:], in_=src, func=AF.Square, accum_out=acc)
 
-        def copy(eng, o, i):
-            if eng == "a":
+        def dot_vector(src0, src1, acc):
+            nc.vector.scalar_tensor_tensor(out=unread_v[:], in0=src0, scalar=1.0, in1=src1, op0=ALU.mult, op1=ALU.mult, accum_out=acc)
+
+        def copy(engine, o, i):
+            if engine == "scalar":
                 nc.scalar.copy(out=o, in_=i)
             else:
                 nc.vector.tensor_copy(out=o, in_=i)
 
+        def mx_pass(o, lhs_words, lhs_scales, rhs_words, rhs_scales):
+            nc.tensor.matmul_mx(
+                out=o, lhsT=lhs_words.bitcast(FP8X4), lhsT_scale=lhs_scales, rhs=rhs_words.bitcast(FP8X4), rhs_scale=rhs_scales,
+                start=True, stop=True,
+            )
+
+        def quantise(grouped, words, scales):
+            nc.vector.quantize_mx(out=words.bitcast(FP8X4), scales=scales, in_=grouped[:])
+
         def word_transposes(raw, half):
-            ct = psum.tile([P, 2, 2, P], F32, tag="ct", bufs=2, name="ct")
-            rawf = raw[:].rearrange("p t d -> p (t d)").bitcast(F32)
+            bank = psum.tile([P, 2, 2, P], F32, tag="words", bufs=2, name="bank")
+            raw_words = raw[:].rearrange("p t d -> p (t d)").bitcast(F32)
             for i in range(2):
-                for uu in range(2):
-                    col = (2 * half + i) * (D // 2) + uu * P
-                    nc.tensor.transpose(ct[:, i, uu, :], rawf[:, col : col + P], ident[:])
-            return ct
+                for h in range(2):
+                    first = (2 * half + i) * (D // 2) + h * P
+                    nc.tensor.transpose(bank[:, i, h, :], raw_words[:, first : first + P], ident[:])
+            return bank
 
-        def word_evac(eng, ct, grp, half):
-            dst = grp[:].bitcast(F32).rearrange("p (c u) -> p c u", u=2)[:, half * 2 * P : (half + 1) * 2 * P, :]
-            copy(eng, dst.rearrange("p (i c) u -> p i c u", i=2), ct[:].rearrange("p i u c -> p i c u"))
+        def word_copy(engine, bank, grouped, half):
+            dst = grouped[:].bitcast(F32).rearrange("p (c h) -> p c h", h=2)[:, half * 2 * P : (half + 1) * 2 * P, :]
+            copy(engine, dst.rearrange("p (i c) h -> p i c h", i=2), bank[:].rearrange("p i h c -> p i c h"))
 
-        def new_grp():
-            return work.tile([P, 4 * UNIT], BF16, tag="grp", bufs=GRP_BUFS, name="grp", align_bytes=64)
+        def row_transposes(rows, r):
+            bank = psum.tile([P, 4, P], F32, tag="sum", bufs=4, name="bank")
+            view = rows[:, r, :].rearrange("p (h q e) -> p h e q", h=2, e=2)
+            for h in range(2):
+                for e in range(2):
+                    nc.tensor.transpose(bank[:, 2 * h + e, :], view[:, h, e, :], ident[:])
+            return bank
 
-        def head_grp():
-            return work.tile([P, 4 * UNIT], BF16, tag="lq", bufs=GROUP, name="hgrp", align_bytes=64)
+        def row_copy(engine, bank, grouped, r):
+            dst = grouped[:].rearrange("p (c t) -> p c t", t=4)[:, r * P : (r + 1) * P, :]
+            copy(engine, dst, bank[:].rearrange("p t c -> p c t"))
 
-        def quantise(grp, words, scales):
-            nc.vector.quantize_mx(out=words.bitcast(FP8X4), scales=scales, in_=grp[:])
-
-        def f32_transposes(src, r):
-            tp = psum.tile([P, 4, P], F32, tag="e", bufs=4, name="tp")
-            view = src[:, r, :].rearrange("p (u q e) -> p u e q", u=2, e=2)
-            for uu in range(2):
-                for ee in range(2):
-                    nc.tensor.transpose(tp[:, 2 * uu + ee, :], view[:, uu, ee, :], ident[:])
-            return tp
-
-        def f32_evac(eng, tp, grp, r):
-            dst = grp[:].rearrange("p (c k) -> p c k", k=4)[:, r * P : (r + 1) * P, :]
-            copy(eng, dst, tp[:].rearrange("p t c -> p c t"))
+        def stage_one_grouped():
+            return work.tile([P, 4 * ROWS], BF16, tag="log", bufs=GROUP, name="grouped", align_bytes=64)
 
         raws = {}
-        state = {"next_load": 0}
+        code_words = {}
+        code_scales = {}
+        loaded = []
 
-        def load_next():
-            u = state["next_load"]
+        def load_next_unit():
+            u = len(loaded)
             if u < N_UNITS:
                 raw = work.tile([P, TILES, D], BF16, tag="raw", bufs=RAW_BUFS, name="raw")
                 nc.sync.dma_start(out=raw[:], in_=code_view[u])
                 raws[u] = raw
-                state["next_load"] = u + 1
+                loaded.append(u)
 
-        def ycol(u, t):
-            return t if t < YS_ACT[u] else 8 + t
+        def prepare_pair(first):
+            pair_units = (first, first + 1)
+            grouped = {}
+            for u in pair_units:
+                word_banks = [word_transposes(raws[u], half) for half in range(2)]
+                grouped[u] = work.tile([P, 4 * UNIT], BF16, tag="grouped", bufs=2, name="grouped", align_bytes=64)
+                for half in range(2):
+                    word_copy("vector", word_banks[half], grouped[u], half)
+            for u in pair_units:
+                code_words[u] = work.tile([P, UNIT], U32, tag="code_words", bufs=WORD_BUFS, name="words", align_bytes=64)
+                code_scales[u] = work.tile([P, UNIT], U8, tag="code_scales", bufs=WORD_BUFS, name="scales", align_bytes=64)
+                quantise(grouped[u], code_words[u][:], code_scales[u][:])
+                for t in range(TILES):
+                    sum_of_squares_scalar(raws[u][:, t, :], y2[:, u, t : t + 1])
+                load_next_unit()
 
-        def prep_pieces(u):
-            box = {}
+            def pair(values):
+                return values[:, first : first + 2, :].rearrange("p u t -> p (u t)")
 
-            def tr(half):
-                box[half] = word_transposes(raws[u], half)
+            ts(pair(shift), pair(y2), -0.5, -0.5, ALU.mult, ALU.add)
+            ts(pair(gap), pair(y2), -1.0, 1.0, ALU.mult, ALU.add)
+            ts1(pair(gap), pair(gap), GAP_MIN, ALU.max)
+            nc.vector.reciprocal(out=pair(beta), in_=pair(gap))
+            ts1(pair(neg_beta), pair(beta), -1.0, ALU.mult)
+            ts(pair(one_minus_beta), pair(beta), -1.0, 1.0, ALU.mult, ALU.add)
+            ts(pair(z_max), pair(gap), T_MAX, 1.0, ALU.mult, ALU.add)
 
-            def ev(half):
-                if half == 0:
-                    box["grp"] = new_grp()
-                word_evac(EV_ENG[u][half], box[half], box["grp"], half)
-
-            def ys(t):
-                c = ycol(u, t)
-                sumsq("a" if t < YS_ACT[u] else "v", raws[u][:, t, :], ysum[:, u, c : c + 1])
-
-            def qz():
-                cws[u] = work.tile([P, UNIT], U32, tag="cw", bufs=CW_BUFS, name="cw", align_bytes=64)
-                css[u] = work.tile([P, UNIT], U8, tag="cs", bufs=CW_BUFS, name="cs", align_bytes=64)
-                quantise(box["grp"], cws[u][:], css[u][:])
-
-            def sc():
-                while fifo_a and fifo_a[0][0] <= u:
-                    fifo_a.pop(0)[1]()
-                load_next()
-                y = ysum[:, u, :]
-                ts(yh[:, u, :], y, -0.5, -0.5, ALU.mult, ALU.add)
-                ts(gap[:, u, :], y, -1.0, 1.0, ALU.mult, ALU.add)
-                ts1(gap[:, u, :], gap[:, u, :], GAP_MIN, ALU.max)
-                nc.vector.reciprocal(out=beta[:, u, :], in_=gap[:, u, :])
-                if FORM[u] == "t":
-                    ts1(nbeta[:, u, :], beta[:, u, :], -1.0, ALU.mult)
-                    ts(ombeta[:, u, :], beta[:, u, :], -1.0, 1.0, ALU.mult, ALU.add)
-                else:
-                    ts1(nbeta[:, u, :], beta[:, u, :], 2.0, ALU.mult)
-                    ts(ombeta[:, u, :], beta[:, u, :], -2.0, 1.0, ALU.mult, ALU.add)
-                ts(zmax[:, u, :], gap[:, u, :], T_MAX, 1.0, ALU.mult, ALU.add)
-
-            for t in range(TILES):
-                if t < YS_ACT[u]:
-                    fifo_a.append((u, lambda t=t: ys(t)))
-            seq = [lambda: tr(0), lambda: tr(1), lambda: ev(0), lambda: ev(1)]
-            for t in range(YS_ACT[u], TILES):
-                seq.append(lambda t=t: ys(t))
-            seq.extend([lambda: qz(), lambda: sc()])
-            for fn in seq:
-                fifo_v.append((u, fn))
-
-        fifo_a = []
-        fifo_v = []
-        for u in range(N_UNITS):
-            prep_pieces(u)
-
-        def fill_a(k):
-            for i in range(k):
-                if fifo_a and fifo_a[0][0] < state["next_load"]:
-                    fifo_a.pop(0)[1]()
-
-        def fill_v(k):
-            for i in range(k):
-                if fifo_v:
-                    fifo_v.pop(0)[1]()
-
-        def fill_to(u):
-            while fifo_v and fifo_v[0][0] <= u:
-                fifo_v.pop(0)[1]()
-
-        n2 = small("n2")
+        norm2 = small("norm2")
         mx2 = small("mx2")
-        mb = small("mb")
-        tm = small("tm")
+        mx_b = small("mx_b")
+        tanh_m = small("tanh_m")
         warm = small("warm", 1)
         nc.vector.memset(warm[:], 1.0)
-        nc.vector.memset(n2[:], 1.0)
+        nc.vector.memset(norm2[:], 1.0)
         nc.vector.memset(mx2[:], 1.0)
-        nc.vector.memset(mb[:], 0.0)
-        nc.vector.memset(tm[:], 0.0)
-        nc.vector.memset(ysum[:].rearrange("p u c -> p (u c)"), 0.0)
-        rv = work.tile([P, TILES, D], BF16, tag="raw", bufs=RAW_BUFS, name="rv")
-        nc.sync.dma_start(out=rv[:], in_=v_view)
-        rw = work.tile([P, TILES, D], BF16, tag="raw", bufs=RAW_BUFS, name="rw")
-        nc.sync.dma_start(out=rw[:], in_=w_view)
+        nc.vector.memset(mx_b[:], 0.0)
+        nc.vector.memset(tanh_m[:], 0.0)
+        raw_v = work.tile([P, TILES, D], BF16, tag="raw", bufs=RAW_BUFS, name="raw_v")
+        nc.sync.dma_start(out=raw_v[:], in_=v_view)
+        raw_w = work.tile([P, TILES, D], BF16, tag="raw", bufs=RAW_BUFS, name="raw_w")
+        nc.sync.dma_start(out=raw_w[:], in_=w_view)
         nc.scalar.dma_start(out=b_bc[:], in_=b.partition_broadcast(P))
         nc.scalar.dma_start(out=t_bc[:], in_=temperature.partition_broadcast(P))
         for i in range(RAW_BUFS - 2):
-            load_next()
+            load_next_unit()
         make_identity(nc, ident[:])
         nc.gpsimd.dma_start(out=fb[:], in_=freq_bias.partition_broadcast(P))
         nc.scalar.activation(out=warm[:], in_=warm[:], func=AF.Sqrt)
 
-        sumsq("a", b_bc[:], n2[:, BCOL : BCOL + 1])
-        sumsq("a", rv[:, 0, :], n2[:, COL[0] : COL[0] + 1])
-        sumsq("v", rv[:, 2, :], n2[:, COL[2] : COL[2] + 1])
-        sumsq("a", rv[:, 1, :], n2[:, COL[1] : COL[1] + 1])
-        sumsq("v", rv[:, 3, :], n2[:, COL[3] : COL[3] + 1])
-        nr = small("nr")
-        nn = small("nn")
-        th = small("th")
-        rn = small("rn")
-        sx = small("sx")
-        nc.scalar.activation(out=nr[:], in_=n2[:], func=AF.Sqrt)
-        nc.scalar.activation(out=th[:], in_=nr[:], func=AF.Tanh)
-        warm2 = small("warm2", 1)
-        nc.scalar.activation(out=warm2[:], in_=th[:, 0:1], func=AF.Sqrt)
-        ts1(nn[:], nr[:], TINY, ALU.max)
-        nc.vector.reciprocal(out=rn[:], in_=nn[:])
-        tt(sx[:], th[:], rn[:], ALU.mult)
-        x_all = work.tile([P, TILES, D], F32, tag="zb", bufs=ZB_BUFS, name="x_all")
-        tps = {}
+        sum_of_squares_scalar(b_bc[:], norm2[:, BCOL : BCOL + 1])
+        sum_of_squares_scalar(raw_v[:, 0, :], norm2[:, COL[0] : COL[0] + 1])
+        dot_vector(raw_v[:, 2, :], raw_v[:, 2, :], norm2[:, COL[2] : COL[2] + 1])
+        sum_of_squares_scalar(raw_v[:, 1, :], norm2[:, COL[1] : COL[1] + 1])
+        dot_vector(raw_v[:, 3, :], raw_v[:, 3, :], norm2[:, COL[3] : COL[3] + 1])
+        norm = small("norm")
+        norm_floor = small("norm_floor")
+        tanh_n = small("tanh_n")
+        scale_x = small("scale_x")
+        nc.scalar.activation(out=norm[:], in_=norm2[:], func=AF.Sqrt)
+        nc.scalar.activation(out=tanh_n[:], in_=norm[:], func=AF.Tanh)
+        warm_2 = small("warm_2", 1)
+        nc.scalar.activation(out=warm_2[:], in_=tanh_n[:, 0:1], func=AF.Sqrt)
+        ts1(norm_floor[:], norm[:], TINY, ALU.max)
+        nc.vector.reciprocal(out=scale_x[:], in_=norm_floor[:])
+        tt(scale_x[:], tanh_n[:], scale_x[:], ALU.mult)
+        x_rows = work.tile([P, TILES, D], F32, tag="z", bufs=Z_BUFS, name="x_rows")
+        banks = {}
         for r in range(TILES):
             c = COL[r]
-            ts1(x_all[:, r, :], rv[:, r, :], sx[:, c : c + 1], ALU.mult)
-            tps[r] = f32_transposes(x_all, r)
-        xgrp = head_grp()
+            ts1(x_rows[:, r, :], raw_v[:, r, :], scale_x[:, c : c + 1], ALU.mult)
+            banks[r] = row_transposes(x_rows, r)
+        x_grouped = stage_one_grouped()
         for r in range(TILES):
-            f32_evac("av"[r % 2], tps[r], xgrp, r)
-        wct0 = word_transposes(rw, 0)
-        wct1 = word_transposes(rw, 1)
-        wgrp = head_grp()
-        word_evac("v", wct0, wgrp, 0)
-        word_evac("a", wct1, wgrp, 1)
-        load_next()
-        load_next()
-        quantise(wgrp, ww[:], ws[:])
-        quantise(xgrp, xw[:], xs[:])
-        mxs = {}
+            row_copy(("scalar", "vector")[r % 2], banks[r], x_grouped, r)
+        w_banks = [word_transposes(raw_w, half) for half in range(2)]
+        w_grouped = stage_one_grouped()
+        word_copy("vector", w_banks[0], w_grouped, 0)
+        word_copy("scalar", w_banks[1], w_grouped, 1)
+        load_next_unit()
+        load_next_unit()
+        quantise(w_grouped, w_words[:], w_scales[:])
+        quantise(x_grouped, x_words[:], x_scales[:])
+        mx = {}
         for r in range(TILES):
             c = COL[r]
-            mx = psum.tile([P, D], F32, tag="e", bufs=4, name="mx")
-            nc.tensor.matmul_mx(
-                out=mx[:], lhsT=xw[:, r * P : (r + 1) * P].bitcast(FP8X4), lhsT_scale=xs[:, r * P : (r + 1) * P],
-                rhs=ww[:].bitcast(FP8X4), rhs_scale=ws[:], start=True, stop=True,
-            )
-            mxs[r] = mx
-            nc.scalar.activation(out=junk_a[:], in_=mx[:], func=AF.Square, accum_out=mx2[:, c : c + 1])
-            mx_v = psum.tile([P, D], F32, tag="s", bufs=2, name="mx_v")
-            nc.tensor.matmul_mx(
-                out=mx_v[:], lhsT=xw[:, r * P : (r + 1) * P].bitcast(FP8X4), lhsT_scale=xs[:, r * P : (r + 1) * P],
-                rhs=ww[:].bitcast(FP8X4), rhs_scale=ws[:], start=True, stop=True,
-            )
-            nc.vector.scalar_tensor_tensor(
-                out=junk_v[:], in0=mx_v[:], scalar=1.0, in1=b_bc[:], op0=ALU.mult, op1=ALU.mult, accum_out=mb[:, c : c + 1]
-            )
-        at = small("at")
+            rows = slice(r * P, (r + 1) * P)
+            mx[r] = psum.tile([P, D], F32, tag="sum", bufs=4, name="mx")
+            mx_pass(mx[r][:], x_words[:, rows], x_scales[:, rows], w_words[:], w_scales[:])
+            nc.scalar.activation(out=unread_a[:], in_=mx[r][:], func=AF.Square, accum_out=mx2[:, c : c + 1])
+            mx_again = psum.tile([P, D], F32, tag="s", bufs=2, name="mx_again")
+            mx_pass(mx_again[:], x_words[:, rows], x_scales[:, rows], w_words[:], w_scales[:])
+            dot_vector(mx_again[:], b_bc[:], mx_b[:, c : c + 1])
         rho = small("rho")
-        y2 = small("y2", 1)
-        y2p1 = small("y2p1", 1)
-        ts1(at[:], nn[:], ATANH_CLIP, ALU.min)
-        ts1(rho[:], th[:], TINY, ALU.max)
+        atanh_x = small("atanh_x")
+        h2 = small("h2", 1)
+        h2_plus_1 = small("h2_plus_1", 1)
+        ts1(atanh_x[:], norm_floor[:], ATANH_CLIP, ALU.min)
+        ts1(rho[:], tanh_n[:], TINY, ALU.max)
         nc.vector.reciprocal(out=rho[:], in_=rho[:])
-        tt(rho[:], rho[:], at[:], ALU.mult)
-        tt(y2[:], th[:, BCOL : BCOL + 1], th[:, BCOL : BCOL + 1], ALU.mult)
-        ts1(y2p1[:], y2[:], 1.0, ALU.add)
-        sb = sx[:, BCOL : BCOL + 1]
-        mr = small("mr")
-        rm = small("rm")
-        w2 = small("w2")
-        nc.scalar.activation(out=mr[:], in_=mx2[:], func=AF.Sqrt)
+        tt(rho[:], rho[:], atanh_x[:], ALU.mult)
+        tt(h2[:], tanh_n[:, BCOL : BCOL + 1], tanh_n[:, BCOL : BCOL + 1], ALU.mult)
+        ts1(h2_plus_1[:], h2[:], 1.0, ALU.add)
+        scale_b = scale_x[:, BCOL : BCOL + 1]
+        mx_norm = small("mx_norm")
+        inv_mx_norm = small("inv_mx_norm")
+        nc.scalar.activation(out=mx_norm[:], in_=mx2[:], func=AF.Sqrt)
         for r in range(TILES):
             c = COL[r]
-            nc.scalar.activation(out=tm[:, c : c + 1], in_=mr[:, c : c + 1], func=AF.Tanh, scale=rho[:, c : c + 1])
-        warm3 = small("warm3", 1)
-        nc.scalar.activation(out=warm3[:], in_=tm[:, COL[3] : COL[3] + 1], func=AF.Sqrt)
-        ts1(rm[:], mr[:], TINY, ALU.max)
-        nc.vector.reciprocal(out=rm[:], in_=rm[:])
-        stt(w2[:], mb[:], sb, rm[:], ALU.mult, ALU.mult)
-        x2 = small("x2")
-        xy2 = small("xy2")
-        den = small("den")
-        num = small("num")
-        qn2 = small("qn2")
-        tt(x2[:], tm[:], tm[:], ALU.mult)
-        stt(xy2[:], tm[:], 2.0, w2[:], ALU.mult, ALU.mult)
-        stt(den[:], x2[:], y2[:], xy2[:], ALU.mult, ALU.add)
-        ts(den[:], den[:], 1.0, TINY, ALU.add, ALU.max)
-        nc.vector.reciprocal(out=den[:], in_=den[:])
-        stt(num[:], x2[:], y2[:], xy2[:], ALU.add, ALU.add)
-        stt(qn2[:], num[:], 0.0, den[:], ALU.max, ALU.mult)
-        dd = small("dd")
-        ff = small("ff")
-        ts1(dd[:], qn2[:], -1.0, ALU.add)
-        ts(ff[:], dd[:], 0.375, -0.5, ALU.mult, ALU.add)
-        tt(ff[:], ff[:], dd[:], ALU.mult)
-        ts(ff[:], ff[:], 1.0, CLIP, ALU.add, ALU.mult)
-        ts1(ff[:], ff[:], 1.0, ALU.min)
-        g1 = small("g1")
-        g2 = small("g2")
-        aa = small("aa")
-        p1 = small("p1")
-        p2 = small("p2")
-        ts(g2[:], x2[:], -1.0, 1.0, ALU.mult, ALU.add)
-        stt(g2[:], g2[:], sb, den[:], ALU.mult, ALU.mult)
-        tt(p2[:], g2[:], ff[:], ALU.mult)
-        tt(g1[:], tm[:], rm[:], ALU.mult)
-        tt(g1[:], g1[:], den[:], ALU.mult)
-        ts1(aa[:], xy2[:], y2p1[:], ALU.add)
-        tt(g1[:], g1[:], aa[:], ALU.mult)
-        tt(p1[:], g1[:], ff[:], ALU.mult)
-        tmp = work.tile([P, TILES, D], F32, tag="a", bufs=GROUP, name="tmp")
-        p_all = work.tile([P, TILES, D], F32, tag="zb", bufs=ZB_BUFS, name="p_all")
-        pgrp = head_grp()
+            nc.scalar.activation(out=tanh_m[:, c : c + 1], in_=mx_norm[:, c : c + 1], func=AF.Tanh, scale=rho[:, c : c + 1])
+        warm_3 = small("warm_3", 1)
+        nc.scalar.activation(out=warm_3[:], in_=tanh_m[:, COL[3] : COL[3] + 1], func=AF.Sqrt)
+        ts1(inv_mx_norm[:], mx_norm[:], TINY, ALU.max)
+        nc.vector.reciprocal(out=inv_mx_norm[:], in_=inv_mx_norm[:])
+        dot_unit = small("dot_unit")
+        stt(dot_unit[:], mx_b[:], scale_b, inv_mx_norm[:], ALU.mult, ALU.mult)
+        m2 = small("m2")
+        two_mh = small("two_mh")
+        inv_den = small("inv_den")
+        q2 = small("q2")
+        tt(m2[:], tanh_m[:], tanh_m[:], ALU.mult)
+        stt(two_mh[:], tanh_m[:], 2.0, dot_unit[:], ALU.mult, ALU.mult)
+        stt(inv_den[:], m2[:], h2[:], two_mh[:], ALU.mult, ALU.add)
+        ts(inv_den[:], inv_den[:], 1.0, TINY, ALU.add, ALU.max)
+        nc.vector.reciprocal(out=inv_den[:], in_=inv_den[:])
+        stt(q2[:], m2[:], h2[:], two_mh[:], ALU.add, ALU.add)
+        stt(q2[:], q2[:], 0.0, inv_den[:], ALU.max, ALU.mult)
+        d_q = small("d_q")
+        shrink = small("shrink")
+        ts1(d_q[:], q2[:], -1.0, ALU.add)
+        ts(shrink[:], d_q[:], 0.375, -0.5, ALU.mult, ALU.add)
+        tt(shrink[:], shrink[:], d_q[:], ALU.mult)
+        ts(shrink[:], shrink[:], 1.0, CLIP, ALU.add, ALU.mult)
+        ts1(shrink[:], shrink[:], 1.0, ALU.min)
+        coef_mx = small("coef_mx")
+        coef_b = small("coef_b")
+        ts(coef_b[:], m2[:], -1.0, 1.0, ALU.mult, ALU.add)
+        stt(coef_b[:], coef_b[:], scale_b, inv_den[:], ALU.mult, ALU.mult)
+        tt(coef_b[:], coef_b[:], shrink[:], ALU.mult)
+        tt(coef_mx[:], tanh_m[:], inv_mx_norm[:], ALU.mult)
+        tt(coef_mx[:], coef_mx[:], inv_den[:], ALU.mult)
+        num_m = small("num_m")
+        ts1(num_m[:], two_mh[:], h2_plus_1[:], ALU.add)
+        tt(coef_mx[:], coef_mx[:], num_m[:], ALU.mult)
+        tt(coef_mx[:], coef_mx[:], shrink[:], ALU.mult)
+        b_part = work.tile([P, TILES, D], F32, tag="a", bufs=GROUP, name="b_part")
+        p_rows = work.tile([P, TILES, D], F32, tag="z", bufs=Z_BUFS, name="p_rows")
+        p_grouped = stage_one_grouped()
         for r in range(TILES):
             c = COL[r]
-            nc.scalar.activation(out=tmp[:, r, :], in_=b_bc[:], func=AF.Copy, scale=p2[:, c : c + 1])
-            stt(p_all[:, r, :], mxs[r][:], p1[:, c : c + 1], tmp[:, r, :], ALU.mult, ALU.add)
-            tps[r] = f32_transposes(p_all, r)
+            nc.scalar.activation(out=b_part[:, r, :], in_=b_bc[:], func=AF.Copy, scale=coef_b[:, c : c + 1])
+            stt(p_rows[:, r, :], mx[r][:], coef_mx[:, c : c + 1], b_part[:, r, :], ALU.mult, ALU.add)
+            banks[r] = row_transposes(p_rows, r)
         for r in range(TILES):
-            f32_evac("av"[r % 2], tps[r], pgrp, r)
-        quantise(pgrp, pw[:], ps[:])
-        a2c = small("a2c")
-        ts(a2c[:], qn2[:], CLIP * CLIP, -1.0, ALU.min, ALU.mult)
-        ts1(a2c[:], a2c[:], 1.0, ALU.add)
-        nc.vector.reciprocal(out=a2c[:], in_=a2c[:])
-        ts1(a2c[:], a2c[:], -2.0, ALU.mult)
-        a2p = psum.tile([P, ROWS], F32, tag="s", bufs=2, name="a2p")
+            row_copy(("scalar", "vector")[r % 2], banks[r], p_grouped, r)
+        quantise(p_grouped, p_words[:], p_scales[:])
+        n2a = small("n2a")
+        ts(n2a[:], q2[:], CLIP * CLIP, -1.0, ALU.min, ALU.mult)
+        ts1(n2a[:], n2a[:], 1.0, ALU.add)
+        nc.vector.reciprocal(out=n2a[:], in_=n2a[:])
+        ts1(n2a[:], n2a[:], -2.0, ALU.mult)
+        spread = psum.tile([P, ROWS], F32, tag="s", bufs=2, name="spread")
         for r in range(TILES):
             c = COL[r]
-            nc.tensor.matmul(out=a2p[:, r * P : (r + 1) * P], lhsT=a2c[:, c : c + 1].to_broadcast([P, P]), rhs=ident[:], start=True, stop=True)
-        copy("a", a2[:], a2p[:])
+            nc.tensor.matmul(out=spread[:, r * P : (r + 1) * P], lhsT=n2a[:, c : c + 1].to_broadcast([P, P]), rhs=ident[:], start=True, stop=True)
+        copy("scalar", neg2alpha[:], spread[:])
+        four_over_t2 = small("four_over_t2", 1)
+        two_over_t = small("two_over_t", 1)
+        tt(four_over_t2[:], t_bc[:], t_bc[:], ALU.mult)
+        nc.vector.reciprocal(out=four_over_t2[:], in_=four_over_t2[:])
+        ts1(four_over_t2[:], four_over_t2[:], 4.0, ALU.mult)
+        nc.vector.tensor_copy(out=two_over_t[:], in_=t_bc[:])
+        nc.vector.reciprocal(out=two_over_t[:], in_=two_over_t[:])
+        ts1(two_over_t[:], two_over_t[:], 2.0, ALU.mult)
 
-        c2 = small("c2", 1)
-        tt(c2[:], t_bc[:], t_bc[:], ALU.mult)
-        nc.vector.reciprocal(out=c2[:], in_=c2[:])
-        ts1(c2[:], c2[:], 4.0, ALU.mult)
-        c2m = small("c2m", 1)
-        ts1(c2m[:], c2[:], 0.25, ALU.mult)
-        neg1 = small("neg1", 1)
-        nc.vector.memset(neg1[:], -1.0)
-        c1 = small("c1", 1)
-        nc.vector.tensor_copy(out=c1[:], in_=t_bc[:])
-        nc.vector.reciprocal(out=c1[:], in_=c1[:])
-        c1m = small("c1m", 1)
-        nc.vector.tensor_copy(out=c1m[:], in_=c1[:])
-        ts1(c1[:], c1[:], 2.0, ALU.mult)
+        z_tiles = {}
+        a_tiles = {}
+        log_tiles = {}
+        sums = {}
+        roots_done = [small("roots_done_%d" % g, 1) for g in range(N_GROUPS)]
+        logs_done = [small("logs_done_%d" % g, 1) for g in range(N_GROUPS)]
 
-        zbs = {}
-        betat = const.tile([P, N_UNITS, 16], F32, name="betat")
-        tok_a = [small("tok_a%d" % g, 1) for g in range(N_UNITS // GROUP)]
-        tok_b = [small("tok_b%d" % g, 1) for g in range(N_UNITS // GROUP)]
-        aas = {}
-        lqs = {}
-        es = {}
+        def vector_adds(u):
+            return u // GROUP >= FIRST_VECTOR_ADD_GROUP and u % GROUP > 0
 
-        def clip(u, t):
-            c = ycol(u, t)
-            part = zbs[u][:, t, :]
-            if CL_ENG[u] == "g":
-                nc.gpsimd.tensor_scalar(out=part, in0=part, scalar1=zmax[:, u, c : c + 1], scalar2=1.0, op0=ALU.min, op1=ALU.max)
-            else:
-                ts(part, part, zmax[:, u, c : c + 1], 1.0, ALU.min, ALU.max)
+        def scalar_squares(u):
+            return u // GROUP == N_GROUPS - 1 and u % 2 == 1
 
-        def front(u):
-            fill_to(u)
-            zb = work.tile([P, TILES, ROWS], F32, tag="zb", bufs=ZB_BUFS, name="zb")
-            zbs[u] = zb
+        def product(u):
+            z = work.tile([P, TILES, ROWS], F32, tag="z", bufs=Z_BUFS, name="z")
+            z_tiles[u] = z
+            unclipped = {}
+
+            def clip(t):
+                ts(z[:, t, :], unclipped[t][:], z_max[:, u, t : t + 1], 1.0, ALU.min, ALU.max)
+
             for t in range(TILES):
-                c = ycol(u, t)
+                codes = slice(t * P, (t + 1) * P)
                 s = psum.tile([P, ROWS], F32, tag="s", bufs=2, name="s")
-                nc.tensor.matmul_mx(
-                    out=s[:], lhsT=cws[u][:, t * P : (t + 1) * P].bitcast(FP8X4), lhsT_scale=css[u][:, t * P : (t + 1) * P],
-                    rhs=pw[:].bitcast(FP8X4), rhs_scale=ps[:], start=True, stop=True,
-                )
-                stt(zb[:, t, :], s[:], yh[:, u, c : c + 1], a2[:], ALU.add, ALU.mult)
+                mx_pass(s[:], code_words[u][:, codes], code_scales[u][:, codes], p_words[:], p_scales[:])
+                unclipped[t] = work.tile([P, ROWS], F32, tag="unclipped", bufs=3, name="unclipped")
+                stt(unclipped[t][:], s[:], shift[:, u, t : t + 1], neg2alpha[:], ALU.add, ALU.mult)
                 if t > 0:
-                    clip(u, t - 1)
-            clip(u, TILES - 1)
+                    clip(t - 1)
+            clip(TILES - 1)
 
         def roots(u):
-            zb = zbs[u]
             g = u // GROUP
             if g > 0:
-                nc.scalar.activation(out=betat[:, u, :], in_=beta[:, u, :], func=AF.Identity, bias=tok_b[g - 1][:])
+                nc.scalar.activation(out=beta_gated[:, u, :], in_=beta[:, u, :], func=AF.Identity, bias=logs_done[g - 1][:])
             else:
-                nc.scalar.copy(out=betat[:, u, :], in_=beta[:, u, :])
-            if FORM[u] == "t":
-                a = work.tile([P, TILES, ROWS], F32, tag="a", bufs=GROUP, name="a")
-                aas[u] = a
-                for t in range(TILES):
-                    c = ycol(u, t)
-                    nc.scalar.activation(out=a[:, t, :], in_=zb[:, t, :], func=AF.Sqrt, scale=betat[:, u, c : c + 1], bias=nbeta[:, u, c : c + 1])
-                    nc.scalar.activation(out=zb[:, t, :], in_=zb[:, t, :], func=AF.Sqrt, scale=betat[:, u, c : c + 1], bias=ombeta[:, u, c : c + 1])
-            else:
-                af = aas[u][:].rearrange("p t i -> p (t i)")
-                nc.scalar.activation(out=af, in_=af, func=AF.Sqrt, bias=neg1[:])
-
-        def cosh_form(u):
-            zb = zbs[u]
+                nc.scalar.copy(out=beta_gated[:, u, :], in_=beta[:, u, :])
             a = work.tile([P, TILES, ROWS], F32, tag="a", bufs=GROUP, name="a")
-            aas[u] = a
+            a_tiles[u] = a
+            z = z_tiles[u]
             for t in range(TILES):
-                c = ycol(u, t)
-                ts(zb[:, t, :], zb[:, t, :], nbeta[:, u, c : c + 1], ombeta[:, u, c : c + 1], ALU.mult, ALU.add)
-            zf = zb[:].rearrange("p t i -> p (t i)")
-            stt(a[:].rearrange("p t i -> p (t i)"), zf, 1.0, zf, ALU.mult, ALU.mult)
+                scale = beta_gated[:, u, t : t + 1]
+                nc.scalar.activation(out=a[:, t, :], in_=z[:, t, :], func=AF.Sqrt, scale=scale, bias=neg_beta[:, u, t : t + 1])
+                nc.scalar.activation(out=z[:, t, :], in_=z[:, t, :], func=AF.Sqrt, scale=scale, bias=one_minus_beta[:, u, t : t + 1])
+            if vector_adds(u):
+                tt(a[:], a[:], z[:], ALU.add)
 
-        def add_t(u, r):
-            e = psum.tile([P, UNIT], F32, tag="e", bufs=4, name="e")
-            es[(u, r)] = e
+        def turn(u, r):
+            bank = psum.tile([P, UNIT], F32, tag="sum", bufs=4, name="bank")
+            sums[(u, r)] = bank
+            rows = slice(r * P, (r + 1) * P)
             for t in range(TILES):
-                o = e[:, t * P : (t + 1) * P]
-                if ADD_ENG[u] == "p":
-                    nc.tensor.matmul(out=o, lhsT=aas[u][:, t, r * P : (r + 1) * P], rhs=ident[:], start=True, stop=False, is_transpose=True)
-                    nc.tensor.matmul(out=o, lhsT=zbs[u][:, t, r * P : (r + 1) * P], rhs=ident[:], start=False, stop=True, is_transpose=True)
+                block = bank[:, t * P : (t + 1) * P]
+                if vector_adds(u):
+                    nc.tensor.transpose(block, a_tiles[u][:, t, rows], ident[:])
                 else:
-                    nc.tensor.transpose(o, aas[u][:, t, r * P : (r + 1) * P], ident[:])
+                    nc.tensor.matmul(out=block, lhsT=a_tiles[u][:, t, rows], rhs=ident[:], start=True, stop=False, is_transpose=True)
+                    nc.tensor.matmul(out=block, lhsT=z_tiles[u][:, t, rows], rhs=ident[:], start=False, stop=True, is_transpose=True)
 
-        def log_r(u, r):
+        def logarithm(u, r):
             if r == 0:
-                lqs[u] = work.tile([P, TILES, UNIT], F32, tag="lq", bufs=GROUP, name="lq", align_bytes=64)
-            nc.scalar.activation(out=lqs[u][:, r, :], in_=es[(u, r)][:], func=AF.Ln, bias=tok_a[u // GROUP][:])
-            if SQ_ENG[u] == "a":
-                nc.scalar.activation(out=lqs[u][:, r, :], in_=lqs[u][:, r, :], func=AF.Square, scale=(c1 if FORM[u] == "t" else c1m)[:])
-            else:
-                fill_a(LN_FILL)
+                log_tiles[u] = work.tile([P, TILES, UNIT], F32, tag="log", bufs=GROUP, name="log", align_bytes=64)
+            part = log_tiles[u][:, r, :]
+            nc.scalar.activation(out=part, in_=sums[(u, r)][:], func=AF.Ln, bias=roots_done[u // GROUP][:])
+            if scalar_squares(u):
+                nc.scalar.activation(out=part, in_=part, func=AF.Square, scale=two_over_t[:])
 
-        def finish(u):
-            lq = lqs[u]
-            flat = lq[:].rearrange("p r j -> p (r j)")
-            if SQ_ENG[u] == "v":
-                stt(flat, flat, (c2 if FORM[u] == "t" else c2m)[:], flat, ALU.mult, ALU.mult)
-            fbu = fb[:, u * UNIT : (u + 1) * UNIT].unsqueeze(1).to_broadcast([P, TILES, UNIT])
-            if FB_ENG[u] == "g":
-                nc.gpsimd.tensor_tensor(out=lq[:], in0=fbu, in1=lq[:], op=ALU.subtract)
-            else:
-                tt(lq[:], fbu, lq[:], ALU.subtract)
-            nc.sync.dma_start(out=out_view[u], in_=lq[:])
+        def finish(u, values, bias, target):
+            if not scalar_squares(u):
+                stt(values, values, four_over_t2[:], values, ALU.mult, ALU.mult)
+            tt(values, bias, values, ALU.subtract)
+            nc.sync.dma_start(out=target, in_=values)
 
-        def finish_r(u, r):
-            part = lqs[u][:, r, :]
-            if SQ_ENG[u] == "v":
-                stt(part, part, (c2 if FORM[u] == "t" else c2m)[:], part, ALU.mult, ALU.mult)
-            tt(part, fb[:, u * UNIT : (u + 1) * UNIT], part, ALU.subtract)
-            nc.sync.dma_start(out=out_view[u][:, r, :], in_=part)
-
-        fill_to(HEAD_UNITS - 1)
-        for u in range(LOOKAHEAD):
-            front(u)
-        for g in range(N_UNITS // GROUP):
+        for u in range(0, PREPARE_AHEAD, 2):
+            prepare_pair(u)
+        for u in range(AHEAD):
+            product(u)
+        for g in range(N_GROUPS):
             first = g * GROUP
-            for i in range(GROUP):
-                u = first + i
-                if i == PREFILL_AT:
+            for u in range(first, first + GROUP):
+                if u == first + 1:
                     for r in range(TILES):
-                        add_t(first, r)
-                if u + LOOKAHEAD < N_UNITS:
-                    front(u + LOOKAHEAD)
+                        turn(first, r)
+                if u + AHEAD < N_UNITS:
+                    product(u + AHEAD)
                 roots(u)
-                if ADD_ENG[u] == "v":
-                    tt(aas[u][:], aas[u][:], zbs[u][:], ALU.add)
-                if u + 1 < N_UNITS and FORM[u + 1] == "m":
-                    cosh_form(u + 1)
-                fill_a(SLOT_A[0])
-                fill_v(SLOT_V[0])
-            nc.scalar.activation(out=tok_a[g][:], in_=zbs[first + GROUP - 1][:, TILES - 1, 0:1], func=AF.Copy, scale=0.0)
-            for i in range(GROUP):
-                u = first + i
+                if u % 2 == 0 and u + PREPARE_AHEAD < N_UNITS:
+                    prepare_pair(u + PREPARE_AHEAD)
+            last = first + GROUP - 1
+            nc.scalar.activation(out=roots_done[g][:], in_=z_tiles[last][:, TILES - 1, 0:1], func=AF.Copy, scale=0.0)
+            for u in range(first, first + GROUP):
+                fb_u = fb[:, u * UNIT : (u + 1) * UNIT]
                 for r in range(TILES):
-                    log_r(u, r)
-                    if i + 1 < GROUP:
-                        add_t(u + 1, r)
-                    if i == GROUP - 1 and r == TILES - 1:
-                        nc.scalar.activation(out=tok_b[g][:], in_=lqs[u][:, r, 0:1], func=AF.Copy, scale=0.0)
+                    logarithm(u, r)
+                    if u < last:
+                        turn(u + 1, r)
+                    elif r == TILES - 1:
+                        nc.scalar.activation(out=logs_done[g][:], in_=log_tiles[u][:, r, 0:1], func=AF.Copy, scale=0.0)
                     if u == N_UNITS - 1:
-                        finish_r(u, r)
+                        finish(u, log_tiles[u][:, r, :], fb_u, out_view[u][:, r, :])
                 if u < N_UNITS - 1:
-                    finish(u)
-                fill_a(SLOT_A[1])
-                fill_v(SLOT_V[1])
+                    finish(u, log_tiles[u][:], fb_u.unsqueeze(1).to_broadcast([P, TILES, UNIT]), out_view[u])

@@ -37,7 +37,7 @@ WORD_BUFS = 6
 Z_BUFS = GROUP + 2
 AHEAD = 2
 PREPARE_AHEAD = 4
-FIRST_VECTOR_ADD_GROUP = 2
+FIRST_VECTOR_ADD_GROUP = 4
 
 
 def tile_hyperbolicdistancedecoder_kernel(tc, v_tangent, code_points, W, b, freq_bias, temperature, out):

@@ -37,7 +37,7 @@ WORD_BUFS = 6
 Z_BUFS = GROUP + 2
 AHEAD = 2
 PREPARE_AHEAD = 4
-FIRST_VECTOR_ADD_GROUP = 4
+VECTOR_SUM_PAIRS = (6, 12)
 
 
 def tile_hyperbolicdistancedecoder_kernel(tc, v_tangent, code_points, W, b, freq_bias, temperature, out):
@@ -50,7 +50,7 @@ def tile_hyperbolicdistancedecoder_kernel(tc, v_tangent, code_points, W, b, freq
         v_view = v_tangent.flatten_outer_dims().rearrange("(r p) d -> p r d", p=P)
         w_view = W.rearrange("(t p) d -> p t d", p=P)
         code_view = code_points.rearrange("(u t p) d -> u p t d", t=TILES, p=P)
-        out_view = out.flatten_outer_dims().rearrange("(r p) (u j) -> u p r j", p=P, j=UNIT)
+        out_view = out.flatten_outer_dims().rearrange("(r p) (u n) -> u p r n", p=P, n=UNIT)
 
         def small(name, cols=16):
             return const.tile([P, cols], F32, name=name)
@@ -118,25 +118,25 @@ def tile_hyperbolicdistancedecoder_kernel(tc, v_tangent, code_points, W, b, freq
             raw_words = raw[:].rearrange("p t d -> p (t d)").bitcast(F32)
             for i in range(2):
                 for h in range(2):
-                    first = (2 * half + i) * (D // 2) + h * P
-                    nc.tensor.transpose(bank[:, i, h, :], raw_words[:, first : first + P], ident[:])
+                    start = (2 * half + i) * (D // 2) + h * P
+                    nc.tensor.transpose(bank[:, i, h, :], raw_words[:, start : start + P], ident[:])
             return bank
 
         def word_copy(engine, bank, grouped, half):
             dst = grouped[:].bitcast(F32).rearrange("p (c h) -> p c h", h=2)[:, half * 2 * P : (half + 1) * 2 * P, :]
             copy(engine, dst.rearrange("p (i c) h -> p i c h", i=2), bank[:].rearrange("p i h c -> p i c h"))
 
-        def row_transposes(rows, r):
+        def row_transposes(values, r):
             bank = psum.tile([P, 4, P], F32, tag="sum", bufs=4, name="bank")
-            view = rows[:, r, :].rearrange("p (h q e) -> p h e q", h=2, e=2)
+            view = values[:, r, :].rearrange("p (h q e) -> p h e q", h=2, e=2)
             for h in range(2):
                 for e in range(2):
                     nc.tensor.transpose(bank[:, 2 * h + e, :], view[:, h, e, :], ident[:])
             return bank
 
         def row_copy(engine, bank, grouped, r):
-            dst = grouped[:].rearrange("p (c t) -> p c t", t=4)[:, r * P : (r + 1) * P, :]
-            copy(engine, dst, bank[:].rearrange("p t c -> p c t"))
+            dst = grouped[:].rearrange("p (c j) -> p c j", j=4)[:, r * P : (r + 1) * P, :]
+            copy(engine, dst, bank[:].rearrange("p j c -> p c j"))
 
         def stage_one_grouped():
             return work.tile([P, 4 * ROWS], BF16, tag="log", bufs=GROUP, name="grouped", align_bytes=64)
@@ -167,7 +167,10 @@ def tile_hyperbolicdistancedecoder_kernel(tc, v_tangent, code_points, W, b, freq
                 code_scales[u] = work.tile([P, UNIT], U8, tag="code_scales", bufs=WORD_BUFS, name="scales", align_bytes=64)
                 quantise(grouped[u], code_words[u][:], code_scales[u][:])
                 for t in range(TILES):
-                    sum_of_squares_scalar(raws[u][:, t, :], y2[:, u, t : t + 1])
+                    if first in VECTOR_SUM_PAIRS:
+                        dot_vector(raws[u][:, t, :], raws[u][:, t, :], y2[:, u, t : t + 1])
+                    else:
+                        sum_of_squares_scalar(raws[u][:, t, :], y2[:, u, t : t + 1])
                 load_next_unit()
 
             def pair(values):
@@ -248,14 +251,14 @@ def tile_hyperbolicdistancedecoder_kernel(tc, v_tangent, code_points, W, b, freq
             dot_vector(mx_again[:], b_bc[:], mx_b[:, c : c + 1])
         rho = small("rho")
         atanh_x = small("atanh_x")
-        h2 = small("h2", 1)
-        h2_plus_1 = small("h2_plus_1", 1)
+        bh2 = small("bh2", 1)
+        bh2_plus_1 = small("bh2_plus_1", 1)
         ts1(atanh_x[:], norm_floor[:], ATANH_CLIP, ALU.min)
         ts1(rho[:], tanh_n[:], TINY, ALU.max)
         nc.vector.reciprocal(out=rho[:], in_=rho[:])
         tt(rho[:], rho[:], atanh_x[:], ALU.mult)
-        tt(h2[:], tanh_n[:, BCOL : BCOL + 1], tanh_n[:, BCOL : BCOL + 1], ALU.mult)
-        ts1(h2_plus_1[:], h2[:], 1.0, ALU.add)
+        tt(bh2[:], tanh_n[:, BCOL : BCOL + 1], tanh_n[:, BCOL : BCOL + 1], ALU.mult)
+        ts1(bh2_plus_1[:], bh2[:], 1.0, ALU.add)
         scale_b = scale_x[:, BCOL : BCOL + 1]
         mx_norm = small("mx_norm")
         inv_mx_norm = small("inv_mx_norm")
@@ -270,15 +273,15 @@ def tile_hyperbolicdistancedecoder_kernel(tc, v_tangent, code_points, W, b, freq
         dot_unit = small("dot_unit")
         stt(dot_unit[:], mx_b[:], scale_b, inv_mx_norm[:], ALU.mult, ALU.mult)
         m2 = small("m2")
-        two_mh = small("two_mh")
+        two_mbh = small("two_mbh")
         inv_den = small("inv_den")
         q2 = small("q2")
         tt(m2[:], tanh_m[:], tanh_m[:], ALU.mult)
-        stt(two_mh[:], tanh_m[:], 2.0, dot_unit[:], ALU.mult, ALU.mult)
-        stt(inv_den[:], m2[:], h2[:], two_mh[:], ALU.mult, ALU.add)
+        stt(two_mbh[:], tanh_m[:], 2.0, dot_unit[:], ALU.mult, ALU.mult)
+        stt(inv_den[:], m2[:], bh2[:], two_mbh[:], ALU.mult, ALU.add)
         ts(inv_den[:], inv_den[:], 1.0, TINY, ALU.add, ALU.max)
         nc.vector.reciprocal(out=inv_den[:], in_=inv_den[:])
-        stt(q2[:], m2[:], h2[:], two_mh[:], ALU.add, ALU.add)
+        stt(q2[:], m2[:], bh2[:], two_mbh[:], ALU.add, ALU.add)
         stt(q2[:], q2[:], 0.0, inv_den[:], ALU.max, ALU.mult)
         d_q = small("d_q")
         shrink = small("shrink")
@@ -295,7 +298,7 @@ def tile_hyperbolicdistancedecoder_kernel(tc, v_tangent, code_points, W, b, freq
         tt(coef_mx[:], tanh_m[:], inv_mx_norm[:], ALU.mult)
         tt(coef_mx[:], coef_mx[:], inv_den[:], ALU.mult)
         num_m = small("num_m")
-        ts1(num_m[:], two_mh[:], h2_plus_1[:], ALU.add)
+        ts1(num_m[:], two_mbh[:], bh2_plus_1[:], ALU.add)
         tt(coef_mx[:], coef_mx[:], num_m[:], ALU.mult)
         tt(coef_mx[:], coef_mx[:], shrink[:], ALU.mult)
         b_part = work.tile([P, TILES, D], F32, tag="a", bufs=GROUP, name="b_part")
@@ -335,9 +338,6 @@ def tile_hyperbolicdistancedecoder_kernel(tc, v_tangent, code_points, W, b, freq
         roots_done = [small("roots_done_%d" % g, 1) for g in range(N_GROUPS)]
         logs_done = [small("logs_done_%d" % g, 1) for g in range(N_GROUPS)]
 
-        def vector_adds(u):
-            return u // GROUP >= FIRST_VECTOR_ADD_GROUP and u % GROUP > 0
-
         def scalar_squares(u):
             return u // GROUP == N_GROUPS - 1 and u % 2 == 1
 
@@ -372,8 +372,6 @@ def tile_hyperbolicdistancedecoder_kernel(tc, v_tangent, code_points, W, b, freq
                 scale = beta_gated[:, u, t : t + 1]
                 nc.scalar.activation(out=a[:, t, :], in_=z[:, t, :], func=AF.Sqrt, scale=scale, bias=neg_beta[:, u, t : t + 1])
                 nc.scalar.activation(out=z[:, t, :], in_=z[:, t, :], func=AF.Sqrt, scale=scale, bias=one_minus_beta[:, u, t : t + 1])
-            if vector_adds(u):
-                tt(a[:], a[:], z[:], ALU.add)
 
         def turn(u, r):
             bank = psum.tile([P, UNIT], F32, tag="sum", bufs=4, name="bank")
@@ -381,11 +379,8 @@ def tile_hyperbolicdistancedecoder_kernel(tc, v_tangent, code_points, W, b, freq
             rows = slice(r * P, (r + 1) * P)
             for t in range(TILES):
                 block = bank[:, t * P : (t + 1) * P]
-                if vector_adds(u):
-                    nc.tensor.transpose(block, a_tiles[u][:, t, rows], ident[:])
-                else:
-                    nc.tensor.matmul(out=block, lhsT=a_tiles[u][:, t, rows], rhs=ident[:], start=True, stop=False, is_transpose=True)
-                    nc.tensor.matmul(out=block, lhsT=z_tiles[u][:, t, rows], rhs=ident[:], start=False, stop=True, is_transpose=True)
+                nc.tensor.matmul(out=block, lhsT=a_tiles[u][:, t, rows], rhs=ident[:], start=True, stop=False, is_transpose=True)
+                nc.tensor.matmul(out=block, lhsT=z_tiles[u][:, t, rows], rhs=ident[:], start=False, stop=True, is_transpose=True)
 
         def logarithm(u, r):
             if r == 0:

@@ -32,8 +32,8 @@ GAP_MIN = 1e-8
 COL = (0, 1, 8, 9)
 BCOL = 2
 
-RAW_BUFS = 6
-WORD_BUFS = 6
+RAW_BUFS = 10
+WORD_BUFS = 10
 Z_BUFS = GROUP + 2
 AHEAD = 2
 PREPARE_AHEAD = 4
@@ -347,7 +347,9 @@ def tile_hyperbolicdistancedecoder_kernel(tc, v_tangent, code_points, W, b, freq
             unclipped = {}
 
             def clip(t):
-                ts(z[:, t, :], unclipped[t][:], z_max[:, u, t : t + 1], 1.0, ALU.min, ALU.max)
+                nc.gpsimd.tensor_scalar(
+                    out=z[:, t, :], in0=unclipped[t][:], scalar1=z_max[:, u, t : t + 1], scalar2=1.0, op0=ALU.min, op1=ALU.max
+                )
 
             for t in range(TILES):
                 codes = slice(t * P, (t + 1) * P)

@@ -19,8 +19,7 @@ CODES = 8192
 TILES = 4
 UNIT = TILES * P
 N_UNITS = CODES // UNIT
-GROUP = 4
-N_GROUPS = N_UNITS // GROUP
+GROUPS = (4, 4, 4, 4)
 FLOPS = 2 * ROWS * D * D + 2 * ROWS * CODES * D
 
 CLIP = 1.0 - 1e-5
@@ -29,20 +28,35 @@ T_MAX = CLIP * CLIP / (1.0 - CLIP * CLIP)
 TINY = 1e-15
 GAP_MIN = 1e-8
 
-COL = (0, 1, 8, 9)
-BCOL = 2
+COLS = 5
+BCOL = 4
 
 RAW_BUFS = 10
-WORD_BUFS = 10
-Z_BUFS = GROUP + 2
-AHEAD = 2
-PREPARE_AHEAD = 4
-VECTOR_SUM_PAIRS = (6, 12)
+WORD_BUFS = 6
+A_BUFS = max(GROUPS)
+LOG_BUFS = 4
+AHEAD = 4
+TURN_AT = 1
+ADV_ROOT = ((1, 1, 1, 1), (0, 1, 1, 0), (0, 1, 1, 0), (0, 1, 1, 0))
+ADV_LOG = ((0, 0, 1, 1), (0, 0, 1, 1), (0, 0, 1, 1), (0, 0, 0, 0))
+BATCHES = ((0, 1), (1, 2), (2, 3), (3, 4), (4, 5), (5, 6), (6, 8), (8, 12), (12, 14), (14, 16))
+ROOT_SUMS = ((3, 4, 4, 4), (0, 0, 0, 0), (0, 0, 0, 0), (0, 0, 0, 0))
+LOG_SUMS = (3, 3, 4, 0)
+Z_BUFS = max(GROUPS) + AHEAD
+CLIP_G = tuple(range(1, 16))
+SQUARE_G = tuple(range(14))
+SQUARE_S = (14, 15)
+FB_PSUM = True
+SUM_V = ()
+VECTOR_ADDS = (2, 6, 10, 13, 14, 15)
+KEEP = 1
+FINISH_FROM = 0
 
 
 def tile_hyperbolicdistancedecoder_kernel(tc, v_tangent, code_points, W, b, freq_bias, temperature, out):
     nc = tc.nc
     with ExitStack() as ctx:
+        ctx.enter_context(tc.manual_schedule())
         const = ctx.enter_context(tc.tile_pool(name="const", bufs=1))
         work = ctx.enter_context(tc.tile_pool(name="work", bufs=1))
         psum = ctx.enter_context(tc.psum_pool(name="psum", bufs=1))
@@ -52,7 +66,7 @@ def tile_hyperbolicdistancedecoder_kernel(tc, v_tangent, code_points, W, b, freq
         code_view = code_points.rearrange("(u t p) d -> u p t d", t=TILES, p=P)
         out_view = out.flatten_outer_dims().rearrange("(r p) (u n) -> u p r n", p=P, n=UNIT)
 
-        def small(name, cols=16):
+        def small(name, cols=COLS):
             return const.tile([P, cols], F32, name=name)
 
         def per_code(name):
@@ -63,6 +77,7 @@ def tile_hyperbolicdistancedecoder_kernel(tc, v_tangent, code_points, W, b, freq
         b_bc = const.tile([P, D], BF16, name="b_bc")
         t_bc = const.tile([P, 1], BF16, name="t_bc")
         fb = const.tile([P, CODES], BF16, name="fb")
+        ones = const.tile([P, P], BF16, name="ones")
         x_words = const.tile([P, ROWS], U32, name="x_words", align_bytes=64)
         x_scales = const.tile([P, ROWS], U8, name="x_scales", align_bytes=64)
         w_words = const.tile([P, D], U32, name="w_words", align_bytes=64)
@@ -70,12 +85,11 @@ def tile_hyperbolicdistancedecoder_kernel(tc, v_tangent, code_points, W, b, freq
         p_words = const.tile([P, ROWS], U32, name="p_words", align_bytes=64)
         p_scales = const.tile([P, ROWS], U8, name="p_scales", align_bytes=64)
         unread_a = const.tile([P, D], BF16, name="unread_a")
-        unread_v = const.tile([P, D], F32, name="unread_v")
+        unread_v = const.tile([P, D], BF16, name="unread_v")
         y2 = per_code("y2")
         shift = per_code("shift")
         gap = per_code("gap")
         beta = per_code("beta")
-        beta_gated = per_code("beta_gated")
         neg_beta = per_code("neg_beta")
         one_minus_beta = per_code("one_minus_beta")
         z_max = per_code("z_max")
@@ -91,6 +105,9 @@ def tile_hyperbolicdistancedecoder_kernel(tc, v_tangent, code_points, W, b, freq
 
         def tt(o, i0, i1, op):
             nc.vector.tensor_tensor(out=o, in0=i0, in1=i1, op=op)
+
+        def power(o, i, exponent):
+            nc.gpsimd.tensor_tensor(out=o, in0=i, in1=exponent, op=ALU.pow)
 
         def sum_of_squares_scalar(src, acc):
             nc.scalar.activation(out=unread_a[:], in_=src, func=AF.Square, accum_out=acc)
@@ -113,8 +130,8 @@ def tile_hyperbolicdistancedecoder_kernel(tc, v_tangent, code_points, W, b, freq
         def quantise(grouped, words, scales):
             nc.vector.quantize_mx(out=words.bitcast(FP8X4), scales=scales, in_=grouped[:])
 
-        def word_transposes(raw, half):
-            bank = psum.tile([P, 2, 2, P], F32, tag="words", bufs=2, name="bank")
+        def word_transposes(raw, half, tag):
+            bank = psum.tile([P, 2, 2, P], F32, tag=tag, bufs=4 if tag == "sum" else 2, name="bank")
             raw_words = raw[:].rearrange("p t d -> p (t d)").bitcast(F32)
             for i in range(2):
                 for h in range(2):
@@ -126,24 +143,14 @@ def tile_hyperbolicdistancedecoder_kernel(tc, v_tangent, code_points, W, b, freq
             dst = grouped[:].bitcast(F32).rearrange("p (c h) -> p c h", h=2)[:, half * 2 * P : (half + 1) * 2 * P, :]
             copy(engine, dst.rearrange("p (i c) h -> p i c h", i=2), bank[:].rearrange("p i h c -> p i c h"))
 
-        def row_transposes(values, r):
-            bank = psum.tile([P, 4, P], F32, tag="sum", bufs=4, name="bank")
-            view = values[:, r, :].rearrange("p (h q e) -> p h e q", h=2, e=2)
-            for h in range(2):
-                for e in range(2):
-                    nc.tensor.transpose(bank[:, 2 * h + e, :], view[:, h, e, :], ident[:])
-            return bank
-
-        def row_copy(engine, bank, grouped, r):
-            dst = grouped[:].rearrange("p (c j) -> p c j", j=4)[:, r * P : (r + 1) * P, :]
-            copy(engine, dst, bank[:].rearrange("p j c -> p c j"))
-
-        def stage_one_grouped():
-            return work.tile([P, 4 * ROWS], BF16, tag="log", bufs=GROUP, name="grouped", align_bytes=64)
+        def grouped_tile(tag, bufs):
+            return work.tile([P, 4 * ROWS], BF16, tag=tag, bufs=bufs, name="grouped", align_bytes=64)
 
         raws = {}
         code_words = {}
         code_scales = {}
+        banks = {}
+        grouped = {}
         loaded = []
 
         def load_next_unit():
@@ -154,276 +161,385 @@ def tile_hyperbolicdistancedecoder_kernel(tc, v_tangent, code_points, W, b, freq
                 raws[u] = raw
                 loaded.append(u)
 
-        def prepare_pair(first):
-            pair_units = (first, first + 1)
-            grouped = {}
-            for u in pair_units:
-                word_banks = [word_transposes(raws[u], half) for half in range(2)]
-                grouped[u] = work.tile([P, 4 * UNIT], BF16, tag="grouped", bufs=2, name="grouped", align_bytes=64)
-                for half in range(2):
-                    word_copy("vector", word_banks[half], grouped[u], half)
-            for u in pair_units:
-                code_words[u] = work.tile([P, UNIT], U32, tag="code_words", bufs=WORD_BUFS, name="words", align_bytes=64)
-                code_scales[u] = work.tile([P, UNIT], U8, tag="code_scales", bufs=WORD_BUFS, name="scales", align_bytes=64)
-                quantise(grouped[u], code_words[u][:], code_scales[u][:])
-                for t in range(TILES):
-                    if first in VECTOR_SUM_PAIRS:
-                        dot_vector(raws[u][:, t, :], raws[u][:, t, :], y2[:, u, t : t + 1])
-                    else:
-                        sum_of_squares_scalar(raws[u][:, t, :], y2[:, u, t : t + 1])
-                load_next_unit()
+        def turn_words(u):
+            banks[u] = [word_transposes(raws[u], half, "words") for half in range(2)]
+            grouped[u] = grouped_tile("grouped", 2)
 
-            def pair(values):
-                return values[:, first : first + 2, :].rearrange("p u t -> p (u t)")
+        def quantise_words(u):
+            code_words[u] = work.tile([P, UNIT], U32, tag="code_words", bufs=WORD_BUFS, name="words", align_bytes=64)
+            code_scales[u] = work.tile([P, UNIT], U8, tag="code_scales", bufs=WORD_BUFS, name="scales", align_bytes=64)
+            quantise(grouped[u], code_words[u][:], code_scales[u][:])
 
-            ts(pair(shift), pair(y2), -0.5, -0.5, ALU.mult, ALU.add)
-            ts(pair(gap), pair(y2), -1.0, 1.0, ALU.mult, ALU.add)
-            ts1(pair(gap), pair(gap), GAP_MIN, ALU.max)
-            nc.vector.reciprocal(out=pair(beta), in_=pair(gap))
-            ts1(pair(neg_beta), pair(beta), -1.0, ALU.mult)
-            ts(pair(one_minus_beta), pair(beta), -1.0, 1.0, ALU.mult, ALU.add)
-            ts(pair(z_max), pair(gap), T_MAX, 1.0, ALU.mult, ALU.add)
+        def sum_scalar(u, t):
+            sum_of_squares_scalar(raws[u][:, t, :], y2[:, u, t : t + 1])
+
+        def sum_vector(u, t):
+            dot_vector(raws[u][:, t, :], raws[u][:, t, :], y2[:, u, t : t + 1])
+
+        waiting = []
+
+        def trickle(count=1):
+            for i in range(count):
+                if waiting:
+                    waiting.pop(0)()
+
+        def code_scalars(first, last):
+            def some(values):
+                return values[:, first:last, :].rearrange("p u t -> p (u t)")
+
+            waiting.append(lambda: ts(some(gap), some(y2), -1.0, 1.0, ALU.mult, ALU.add))
+            waiting.append(lambda: ts(some(shift), some(y2), -0.5, -0.5, ALU.mult, ALU.add))
+            waiting.append(lambda: ts1(some(gap), some(gap), GAP_MIN, ALU.max))
+            waiting.append(lambda: nc.vector.reciprocal(out=some(beta), in_=some(gap)))
+            waiting.append(lambda: ts1(some(neg_beta), some(beta), -1.0, ALU.mult))
+            waiting.append(lambda: ts(some(one_minus_beta), some(beta), -1.0, 1.0, ALU.mult, ALU.add))
+            waiting.append(lambda: (ts(some(z_max), some(gap), T_MAX, 1.0, ALU.mult, ALU.add), ready.append(last)))
+
+        scaled = [0]
+        ready = [0]
+        vector_sums = [(u, t) for u in range(6, N_UNITS) for t in SUM_V]
+        sums_todo = [(u, t) for u in range(N_UNITS) for t in range(TILES) if (u, t) not in vector_sums]
+
+        def fill(count):
+            for i in range(count):
+                if not sums_todo:
+                    break
+                u, t = sums_todo.pop(0)
+                sum_scalar(u, t)
+                for first, last in BATCHES:
+                    if u == last - 1 and (u + 1 == N_UNITS and not sums_todo or sums_todo and sums_todo[0][0] == last):
+                        code_scalars(first, last)
+                        scaled.append(last)
+                        while len(loaded) < last + 6:
+                            if len(loaded) == N_UNITS:
+                                break
+                            load_next_unit()
+
+        def ensure(u):
+            while scaled[-1] <= u:
+                fill(1)
+            while ready[-1] <= u:
+                trickle()
 
         norm2 = small("norm2")
         mx2 = small("mx2")
         mx_b = small("mx_b")
         tanh_m = small("tanh_m")
+        half = small("half")
         warm = small("warm", 1)
-        nc.vector.memset(warm[:], 1.0)
+        nc.vector.memset(warm[:], 0.0)
         nc.vector.memset(norm2[:], 1.0)
         nc.vector.memset(mx2[:], 1.0)
         nc.vector.memset(mx_b[:], 0.0)
-        nc.vector.memset(tanh_m[:], 0.0)
+        nc.gpsimd.memset(half[:], 0.5)
         raw_v = work.tile([P, TILES, D], BF16, tag="raw", bufs=RAW_BUFS, name="raw_v")
-        nc.sync.dma_start(out=raw_v[:], in_=v_view)
+        for r in (0, 2, 1, 3):
+            nc.sync.dma_start(out=raw_v[:, r, :], in_=v_view[:, r, :])
+        nc.scalar.dma_start(out=b_bc[:], in_=b.partition_broadcast(P))
         raw_w = work.tile([P, TILES, D], BF16, tag="raw", bufs=RAW_BUFS, name="raw_w")
         nc.sync.dma_start(out=raw_w[:], in_=w_view)
-        nc.scalar.dma_start(out=b_bc[:], in_=b.partition_broadcast(P))
         nc.scalar.dma_start(out=t_bc[:], in_=temperature.partition_broadcast(P))
         for i in range(RAW_BUFS - 2):
             load_next_unit()
         make_identity(nc, ident[:])
-        nc.gpsimd.dma_start(out=fb[:], in_=freq_bias.partition_broadcast(P))
-        nc.scalar.activation(out=warm[:], in_=warm[:], func=AF.Sqrt)
+        nc.scalar.activation(out=warm[:], in_=warm[:], func=AF.Tanh)
+        if FB_PSUM:
+            nc.gpsimd.memset(ones[:], 1.0)
 
+        sum_of_squares_scalar(raw_v[:, 0, :], norm2[:, 0:1])
+        dot_vector(raw_v[:, 2, :], raw_v[:, 2, :], norm2[:, 2:3])
+        sum_of_squares_scalar(raw_v[:, 1, :], norm2[:, 1:2])
+        dot_vector(raw_v[:, 3, :], raw_v[:, 3, :], norm2[:, 3:4])
         sum_of_squares_scalar(b_bc[:], norm2[:, BCOL : BCOL + 1])
-        sum_of_squares_scalar(raw_v[:, 0, :], norm2[:, COL[0] : COL[0] + 1])
-        dot_vector(raw_v[:, 2, :], raw_v[:, 2, :], norm2[:, COL[2] : COL[2] + 1])
-        sum_of_squares_scalar(raw_v[:, 1, :], norm2[:, COL[1] : COL[1] + 1])
-        dot_vector(raw_v[:, 3, :], raw_v[:, 3, :], norm2[:, COL[3] : COL[3] + 1])
+        norm2_floor = small("norm2_floor")
         norm = small("norm")
-        norm_floor = small("norm_floor")
+        inv_norm = small("inv_norm")
         tanh_n = small("tanh_n")
         scale_x = small("scale_x")
-        nc.scalar.activation(out=norm[:], in_=norm2[:], func=AF.Sqrt)
-        nc.scalar.activation(out=tanh_n[:], in_=norm[:], func=AF.Tanh)
-        warm_2 = small("warm_2", 1)
-        nc.scalar.activation(out=warm_2[:], in_=tanh_n[:, 0:1], func=AF.Sqrt)
-        ts1(norm_floor[:], norm[:], TINY, ALU.max)
-        nc.vector.reciprocal(out=scale_x[:], in_=norm_floor[:])
-        tt(scale_x[:], tanh_n[:], scale_x[:], ALU.mult)
-        x_rows = work.tile([P, TILES, D], F32, tag="z", bufs=Z_BUFS, name="x_rows")
-        banks = {}
-        for r in range(TILES):
-            c = COL[r]
-            ts1(x_rows[:, r, :], raw_v[:, r, :], scale_x[:, c : c + 1], ALU.mult)
-            banks[r] = row_transposes(x_rows, r)
-        x_grouped = stage_one_grouped()
-        for r in range(TILES):
-            row_copy(("scalar", "vector")[r % 2], banks[r], x_grouped, r)
-        w_banks = [word_transposes(raw_w, half) for half in range(2)]
-        w_grouped = stage_one_grouped()
+        w_banks = [word_transposes(raw_w, i, "words") for i in range(2)]
+        w_grouped = grouped_tile("log", LOG_BUFS)
+        ts1(norm2_floor[:], norm2[:], TINY * TINY, ALU.max)
+        power(norm[:], norm2_floor[:], half[:])
         word_copy("vector", w_banks[0], w_grouped, 0)
+        nc.vector.reciprocal(out=inv_norm[:], in_=norm[:])
+        nc.scalar.activation(out=tanh_n[:], in_=norm[:], func=AF.Tanh)
+        tt(scale_x[:], tanh_n[:], inv_norm[:], ALU.mult)
         word_copy("scalar", w_banks[1], w_grouped, 1)
-        load_next_unit()
-        load_next_unit()
+        fill(1)
+        x_rows = work.tile([P, TILES, D], BF16, tag="a", bufs=A_BUFS, name="x_rows")
+        for r in range(TILES):
+            ts1(x_rows[:, r, :], raw_v[:, r, :], scale_x[:, r : r + 1], ALU.mult)
+        x_banks = [word_transposes(x_rows, i, "sum") for i in range(2)]
+        turn_words(0)
+        x_grouped = grouped_tile("log", LOG_BUFS)
         quantise(w_grouped, w_words[:], w_scales[:])
+        word_copy("scalar", x_banks[0], x_grouped, 0)
+        rho = small("rho")
+        inv_x = small("inv_x")
+        bh2 = small("bh2", 1)
+        bh2_plus_1 = small("bh2_plus_1", 1)
+        ts1(inv_x[:], tanh_n[:], TINY, ALU.max)
+        word_copy("vector", x_banks[1], x_grouped, 1)
+        nc.vector.reciprocal(out=inv_x[:], in_=inv_x[:])
         quantise(x_grouped, x_words[:], x_scales[:])
+        stt(rho[:], norm[:], ATANH_CLIP, inv_x[:], ALU.min, ALU.mult)
+        tt(bh2[:], tanh_n[:, BCOL : BCOL + 1], tanh_n[:, BCOL : BCOL + 1], ALU.mult)
+        ts1(bh2_plus_1[:], bh2[:], 1.0, ALU.add)
+        minus_four_over_t2 = small("minus_four_over_t2", 1)
+        q_min = small("q_min", 1)
+        tt(minus_four_over_t2[:], t_bc[:], t_bc[:], ALU.mult)
+        nc.vector.reciprocal(out=minus_four_over_t2[:], in_=minus_four_over_t2[:])
+        waiting.append(lambda: ts1(minus_four_over_t2[:], minus_four_over_t2[:], -4.0, ALU.mult))
+        waiting.append(lambda: ts1(q_min[:], minus_four_over_t2[:], ATANH_CLIP * ATANH_CLIP, ALU.mult))
+        fill(1)
+        word_copy("scalar", banks[0][0], grouped[0], 0)
+        word_copy("scalar", banks[0][1], grouped[0], 1)
         mx = {}
         for r in range(TILES):
-            c = COL[r]
             rows = slice(r * P, (r + 1) * P)
             mx[r] = psum.tile([P, D], F32, tag="sum", bufs=4, name="mx")
             mx_pass(mx[r][:], x_words[:, rows], x_scales[:, rows], w_words[:], w_scales[:])
-            nc.scalar.activation(out=unread_a[:], in_=mx[r][:], func=AF.Square, accum_out=mx2[:, c : c + 1])
+            nc.scalar.activation(out=unread_a[:], in_=mx[r][:], func=AF.Square, accum_out=mx2[:, r : r + 1])
             mx_again = psum.tile([P, D], F32, tag="s", bufs=2, name="mx_again")
             mx_pass(mx_again[:], x_words[:, rows], x_scales[:, rows], w_words[:], w_scales[:])
-            dot_vector(mx_again[:], b_bc[:], mx_b[:, c : c + 1])
-        rho = small("rho")
-        atanh_x = small("atanh_x")
-        bh2 = small("bh2", 1)
-        bh2_plus_1 = small("bh2_plus_1", 1)
-        ts1(atanh_x[:], norm_floor[:], ATANH_CLIP, ALU.min)
-        ts1(rho[:], tanh_n[:], TINY, ALU.max)
-        nc.vector.reciprocal(out=rho[:], in_=rho[:])
-        tt(rho[:], rho[:], atanh_x[:], ALU.mult)
-        tt(bh2[:], tanh_n[:, BCOL : BCOL + 1], tanh_n[:, BCOL : BCOL + 1], ALU.mult)
-        ts1(bh2_plus_1[:], bh2[:], 1.0, ALU.add)
+            dot_vector(mx_again[:], b_bc[:], mx_b[:, r : r + 1])
+            trickle()
+        fill(1)
+        turn_words(1)
+        load_next_unit()
+        load_next_unit()
         scale_b = scale_x[:, BCOL : BCOL + 1]
+        arg = small("arg")
+        mx2_floor = small("mx2_floor")
         mx_norm = small("mx_norm")
         inv_mx_norm = small("inv_mx_norm")
-        nc.scalar.activation(out=mx_norm[:], in_=mx2[:], func=AF.Sqrt)
-        for r in range(TILES):
-            c = COL[r]
-            nc.scalar.activation(out=tanh_m[:, c : c + 1], in_=mx_norm[:, c : c + 1], func=AF.Tanh, scale=rho[:, c : c + 1])
-        warm_3 = small("warm_3", 1)
-        nc.scalar.activation(out=warm_3[:], in_=tanh_m[:, COL[3] : COL[3] + 1], func=AF.Sqrt)
-        ts1(inv_mx_norm[:], mx_norm[:], TINY, ALU.max)
-        nc.vector.reciprocal(out=inv_mx_norm[:], in_=inv_mx_norm[:])
         dot_unit = small("dot_unit")
+        ts1(mx2_floor[:], mx2[:], TINY * TINY, ALU.max)
+        power(mx_norm[:], mx2_floor[:], half[:])
+        word_copy("vector", banks[1][0], grouped[1], 0)
+        tt(arg[:], mx_norm[:], rho[:], ALU.mult)
+        nc.scalar.activation(out=tanh_m[:], in_=arg[:], func=AF.Tanh)
+        nc.vector.reciprocal(out=inv_mx_norm[:], in_=mx_norm[:])
+        warm_2 = small("warm_2", 1)
+        nc.scalar.activation(out=warm_2[:], in_=tanh_m[:, 0:1], func=AF.Sqrt)
         stt(dot_unit[:], mx_b[:], scale_b, inv_mx_norm[:], ALU.mult, ALU.mult)
+        quantise_words(0)
+        fill(3)
         m2 = small("m2")
         two_mbh = small("two_mbh")
+        m_scale = small("m_scale")
         inv_den = small("inv_den")
         q2 = small("q2")
-        tt(m2[:], tanh_m[:], tanh_m[:], ALU.mult)
-        stt(two_mbh[:], tanh_m[:], 2.0, dot_unit[:], ALU.mult, ALU.mult)
-        stt(inv_den[:], m2[:], bh2[:], two_mbh[:], ALU.mult, ALU.add)
-        ts(inv_den[:], inv_den[:], 1.0, TINY, ALU.add, ALU.max)
-        nc.vector.reciprocal(out=inv_den[:], in_=inv_den[:])
-        stt(q2[:], m2[:], bh2[:], two_mbh[:], ALU.add, ALU.add)
-        stt(q2[:], q2[:], 0.0, inv_den[:], ALU.max, ALU.mult)
-        d_q = small("d_q")
         shrink = small("shrink")
-        ts1(d_q[:], q2[:], -1.0, ALU.add)
-        ts(shrink[:], d_q[:], 0.375, -0.5, ALU.mult, ALU.add)
-        tt(shrink[:], shrink[:], d_q[:], ALU.mult)
-        ts(shrink[:], shrink[:], 1.0, CLIP, ALU.add, ALU.mult)
-        ts1(shrink[:], shrink[:], 1.0, ALU.min)
+        num_m = small("num_m")
         coef_mx = small("coef_mx")
         coef_b = small("coef_b")
+        tt(m2[:], tanh_m[:], tanh_m[:], ALU.mult)
+        stt(two_mbh[:], tanh_m[:], 2.0, dot_unit[:], ALU.mult, ALU.mult)
+        tt(m_scale[:], tanh_m[:], inv_mx_norm[:], ALU.mult)
+        stt(inv_den[:], m2[:], bh2[:], two_mbh[:], ALU.mult, ALU.add)
+        stt(q2[:], m2[:], bh2[:], two_mbh[:], ALU.add, ALU.add)
+        ts(inv_den[:], inv_den[:], 1.0, TINY, ALU.add, ALU.max)
+        stt(num_m[:], two_mbh[:], bh2_plus_1[:], m_scale[:], ALU.add, ALU.mult)
+        nc.vector.reciprocal(out=inv_den[:], in_=inv_den[:])
         ts(coef_b[:], m2[:], -1.0, 1.0, ALU.mult, ALU.add)
-        stt(coef_b[:], coef_b[:], scale_b, inv_den[:], ALU.mult, ALU.mult)
-        tt(coef_b[:], coef_b[:], shrink[:], ALU.mult)
-        tt(coef_mx[:], tanh_m[:], inv_mx_norm[:], ALU.mult)
-        tt(coef_mx[:], coef_mx[:], inv_den[:], ALU.mult)
-        num_m = small("num_m")
-        ts1(num_m[:], two_mbh[:], bh2_plus_1[:], ALU.add)
-        tt(coef_mx[:], coef_mx[:], num_m[:], ALU.mult)
-        tt(coef_mx[:], coef_mx[:], shrink[:], ALU.mult)
-        b_part = work.tile([P, TILES, D], F32, tag="a", bufs=GROUP, name="b_part")
-        p_rows = work.tile([P, TILES, D], F32, tag="z", bufs=Z_BUFS, name="p_rows")
-        p_grouped = stage_one_grouped()
-        for r in range(TILES):
-            c = COL[r]
-            nc.scalar.activation(out=b_part[:, r, :], in_=b_bc[:], func=AF.Copy, scale=coef_b[:, c : c + 1])
-            stt(p_rows[:, r, :], mx[r][:], coef_mx[:, c : c + 1], b_part[:, r, :], ALU.mult, ALU.add)
-            banks[r] = row_transposes(p_rows, r)
-        for r in range(TILES):
-            row_copy(("scalar", "vector")[r % 2], banks[r], p_grouped, r)
-        quantise(p_grouped, p_words[:], p_scales[:])
+        stt(q2[:], q2[:], 0.0, inv_den[:], ALU.max, ALU.mult)
+        ts1(coef_b[:], coef_b[:], scale_b, ALU.mult)
+        ts(shrink[:], q2[:], -0.5 * CLIP, 1.5 * CLIP, ALU.mult, ALU.add)
         n2a = small("n2a")
-        ts(n2a[:], q2[:], CLIP * CLIP, -1.0, ALU.min, ALU.mult)
-        ts1(n2a[:], n2a[:], 1.0, ALU.add)
+        ts(n2a[:], q2[:], CLIP * CLIP, -1.0, ALU.min, ALU.add)
+        stt(inv_den[:], shrink[:], 1.0, inv_den[:], ALU.min, ALU.mult)
+        ts1(n2a[:], n2a[:], 0.5, ALU.mult)
+        tt(coef_b[:], coef_b[:], inv_den[:], ALU.mult)
+        tt(coef_mx[:], num_m[:], inv_den[:], ALU.mult)
         nc.vector.reciprocal(out=n2a[:], in_=n2a[:])
-        ts1(n2a[:], n2a[:], -2.0, ALU.mult)
+        b_part = work.tile([P, TILES, D], F32, tag="a", bufs=A_BUFS, name="b_part")
+        p_rows = work.tile([P, TILES, D], BF16, tag="a", bufs=A_BUFS, name="p_rows")
+        p_grouped = grouped_tile("log", LOG_BUFS)
+        p_banks = []
         spread = psum.tile([P, ROWS], F32, tag="s", bufs=2, name="spread")
         for r in range(TILES):
-            c = COL[r]
-            nc.tensor.matmul(out=spread[:, r * P : (r + 1) * P], lhsT=n2a[:, c : c + 1].to_broadcast([P, P]), rhs=ident[:], start=True, stop=True)
+            nc.tensor.matmul(out=spread[:, r * P : (r + 1) * P], lhsT=n2a[:, r : r + 1].to_broadcast([P, P]), rhs=ident[:], start=True, stop=True)
+        for r in range(TILES):
+            nc.scalar.activation(out=b_part[:, r, :], in_=b_bc[:], func=AF.Copy, scale=coef_b[:, r : r + 1])
+            stt(p_rows[:, r, :], mx[r][:], coef_mx[:, r : r + 1], b_part[:, r, :], ALU.mult, ALU.add)
+            trickle(2)
+            if r % 2 == 1:
+                p_banks.append(word_transposes(p_rows, r // 2, "sum"))
+        word_copy("scalar", p_banks[0], p_grouped, 0)
         copy("scalar", neg2alpha[:], spread[:])
-        four_over_t2 = small("four_over_t2", 1)
-        two_over_t = small("two_over_t", 1)
-        tt(four_over_t2[:], t_bc[:], t_bc[:], ALU.mult)
-        nc.vector.reciprocal(out=four_over_t2[:], in_=four_over_t2[:])
-        ts1(four_over_t2[:], four_over_t2[:], 4.0, ALU.mult)
-        nc.vector.tensor_copy(out=two_over_t[:], in_=t_bc[:])
-        nc.vector.reciprocal(out=two_over_t[:], in_=two_over_t[:])
-        ts1(two_over_t[:], two_over_t[:], 2.0, ALU.mult)
+        word_copy("vector", banks[1][1], grouped[1], 1)
+        word_copy("vector", p_banks[1], p_grouped, 1)
+        trickle(2)
+        quantise(p_grouped, p_words[:], p_scales[:])
+        fill(7)
+        if not FB_PSUM:
+            nc.gpsimd.dma_start(out=fb[:], in_=freq_bias.partition_broadcast(P))
+        else:
+            nc.gpsimd.memset(fb[:], 0.0)
+            nc.gpsimd.dma_start(out=fb[0:1, :], in_=freq_bias.unsqueeze(0))
 
         z_tiles = {}
         a_tiles = {}
         log_tiles = {}
-        sums = {}
-        roots_done = [small("roots_done_%d" % g, 1) for g in range(N_GROUPS)]
-        logs_done = [small("logs_done_%d" % g, 1) for g in range(N_GROUPS)]
+        sum_banks = {}
+        bias_banks = {}
 
-        def scalar_squares(u):
-            return u // GROUP == N_GROUPS - 1 and u % 2 == 1
+        def product_tile(u, t):
+            if t == 0:
+                z_tiles[u] = work.tile([P, TILES, ROWS], F32, tag="z", bufs=Z_BUFS, name="z")
+            codes = slice(t * P, (t + 1) * P)
+            s = psum.tile([P, ROWS], F32, tag="s", bufs=2, name="s")
+            mx_pass(s[:], code_words[u][:, codes], code_scales[u][:, codes], p_words[:], p_scales[:])
+            stt(z_tiles[u][:, t, :], s[:], shift[:, u, t : t + 1], neg2alpha[:], ALU.add, ALU.mult)
+
+        def clip(u, first=0, last=TILES):
+            z = z_tiles[u][:, first:last, :]
+            if u in CLIP_G or u in SQUARE_G or u in SQUARE_S:
+                engine = nc.gpsimd if u in CLIP_G else nc.vector
+                for t in range(first, last):
+                    z = z_tiles[u][:, t, :]
+                    engine.tensor_scalar(out=z, in0=z, scalar1=z_max[:, u, t : t + 1], scalar2=1.0, op0=ALU.min, op1=ALU.max)
+            else:
+                ts1(z, z, 1.0, ALU.max)
 
         def product(u):
-            z = work.tile([P, TILES, ROWS], F32, tag="z", bufs=Z_BUFS, name="z")
-            z_tiles[u] = z
-            unclipped = {}
-
-            def clip(t):
-                nc.gpsimd.tensor_scalar(
-                    out=z[:, t, :], in0=unclipped[t][:], scalar1=z_max[:, u, t : t + 1], scalar2=1.0, op0=ALU.min, op1=ALU.max
-                )
-
+            ensure(u)
             for t in range(TILES):
-                codes = slice(t * P, (t + 1) * P)
-                s = psum.tile([P, ROWS], F32, tag="s", bufs=2, name="s")
-                mx_pass(s[:], code_words[u][:, codes], code_scales[u][:, codes], p_words[:], p_scales[:])
-                unclipped[t] = work.tile([P, ROWS], F32, tag="unclipped", bufs=3, name="unclipped")
-                stt(unclipped[t][:], s[:], shift[:, u, t : t + 1], neg2alpha[:], ALU.add, ALU.mult)
-                if t > 0:
-                    clip(t - 1)
-            clip(TILES - 1)
+                product_tile(u, t)
+                trickle()
+                if u in CLIP_G:
+                    clip(u, t, t + 1)
 
         def roots(u):
-            g = u // GROUP
-            if g > 0:
-                nc.scalar.activation(out=beta_gated[:, u, :], in_=beta[:, u, :], func=AF.Identity, bias=logs_done[g - 1][:])
-            else:
-                nc.scalar.copy(out=beta_gated[:, u, :], in_=beta[:, u, :])
-            a = work.tile([P, TILES, ROWS], F32, tag="a", bufs=GROUP, name="a")
+            a = work.tile([P, TILES, ROWS], F32, tag="a", bufs=A_BUFS, name="a")
             a_tiles[u] = a
             z = z_tiles[u]
             for t in range(TILES):
-                scale = beta_gated[:, u, t : t + 1]
+                scale = beta[:, u, t : t + 1]
                 nc.scalar.activation(out=a[:, t, :], in_=z[:, t, :], func=AF.Sqrt, scale=scale, bias=neg_beta[:, u, t : t + 1])
                 nc.scalar.activation(out=z[:, t, :], in_=z[:, t, :], func=AF.Sqrt, scale=scale, bias=one_minus_beta[:, u, t : t + 1])
 
+        def add_roots(u):
+            if u in VECTOR_ADDS:
+                tt(z_tiles[u][:], a_tiles[u][:], z_tiles[u][:], ALU.add)
+
         def turn(u, r):
             bank = psum.tile([P, UNIT], F32, tag="sum", bufs=4, name="bank")
-            sums[(u, r)] = bank
+            sum_banks[(u, r)] = bank
             rows = slice(r * P, (r + 1) * P)
             for t in range(TILES):
                 block = bank[:, t * P : (t + 1) * P]
-                nc.tensor.matmul(out=block, lhsT=a_tiles[u][:, t, rows], rhs=ident[:], start=True, stop=False, is_transpose=True)
-                nc.tensor.matmul(out=block, lhsT=z_tiles[u][:, t, rows], rhs=ident[:], start=False, stop=True, is_transpose=True)
+                if u in VECTOR_ADDS:
+                    nc.tensor.transpose(block, z_tiles[u][:, t, rows], ident[:])
+                else:
+                    nc.tensor.matmul(out=block, lhsT=a_tiles[u][:, t, rows], rhs=ident[:], start=True, stop=False, is_transpose=True)
+                    nc.tensor.matmul(out=block, lhsT=z_tiles[u][:, t, rows], rhs=ident[:], start=False, stop=True, is_transpose=True)
 
         def logarithm(u, r):
             if r == 0:
-                log_tiles[u] = work.tile([P, TILES, UNIT], F32, tag="log", bufs=GROUP, name="log", align_bytes=64)
-            part = log_tiles[u][:, r, :]
-            nc.scalar.activation(out=part, in_=sums[(u, r)][:], func=AF.Ln, bias=roots_done[u // GROUP][:])
-            if scalar_squares(u):
-                nc.scalar.activation(out=part, in_=part, func=AF.Square, scale=two_over_t[:])
+                log_tiles[u] = work.tile([P, TILES, UNIT], F32, tag="log", bufs=LOG_BUFS, name="log", align_bytes=64)
+            nc.scalar.activation(out=log_tiles[u][:, r, :], in_=sum_banks[(u, r)][:], func=AF.Ln)
 
-        def finish(u, values, bias, target):
-            if not scalar_squares(u):
-                stt(values, values, four_over_t2[:], values, ALU.mult, ALU.mult)
-            tt(values, bias, values, ALU.subtract)
-            nc.sync.dma_start(out=target, in_=values)
+        def bias_of(u, pieces):
+            if FB_PSUM:
+                if u not in bias_banks:
+                    bias_banks[u] = psum.tile([P, UNIT], F32, tag="s", bufs=2, name="bias")
+                    nc.tensor.matmul(out=bias_banks[u][:], lhsT=ones[:], rhs=fb[:, u * UNIT : (u + 1) * UNIT], start=True, stop=True)
+                row = bias_banks[u][:]
+            else:
+                row = fb[:, u * UNIT : (u + 1) * UNIT]
+            return row if pieces == 1 else row.unsqueeze(1).to_broadcast([P, pieces, UNIT])
 
-        for u in range(0, PREPARE_AHEAD, 2):
-            prepare_pair(u)
-        for u in range(AHEAD):
-            product(u)
-        for g in range(N_GROUPS):
-            first = g * GROUP
-            for u in range(first, first + GROUP):
-                if u == first + 1:
+        def square(u, first=0, last=TILES):
+            part = log_tiles[u][:, first:last, :]
+            if u in SQUARE_G:
+                nc.gpsimd.tensor_tensor(out=part, in0=part, in1=part, op=ALU.mult)
+            elif u in SQUARE_S:
+                for r in range(first, last):
+                    nc.scalar.activation(out=log_tiles[u][:, r, :], in_=log_tiles[u][:, r, :], func=AF.Square)
+            else:
+                stt(part, part, minus_four_over_t2[:], part, ALU.mult, ALU.mult)
+
+        def finish(u, first=0, last=TILES):
+            n = last - first
+            part = log_tiles[u][:, first, :] if n == 1 else log_tiles[u][:, first:last, :]
+            if u in SQUARE_G or u in SQUARE_S:
+                stt(part, part, minus_four_over_t2[:], bias_of(u, n), ALU.mult, ALU.add)
+            else:
+                stt(part, part, q_min[:], bias_of(u, n), ALU.max, ALU.add)
+            nc.sync.dma_start(out=out_view[u][:, first, :] if n == 1 else out_view[u][:, first:last, :], in_=part)
+
+        reached = [0, 2]
+
+        def advance():
+            u, w = reached
+            if w < N_UNITS:
+                turn_words(w)
+            if u < N_UNITS:
+                product(u)
+            if w < N_UNITS:
+                for i in range(2):
+                    word_copy("vector", banks[w][i], grouped[w], i)
+                    trickle()
+            if u < N_UNITS and u not in CLIP_G:
+                clip(u)
+            if w < N_UNITS:
+                quantise_words(w)
+            while vector_sums and vector_sums[0][0] <= w + 4:
+                sum_vector(*vector_sums.pop(0))
+                trickle()
+            reached[0] = u + 1
+            reached[1] = w + 1
+
+        ensure(0)
+        for t in range(TILES):
+            product_tile(0, t)
+            if t > 0:
+                clip(0, t - 1, t)
+        quantise_words(1)
+        clip(0, 3, 4)
+        reached[0] = 1
+        advance()
+        first = 0
+        pending = []
+        for g in range(len(GROUPS)):
+            last = first + GROUPS[g] - 1
+            final = g == len(GROUPS) - 1
+            for u in range(first, last + 1):
+                roots(u)
+                if u == first + TURN_AT:
                     for r in range(TILES):
                         turn(first, r)
-                if u + AHEAD < N_UNITS:
-                    product(u + AHEAD)
-                roots(u)
-                if u % 2 == 0 and u + PREPARE_AHEAD < N_UNITS:
-                    prepare_pair(u + PREPARE_AHEAD)
-            last = first + GROUP - 1
-            nc.scalar.activation(out=roots_done[g][:], in_=z_tiles[last][:, TILES - 1, 0:1], func=AF.Copy, scale=0.0)
-            for u in range(first, first + GROUP):
-                fb_u = fb[:, u * UNIT : (u + 1) * UNIT]
+                for i in range(ADV_ROOT[g][u - first]):
+                    advance()
+                if u > first:
+                    add_roots(u - 1)
+                fill(ROOT_SUMS[g][u - first])
+                if pending and u - first >= FINISH_FROM:
+                    finish(pending.pop(0))
+            add_roots(last)
+            for u in range(first, last + 1):
                 for r in range(TILES):
                     logarithm(u, r)
                     if u < last:
                         turn(u + 1, r)
-                    elif r == TILES - 1:
-                        nc.scalar.activation(out=logs_done[g][:], in_=log_tiles[u][:, r, 0:1], func=AF.Copy, scale=0.0)
+                    if r < LOG_SUMS[g]:
+                        fill(1)
+                    if u in SQUARE_S or (u in SQUARE_G and u == N_UNITS - 1):
+                        square(u, r, r + 1)
                     if u == N_UNITS - 1:
-                        finish(u, log_tiles[u][:, r, :], fb_u, out_view[u][:, r, :])
+                        if u not in SQUARE_S and u not in SQUARE_G:
+                            square(u, r, r + 1)
+                        finish(u, r, r + 1)
                 if u < N_UNITS - 1:
-                    finish(u, log_tiles[u][:], fb_u.unsqueeze(1).to_broadcast([P, TILES, UNIT]), out_view[u])
+                    if u not in SQUARE_S:
+                        square(u)
+                    pending.append(u)
+                    if len(pending) > (0 if final and u in SQUARE_S else KEEP):
+                        finish(pending.pop(0))
+                for i in range(ADV_LOG[g][u - first]):
+                    advance()
+            first = last + 1
+        while pending:
+            finish(pending.pop(0))

@@ -39,24 +39,27 @@ AHEAD = 4
 TURN_AT = 1
 ADV_ROOT = ((1, 1, 1, 1), (0, 1, 1, 0), (0, 1, 1, 0), (0, 1, 1, 0))
 ADV_LOG = ((0, 0, 1, 1), (0, 0, 1, 1), (0, 0, 1, 1), (0, 0, 0, 0))
-BATCHES = ((0, 1), (1, 2), (2, 3), (3, 4), (4, 5), (5, 6), (6, 8), (8, 12), (12, 14), (14, 16))
-ROOT_SUMS = ((3, 4, 4, 4), (0, 0, 0, 0), (0, 0, 0, 0), (0, 0, 0, 0))
-LOG_SUMS = (3, 3, 4, 0)
+BATCHES = ((0, 1), (1, 2), (2, 3), (3, 4), (4, 5), (5, 6), (6, 8), (8, 10), (10, 12), (12, 14), (14, 16))
+ROOT_SUMS = ((3, 4, 4, 0), (0, 0, 0, 0), (0, 0, 0, 0), (0, 0, 0, 0))
+LOG_SUMS = (2, 2, 2, 0)
 Z_BUFS = max(GROUPS) + AHEAD
 CLIP_G = tuple(range(1, 16))
 SQUARE_G = tuple(range(14))
 SQUARE_S = (14, 15)
 FB_PSUM = True
-SUM_V = ()
+SUM_V = (2, 3)
 VECTOR_ADDS = (2, 6, 10, 13, 14, 15)
+GPSIMD_ADDS = ()
 KEEP = 1
+SQUARE_STEP = 4
+VECTOR_SUMS = ((4, 4, 0, 0), (4, 4, 0, 0), (4, 0, 0, 0), (0, 0, 0, 0))
 FINISH_FROM = 0
 
 
 def tile_hyperbolicdistancedecoder_kernel(tc, v_tangent, code_points, W, b, freq_bias, temperature, out):
     nc = tc.nc
     with ExitStack() as ctx:
-        ctx.enter_context(tc.manual_schedule())
+        ctx.enter_context(tc.manual_schedule(engines={mybir.EngineType.Activation}))
         const = ctx.enter_context(tc.tile_pool(name="const", bufs=1))
         work = ctx.enter_context(tc.tile_pool(name="work", bufs=1))
         psum = ctx.enter_context(tc.psum_pool(name="psum", bufs=1))
@@ -87,6 +90,8 @@ def tile_hyperbolicdistancedecoder_kernel(tc, v_tangent, code_points, W, b, freq
         unread_a = const.tile([P, D], BF16, name="unread_a")
         unread_v = const.tile([P, D], BF16, name="unread_v")
         y2 = per_code("y2")
+        stats = const.tile([P, N_UNITS, TILES, 6], F32, name="stats")
+        moments = per_code("moments")
         shift = per_code("shift")
         gap = per_code("gap")
         beta = per_code("beta")
@@ -105,9 +110,6 @@ def tile_hyperbolicdistancedecoder_kernel(tc, v_tangent, code_points, W, b, freq
 
         def tt(o, i0, i1, op):
             nc.vector.tensor_tensor(out=o, in0=i0, in1=i1, op=op)
-
-        def power(o, i, exponent):
-            nc.gpsimd.tensor_tensor(out=o, in0=i, in1=exponent, op=ALU.pow)
 
         def sum_of_squares_scalar(src, acc):
             nc.scalar.activation(out=unread_a[:], in_=src, func=AF.Square, accum_out=acc)
@@ -174,7 +176,7 @@ def tile_hyperbolicdistancedecoder_kernel(tc, v_tangent, code_points, W, b, freq
             sum_of_squares_scalar(raws[u][:, t, :], y2[:, u, t : t + 1])
 
         def sum_vector(u, t):
-            dot_vector(raws[u][:, t, :], raws[u][:, t, :], y2[:, u, t : t + 1])
+            nc.vector.bn_stats(out=stats[:, u, t, :], in_=raws[u][:, t, :])
 
         waiting = []
 
@@ -187,6 +189,18 @@ def tile_hyperbolicdistancedecoder_kernel(tc, v_tangent, code_points, W, b, freq
             def some(values):
                 return values[:, first:last, :].rearrange("p u t -> p (u t)")
 
+            if SUM_V and first >= 6:
+                lo, hi = SUM_V[0], SUM_V[-1] + 1
+                even, odd = y2[:, first:last, lo:hi], moments[:, first:last, lo:hi]
+
+                def stat(i):
+                    return stats[:, first:last, lo:hi, i]
+
+                waiting.append(lambda: tt(even, stat(1), stat(1), ALU.mult))
+                waiting.append(lambda: tt(odd, stat(4), stat(4), ALU.mult))
+                waiting.append(lambda: stt(even, even, D / 2.0, stat(2), ALU.mult, ALU.add))
+                waiting.append(lambda: stt(odd, odd, D / 2.0, stat(5), ALU.mult, ALU.add))
+                waiting.append(lambda: tt(even, even, odd, ALU.add))
             waiting.append(lambda: ts(some(gap), some(y2), -1.0, 1.0, ALU.mult, ALU.add))
             waiting.append(lambda: ts(some(shift), some(y2), -0.5, -0.5, ALU.mult, ALU.add))
             waiting.append(lambda: ts1(some(gap), some(gap), GAP_MIN, ALU.max))
@@ -225,13 +239,13 @@ def tile_hyperbolicdistancedecoder_kernel(tc, v_tangent, code_points, W, b, freq
         mx2 = small("mx2")
         mx_b = small("mx_b")
         tanh_m = small("tanh_m")
-        half = small("half")
         warm = small("warm", 1)
         nc.vector.memset(warm[:], 0.0)
+        if FB_PSUM:
+            nc.vector.memset(fb[:].bitcast(mybir.dt.int32), 0)
         nc.vector.memset(norm2[:], 1.0)
         nc.vector.memset(mx2[:], 1.0)
         nc.vector.memset(mx_b[:], 0.0)
-        nc.gpsimd.memset(half[:], 0.5)
         raw_v = work.tile([P, TILES, D], BF16, tag="raw", bufs=RAW_BUFS, name="raw_v")
         for r in (0, 2, 1, 3):
             nc.sync.dma_start(out=raw_v[:, r, :], in_=v_view[:, r, :])
@@ -242,7 +256,7 @@ def tile_hyperbolicdistancedecoder_kernel(tc, v_tangent, code_points, W, b, freq
         for i in range(RAW_BUFS - 2):
             load_next_unit()
         make_identity(nc, ident[:])
-        nc.scalar.activation(out=warm[:], in_=warm[:], func=AF.Tanh)
+        nc.scalar.activation(out=warm[:], in_=warm[:], func=AF.Sqrt)
         if FB_PSUM:
             nc.gpsimd.memset(ones[:], 1.0)
 
@@ -258,11 +272,13 @@ def tile_hyperbolicdistancedecoder_kernel(tc, v_tangent, code_points, W, b, freq
         scale_x = small("scale_x")
         w_banks = [word_transposes(raw_w, i, "words") for i in range(2)]
         w_grouped = grouped_tile("log", LOG_BUFS)
-        ts1(norm2_floor[:], norm2[:], TINY * TINY, ALU.max)
-        power(norm[:], norm2_floor[:], half[:])
+        nc.scalar.activation(out=norm2_floor[:], in_=norm2[:], func=AF.Sqrt)
+        nc.scalar.activation(out=tanh_n[:], in_=norm2_floor[:], func=AF.Tanh)
+        ts1(norm[:], norm2_floor[:], TINY, ALU.max)
         word_copy("vector", w_banks[0], w_grouped, 0)
         nc.vector.reciprocal(out=inv_norm[:], in_=norm[:])
-        nc.scalar.activation(out=tanh_n[:], in_=norm[:], func=AF.Tanh)
+        warm_1 = small("warm_1", 1)
+        nc.scalar.activation(out=warm_1[:], in_=tanh_n[:, 0:1], func=AF.Sqrt)
         tt(scale_x[:], tanh_n[:], inv_norm[:], ALU.mult)
         word_copy("scalar", w_banks[1], w_grouped, 1)
         fill(1)
@@ -314,8 +330,8 @@ def tile_hyperbolicdistancedecoder_kernel(tc, v_tangent, code_points, W, b, freq
         mx_norm = small("mx_norm")
         inv_mx_norm = small("inv_mx_norm")
         dot_unit = small("dot_unit")
-        ts1(mx2_floor[:], mx2[:], TINY * TINY, ALU.max)
-        power(mx_norm[:], mx2_floor[:], half[:])
+        nc.scalar.activation(out=mx2_floor[:], in_=mx2[:], func=AF.Sqrt)
+        ts1(mx_norm[:], mx2_floor[:], TINY, ALU.max)
         word_copy("vector", banks[1][0], grouped[1], 0)
         tt(arg[:], mx_norm[:], rho[:], ALU.mult)
         nc.scalar.activation(out=tanh_m[:], in_=arg[:], func=AF.Tanh)
@@ -376,8 +392,7 @@ def tile_hyperbolicdistancedecoder_kernel(tc, v_tangent, code_points, W, b, freq
         if not FB_PSUM:
             nc.gpsimd.dma_start(out=fb[:], in_=freq_bias.partition_broadcast(P))
         else:
-            nc.gpsimd.memset(fb[:], 0.0)
-            nc.gpsimd.dma_start(out=fb[0:1, :], in_=freq_bias.unsqueeze(0))
+            nc.sync.dma_start(out=fb[0:1, :], in_=freq_bias.unsqueeze(0))
 
         z_tiles = {}
         a_tiles = {}
@@ -421,7 +436,9 @@ def tile_hyperbolicdistancedecoder_kernel(tc, v_tangent, code_points, W, b, freq
                 nc.scalar.activation(out=z[:, t, :], in_=z[:, t, :], func=AF.Sqrt, scale=scale, bias=one_minus_beta[:, u, t : t + 1])
 
         def add_roots(u):
-            if u in VECTOR_ADDS:
+            if u in GPSIMD_ADDS:
+                nc.gpsimd.tensor_tensor(out=z_tiles[u][:], in0=a_tiles[u][:], in1=z_tiles[u][:], op=ALU.add)
+            elif u in VECTOR_ADDS:
                 tt(z_tiles[u][:], a_tiles[u][:], z_tiles[u][:], ALU.add)
 
         def turn(u, r):
@@ -454,7 +471,9 @@ def tile_hyperbolicdistancedecoder_kernel(tc, v_tangent, code_points, W, b, freq
         def square(u, first=0, last=TILES):
             part = log_tiles[u][:, first:last, :]
             if u in SQUARE_G:
-                nc.gpsimd.tensor_tensor(out=part, in0=part, in1=part, op=ALU.mult)
+                for r in range(first, last, SQUARE_STEP):
+                    piece = log_tiles[u][:, r : min(r + SQUARE_STEP, last), :]
+                    nc.gpsimd.tensor_tensor(out=piece, in0=piece, in1=piece, op=ALU.mult)
             elif u in SQUARE_S:
                 for r in range(first, last):
                     nc.scalar.activation(out=log_tiles[u][:, r, :], in_=log_tiles[u][:, r, :], func=AF.Square)
@@ -486,9 +505,6 @@ def tile_hyperbolicdistancedecoder_kernel(tc, v_tangent, code_points, W, b, freq
                 clip(u)
             if w < N_UNITS:
                 quantise_words(w)
-            while vector_sums and vector_sums[0][0] <= w + 4:
-                sum_vector(*vector_sums.pop(0))
-                trickle()
             reached[0] = u + 1
             reached[1] = w + 1
 
@@ -520,6 +536,10 @@ def tile_hyperbolicdistancedecoder_kernel(tc, v_tangent, code_points, W, b, freq
                     finish(pending.pop(0))
             add_roots(last)
             for u in range(first, last + 1):
+                for i in range(VECTOR_SUMS[g][u - first]):
+                    if vector_sums:
+                        sum_vector(*vector_sums.pop(0))
+                        trickle()
                 for r in range(TILES):
                     logarithm(u, r)
                     if u < last:
@@ -528,15 +548,17 @@ def tile_hyperbolicdistancedecoder_kernel(tc, v_tangent, code_points, W, b, freq
                         fill(1)
                     if u in SQUARE_S or (u in SQUARE_G and u == N_UNITS - 1):
                         square(u, r, r + 1)
+                    elif u in SQUARE_G and (r + 1) % SQUARE_STEP == 0:
+                        square(u, r + 1 - SQUARE_STEP, r + 1)
                     if u == N_UNITS - 1:
                         if u not in SQUARE_S and u not in SQUARE_G:
                             square(u, r, r + 1)
                         finish(u, r, r + 1)
                 if u < N_UNITS - 1:
-                    if u not in SQUARE_S:
+                    if u not in SQUARE_S and u not in SQUARE_G:
                         square(u)
                     pending.append(u)
-                    if len(pending) > (0 if final and u in SQUARE_S else KEEP):
+                    if len(pending) > (0 if final and u in SQUARE_S else 1 if final else KEEP):
                         finish(pending.pop(0))
                 for i in range(ADV_LOG[g][u - first]):
                     advance()

@@ -54,6 +54,7 @@ KEEP = 1
 SQUARE_STEP = 4
 VECTOR_SUMS = ((4, 4, 0, 0), (4, 4, 0, 0), (4, 0, 0, 0), (0, 0, 0, 0))
 FINISH_FROM = 0
+STAGE_ONE_PINS = {mybir.EngineType.Activation, mybir.EngineType.DVE, mybir.EngineType.PE}
 
 
 def tile_hyperbolicdistancedecoder_kernel(tc, v_tangent, code_points, W, b, freq_bias, temperature, out):
@@ -87,8 +88,6 @@ def tile_hyperbolicdistancedecoder_kernel(tc, v_tangent, code_points, W, b, freq
         w_scales = const.tile([P, D], U8, name="w_scales", align_bytes=64)
         p_words = const.tile([P, ROWS], U32, name="p_words", align_bytes=64)
         p_scales = const.tile([P, ROWS], U8, name="p_scales", align_bytes=64)
-        unread_a = const.tile([P, D], BF16, name="unread_a")
-        unread_v = const.tile([P, D], BF16, name="unread_v")
         y2 = per_code("y2")
         stats = const.tile([P, N_UNITS, TILES, 6], F32, name="stats")
         moments = per_code("moments")
@@ -112,10 +111,12 @@ def tile_hyperbolicdistancedecoder_kernel(tc, v_tangent, code_points, W, b, freq
             nc.vector.tensor_tensor(out=o, in0=i0, in1=i1, op=op)
 
         def sum_of_squares_scalar(src, acc):
-            nc.scalar.activation(out=unread_a[:], in_=src, func=AF.Square, accum_out=acc)
+            unread = work.tile([P, D], BF16, tag="unread_a", bufs=4, name="unread")
+            nc.scalar.activation(out=unread[:], in_=src, func=AF.Square, accum_out=acc)
 
         def dot_vector(src0, src1, acc):
-            nc.vector.scalar_tensor_tensor(out=unread_v[:], in0=src0, scalar=1.0, in1=src1, op0=ALU.mult, op1=ALU.mult, accum_out=acc)
+            unread = work.tile([P, D], BF16, tag="unread_v", bufs=4, name="unread")
+            nc.vector.scalar_tensor_tensor(out=unread[:], in0=src0, scalar=1.0, in1=src1, op0=ALU.mult, op1=ALU.mult, accum_out=acc)
 
         def copy(engine, o, i):
             if engine == "scalar":
@@ -235,164 +236,175 @@ def tile_hyperbolicdistancedecoder_kernel(tc, v_tangent, code_points, W, b, freq
             while ready[-1] <= u:
                 trickle()
 
-        norm2 = small("norm2")
-        mx2 = small("mx2")
-        mx_b = small("mx_b")
-        tanh_m = small("tanh_m")
-        warm = small("warm", 1)
-        nc.vector.memset(warm[:], 0.0)
-        if FB_PSUM:
-            nc.vector.memset(fb[:].bitcast(mybir.dt.int32), 0)
-        nc.vector.memset(norm2[:], 1.0)
-        nc.vector.memset(mx2[:], 1.0)
-        nc.vector.memset(mx_b[:], 0.0)
-        raw_v = work.tile([P, TILES, D], BF16, tag="raw", bufs=RAW_BUFS, name="raw_v")
-        for r in (0, 2, 1, 3):
-            nc.sync.dma_start(out=raw_v[:, r, :], in_=v_view[:, r, :])
-        nc.scalar.dma_start(out=b_bc[:], in_=b.partition_broadcast(P))
-        raw_w = work.tile([P, TILES, D], BF16, tag="raw", bufs=RAW_BUFS, name="raw_w")
-        nc.sync.dma_start(out=raw_w[:], in_=w_view)
-        nc.scalar.dma_start(out=t_bc[:], in_=temperature.partition_broadcast(P))
-        for i in range(RAW_BUFS - 2):
-            load_next_unit()
-        make_identity(nc, ident[:])
-        nc.scalar.activation(out=warm[:], in_=warm[:], func=AF.Sqrt)
-        if FB_PSUM:
-            nc.gpsimd.memset(ones[:], 1.0)
-
-        sum_of_squares_scalar(raw_v[:, 0, :], norm2[:, 0:1])
-        dot_vector(raw_v[:, 2, :], raw_v[:, 2, :], norm2[:, 2:3])
-        sum_of_squares_scalar(raw_v[:, 1, :], norm2[:, 1:2])
-        dot_vector(raw_v[:, 3, :], raw_v[:, 3, :], norm2[:, 3:4])
-        sum_of_squares_scalar(b_bc[:], norm2[:, BCOL : BCOL + 1])
-        norm2_floor = small("norm2_floor")
-        norm = small("norm")
-        inv_norm = small("inv_norm")
-        tanh_n = small("tanh_n")
-        scale_x = small("scale_x")
-        w_banks = [word_transposes(raw_w, i, "words") for i in range(2)]
-        w_grouped = grouped_tile("log", LOG_BUFS)
-        nc.scalar.activation(out=norm2_floor[:], in_=norm2[:], func=AF.Sqrt)
-        nc.scalar.activation(out=tanh_n[:], in_=norm2_floor[:], func=AF.Tanh)
-        ts1(norm[:], norm2_floor[:], TINY, ALU.max)
-        word_copy("vector", w_banks[0], w_grouped, 0)
-        nc.vector.reciprocal(out=inv_norm[:], in_=norm[:])
-        warm_1 = small("warm_1", 1)
-        nc.scalar.activation(out=warm_1[:], in_=tanh_n[:, 0:1], func=AF.Sqrt)
-        tt(scale_x[:], tanh_n[:], inv_norm[:], ALU.mult)
-        word_copy("scalar", w_banks[1], w_grouped, 1)
-        fill(1)
-        x_rows = work.tile([P, TILES, D], BF16, tag="a", bufs=A_BUFS, name="x_rows")
-        for r in range(TILES):
-            ts1(x_rows[:, r, :], raw_v[:, r, :], scale_x[:, r : r + 1], ALU.mult)
-        x_banks = [word_transposes(x_rows, i, "sum") for i in range(2)]
-        turn_words(0)
-        x_grouped = grouped_tile("log", LOG_BUFS)
-        quantise(w_grouped, w_words[:], w_scales[:])
-        word_copy("scalar", x_banks[0], x_grouped, 0)
-        rho = small("rho")
-        inv_x = small("inv_x")
-        bh2 = small("bh2", 1)
-        bh2_plus_1 = small("bh2_plus_1", 1)
-        ts1(inv_x[:], tanh_n[:], TINY, ALU.max)
-        word_copy("vector", x_banks[1], x_grouped, 1)
-        nc.vector.reciprocal(out=inv_x[:], in_=inv_x[:])
-        quantise(x_grouped, x_words[:], x_scales[:])
-        stt(rho[:], norm[:], ATANH_CLIP, inv_x[:], ALU.min, ALU.mult)
-        tt(bh2[:], tanh_n[:, BCOL : BCOL + 1], tanh_n[:, BCOL : BCOL + 1], ALU.mult)
-        ts1(bh2_plus_1[:], bh2[:], 1.0, ALU.add)
         minus_four_over_t2 = small("minus_four_over_t2", 1)
         q_min = small("q_min", 1)
-        tt(minus_four_over_t2[:], t_bc[:], t_bc[:], ALU.mult)
-        nc.vector.reciprocal(out=minus_four_over_t2[:], in_=minus_four_over_t2[:])
-        waiting.append(lambda: ts1(minus_four_over_t2[:], minus_four_over_t2[:], -4.0, ALU.mult))
-        waiting.append(lambda: ts1(q_min[:], minus_four_over_t2[:], ATANH_CLIP * ATANH_CLIP, ALU.mult))
-        fill(1)
-        word_copy("scalar", banks[0][0], grouped[0], 0)
-        word_copy("scalar", banks[0][1], grouped[0], 1)
-        mx = {}
-        for r in range(TILES):
-            rows = slice(r * P, (r + 1) * P)
-            mx[r] = psum.tile([P, D], F32, tag="sum", bufs=4, name="mx")
-            mx_pass(mx[r][:], x_words[:, rows], x_scales[:, rows], w_words[:], w_scales[:])
-            nc.scalar.activation(out=unread_a[:], in_=mx[r][:], func=AF.Square, accum_out=mx2[:, r : r + 1])
-            mx_again = psum.tile([P, D], F32, tag="s", bufs=2, name="mx_again")
-            mx_pass(mx_again[:], x_words[:, rows], x_scales[:, rows], w_words[:], w_scales[:])
-            dot_vector(mx_again[:], b_bc[:], mx_b[:, r : r + 1])
-            trickle()
-        fill(1)
-        turn_words(1)
-        load_next_unit()
-        load_next_unit()
-        scale_b = scale_x[:, BCOL : BCOL + 1]
-        arg = small("arg")
-        mx2_floor = small("mx2_floor")
-        mx_norm = small("mx_norm")
-        inv_mx_norm = small("inv_mx_norm")
-        dot_unit = small("dot_unit")
-        nc.scalar.activation(out=mx2_floor[:], in_=mx2[:], func=AF.Sqrt)
-        ts1(mx_norm[:], mx2_floor[:], TINY, ALU.max)
-        word_copy("vector", banks[1][0], grouped[1], 0)
-        tt(arg[:], mx_norm[:], rho[:], ALU.mult)
-        nc.scalar.activation(out=tanh_m[:], in_=arg[:], func=AF.Tanh)
-        nc.vector.reciprocal(out=inv_mx_norm[:], in_=mx_norm[:])
-        warm_2 = small("warm_2", 1)
-        nc.scalar.activation(out=warm_2[:], in_=tanh_m[:, 0:1], func=AF.Sqrt)
-        stt(dot_unit[:], mx_b[:], scale_b, inv_mx_norm[:], ALU.mult, ALU.mult)
-        quantise_words(0)
-        fill(3)
-        m2 = small("m2")
-        two_mbh = small("two_mbh")
-        m_scale = small("m_scale")
-        inv_den = small("inv_den")
-        q2 = small("q2")
-        shrink = small("shrink")
-        num_m = small("num_m")
-        coef_mx = small("coef_mx")
-        coef_b = small("coef_b")
-        tt(m2[:], tanh_m[:], tanh_m[:], ALU.mult)
-        stt(two_mbh[:], tanh_m[:], 2.0, dot_unit[:], ALU.mult, ALU.mult)
-        tt(m_scale[:], tanh_m[:], inv_mx_norm[:], ALU.mult)
-        stt(inv_den[:], m2[:], bh2[:], two_mbh[:], ALU.mult, ALU.add)
-        stt(q2[:], m2[:], bh2[:], two_mbh[:], ALU.add, ALU.add)
-        ts(inv_den[:], inv_den[:], 1.0, TINY, ALU.add, ALU.max)
-        stt(num_m[:], two_mbh[:], bh2_plus_1[:], m_scale[:], ALU.add, ALU.mult)
-        nc.vector.reciprocal(out=inv_den[:], in_=inv_den[:])
-        ts(coef_b[:], m2[:], -1.0, 1.0, ALU.mult, ALU.add)
-        stt(q2[:], q2[:], 0.0, inv_den[:], ALU.max, ALU.mult)
-        ts1(coef_b[:], coef_b[:], scale_b, ALU.mult)
-        ts(shrink[:], q2[:], -0.5 * CLIP, 1.5 * CLIP, ALU.mult, ALU.add)
-        n2a = small("n2a")
-        ts(n2a[:], q2[:], CLIP * CLIP, -1.0, ALU.min, ALU.add)
-        stt(inv_den[:], shrink[:], 1.0, inv_den[:], ALU.min, ALU.mult)
-        ts1(n2a[:], n2a[:], 0.5, ALU.mult)
-        tt(coef_b[:], coef_b[:], inv_den[:], ALU.mult)
-        tt(coef_mx[:], num_m[:], inv_den[:], ALU.mult)
-        nc.vector.reciprocal(out=n2a[:], in_=n2a[:])
-        b_part = work.tile([P, TILES, D], F32, tag="a", bufs=A_BUFS, name="b_part")
-        p_rows = work.tile([P, TILES, D], BF16, tag="a", bufs=A_BUFS, name="p_rows")
-        p_grouped = grouped_tile("log", LOG_BUFS)
-        p_banks = []
-        spread = psum.tile([P, ROWS], F32, tag="s", bufs=2, name="spread")
-        for r in range(TILES):
-            nc.tensor.matmul(out=spread[:, r * P : (r + 1) * P], lhsT=n2a[:, r : r + 1].to_broadcast([P, P]), rhs=ident[:], start=True, stop=True)
-        for r in range(TILES):
-            nc.scalar.activation(out=b_part[:, r, :], in_=b_bc[:], func=AF.Copy, scale=coef_b[:, r : r + 1])
-            stt(p_rows[:, r, :], mx[r][:], coef_mx[:, r : r + 1], b_part[:, r, :], ALU.mult, ALU.add)
+
+        def stage_one():
+            norm2 = small("norm2")
+            mx2 = small("mx2")
+            mx_b = small("mx_b")
+            tanh_m = small("tanh_m")
+            warm = small("warm", 1)
+            nc.vector.memset(warm[:], 0.0)
+            if FB_PSUM:
+                nc.vector.memset(fb[:].bitcast(mybir.dt.int32), 0)
+            nc.vector.memset(norm2[:], 1.0)
+            nc.vector.memset(mx2[:], 1.0)
+            nc.vector.memset(mx_b[:], 0.0)
+            raw_v = work.tile([P, TILES, D], BF16, tag="raw", bufs=RAW_BUFS, name="raw_v")
+            for r in (0, 2, 1, 3):
+                nc.sync.dma_start(out=raw_v[:, r, :], in_=v_view[:, r, :])
+            nc.scalar.dma_start(out=b_bc[:], in_=b.partition_broadcast(P))
+            raw_w = work.tile([P, TILES, D], BF16, tag="raw", bufs=RAW_BUFS, name="raw_w")
+            nc.sync.dma_start(out=raw_w[:], in_=w_view)
+            nc.scalar.dma_start(out=t_bc[:], in_=temperature.partition_broadcast(P))
+            for i in range(RAW_BUFS - 2):
+                load_next_unit()
+            make_identity(nc, ident[:])
+            nc.scalar.activation(out=warm[:], in_=warm[:], func=AF.Sqrt)
+            if FB_PSUM:
+                nc.gpsimd.memset(ones[:], 1.0)
+
+            sum_of_squares_scalar(raw_v[:, 0, :], norm2[:, 0:1])
+            dot_vector(raw_v[:, 2, :], raw_v[:, 2, :], norm2[:, 2:3])
+            sum_of_squares_scalar(raw_v[:, 1, :], norm2[:, 1:2])
+            dot_vector(raw_v[:, 3, :], raw_v[:, 3, :], norm2[:, 3:4])
+            sum_of_squares_scalar(b_bc[:], norm2[:, BCOL : BCOL + 1])
+            norm2_floor = small("norm2_floor")
+            norm = small("norm")
+            inv_norm = small("inv_norm")
+            tanh_n = small("tanh_n")
+            scale_x = small("scale_x")
+            w_banks = [word_transposes(raw_w, i, "words") for i in range(2)]
+            w_grouped = grouped_tile("log", LOG_BUFS)
+            nc.scalar.activation(out=norm2_floor[:], in_=norm2[:], func=AF.Sqrt)
+            nc.scalar.activation(out=tanh_n[:], in_=norm2_floor[:], func=AF.Tanh)
+            ts1(norm[:], norm2_floor[:], TINY, ALU.max)
+            word_copy("vector", w_banks[0], w_grouped, 0)
+            nc.vector.reciprocal(out=inv_norm[:], in_=norm[:])
+            tt(scale_x[:], tanh_n[:], inv_norm[:], ALU.mult)
+            word_copy("scalar", w_banks[1], w_grouped, 1)
+            fill(1)
+            x_rows = work.tile([P, TILES, D], BF16, tag="a", bufs=A_BUFS, name="x_rows")
+            for r in range(TILES):
+                ts1(x_rows[:, r, :], raw_v[:, r, :], scale_x[:, r : r + 1], ALU.mult)
+            x_banks = [word_transposes(x_rows, i, "sum") for i in range(2)]
+            turn_words(0)
+            x_grouped = grouped_tile("log", LOG_BUFS)
+            quantise(w_grouped, w_words[:], w_scales[:])
+            word_copy("scalar", x_banks[0], x_grouped, 0)
+            warm_1 = small("warm_1", 1)
+            nc.scalar.activation(out=warm_1[:], in_=tanh_n[:, 0:1], func=AF.Sqrt)
+            rho = small("rho")
+            inv_x = small("inv_x")
+            bh2 = small("bh2", 1)
+            bh2_plus_1 = small("bh2_plus_1", 1)
+            ts1(inv_x[:], tanh_n[:], TINY, ALU.max)
+            word_copy("vector", x_banks[1], x_grouped, 1)
+            nc.vector.reciprocal(out=inv_x[:], in_=inv_x[:])
+            quantise(x_grouped, x_words[:], x_scales[:])
+            stt(rho[:], norm[:], ATANH_CLIP, inv_x[:], ALU.min, ALU.mult)
+            tt(bh2[:], tanh_n[:, BCOL : BCOL + 1], tanh_n[:, BCOL : BCOL + 1], ALU.mult)
+            ts1(bh2_plus_1[:], bh2[:], 1.0, ALU.add)
+            tt(minus_four_over_t2[:], t_bc[:], t_bc[:], ALU.mult)
+            nc.vector.reciprocal(out=minus_four_over_t2[:], in_=minus_four_over_t2[:])
+            waiting.append(lambda: ts1(minus_four_over_t2[:], minus_four_over_t2[:], -4.0, ALU.mult))
+            waiting.append(lambda: ts1(q_min[:], minus_four_over_t2[:], ATANH_CLIP * ATANH_CLIP, ALU.mult))
+            fill(1)
+            word_copy("scalar", banks[0][0], grouped[0], 0)
+            word_copy("scalar", banks[0][1], grouped[0], 1)
+            mx = {}
+            for r in range(TILES):
+                rows = slice(r * P, (r + 1) * P)
+                mx[r] = psum.tile([P, D], F32, tag="sum", bufs=4, name="mx")
+                mx_pass(mx[r][:], x_words[:, rows], x_scales[:, rows], w_words[:], w_scales[:])
+                sum_of_squares_scalar(mx[r][:], mx2[:, r : r + 1])
+                mx_again = psum.tile([P, D], F32, tag="s", bufs=2, name="mx_again")
+                mx_pass(mx_again[:], x_words[:, rows], x_scales[:, rows], w_words[:], w_scales[:])
+                dot_vector(mx_again[:], b_bc[:], mx_b[:, r : r + 1])
+                trickle()
+            fill(1)
+            turn_words(1)
+            load_next_unit()
+            load_next_unit()
+            scale_b = scale_x[:, BCOL : BCOL + 1]
+            arg = small("arg")
+            mx2_floor = small("mx2_floor")
+            mx_norm = small("mx_norm")
+            inv_mx_norm = small("inv_mx_norm")
+            dot_unit = small("dot_unit")
+            nc.scalar.activation(out=mx2_floor[:], in_=mx2[:], func=AF.Sqrt)
+            warm_3 = small("warm_3", 1)
+            nc.scalar.activation(out=warm_3[:], in_=mx2_floor[:, 0:1], func=AF.Tanh)
+            ts1(mx_norm[:], mx2_floor[:], TINY, ALU.max)
+            word_copy("vector", banks[1][0], grouped[1], 0)
+            tt(arg[:], mx_norm[:], rho[:], ALU.mult)
+            nc.scalar.activation(out=tanh_m[:], in_=arg[:], func=AF.Tanh)
+            nc.vector.reciprocal(out=inv_mx_norm[:], in_=mx_norm[:])
+            warm_2 = small("warm_2", 1)
+            nc.scalar.activation(out=warm_2[:], in_=tanh_m[:, 0:1], func=AF.Sqrt)
+            stt(dot_unit[:], mx_b[:], scale_b, inv_mx_norm[:], ALU.mult, ALU.mult)
+            quantise_words(0)
+            fill(2)
+            m2 = small("m2")
+            two_mbh = small("two_mbh")
+            m_scale = small("m_scale")
+            inv_den = small("inv_den")
+            q2 = small("q2")
+            shrink = small("shrink")
+            num_m = small("num_m")
+            coef_mx = small("coef_mx")
+            coef_b = small("coef_b")
+            tt(m2[:], tanh_m[:], tanh_m[:], ALU.mult)
+            stt(two_mbh[:], tanh_m[:], 2.0, dot_unit[:], ALU.mult, ALU.mult)
+            tt(m_scale[:], tanh_m[:], inv_mx_norm[:], ALU.mult)
+            stt(inv_den[:], m2[:], bh2[:], two_mbh[:], ALU.mult, ALU.add)
+            stt(q2[:], m2[:], bh2[:], two_mbh[:], ALU.add, ALU.add)
+            ts(inv_den[:], inv_den[:], 1.0, TINY, ALU.add, ALU.max)
+            stt(num_m[:], two_mbh[:], bh2_plus_1[:], m_scale[:], ALU.add, ALU.mult)
+            nc.vector.reciprocal(out=inv_den[:], in_=inv_den[:])
+            ts(coef_b[:], m2[:], -1.0, 1.0, ALU.mult, ALU.add)
+            stt(q2[:], q2[:], 0.0, inv_den[:], ALU.max, ALU.mult)
+            ts1(coef_b[:], coef_b[:], scale_b, ALU.mult)
+            ts(shrink[:], q2[:], -0.5 * CLIP, 1.5 * CLIP, ALU.mult, ALU.add)
+            n2a = small("n2a")
+            ts(n2a[:], q2[:], CLIP * CLIP, -1.0, ALU.min, ALU.add)
+            stt(inv_den[:], shrink[:], 1.0, inv_den[:], ALU.min, ALU.mult)
+            ts1(n2a[:], n2a[:], 0.5, ALU.mult)
+            tt(coef_b[:], coef_b[:], inv_den[:], ALU.mult)
+            tt(coef_mx[:], num_m[:], inv_den[:], ALU.mult)
+            nc.vector.reciprocal(out=n2a[:], in_=n2a[:])
+            b_part = work.tile([P, TILES, D], F32, tag="a", bufs=A_BUFS, name="b_part")
+            p_rows = work.tile([P, TILES, D], BF16, tag="a", bufs=A_BUFS, name="p_rows")
+            p_grouped = grouped_tile("log", LOG_BUFS)
+            p_banks = []
+            spread = psum.tile([P, ROWS], F32, tag="s", bufs=2, name="spread")
+            for r in range(TILES):
+                nc.tensor.matmul(out=spread[:, r * P : (r + 1) * P], lhsT=n2a[:, r : r + 1].to_broadcast([P, P]), rhs=ident[:], start=True, stop=True)
+            for r in range(TILES):
+                nc.scalar.activation(out=b_part[:, r, :], in_=b_bc[:], func=AF.Copy, scale=coef_b[:, r : r + 1])
+                stt(p_rows[:, r, :], mx[r][:], coef_mx[:, r : r + 1], b_part[:, r, :], ALU.mult, ALU.add)
+                trickle(2)
+                if r % 2 == 1:
+                    p_banks.append(word_transposes(p_rows, r // 2, "sum"))
+            word_copy("scalar", p_banks[0], p_grouped, 0)
+            copy("scalar", neg2alpha[:], spread[:])
+            word_copy("vector", banks[1][1], grouped[1], 1)
+            word_copy("vector", p_banks[1], p_grouped, 1)
             trickle(2)
-            if r % 2 == 1:
-                p_banks.append(word_transposes(p_rows, r // 2, "sum"))
-        word_copy("scalar", p_banks[0], p_grouped, 0)
-        copy("scalar", neg2alpha[:], spread[:])
-        word_copy("vector", banks[1][1], grouped[1], 1)
-        word_copy("vector", p_banks[1], p_grouped, 1)
-        trickle(2)
-        quantise(p_grouped, p_words[:], p_scales[:])
-        fill(7)
-        if not FB_PSUM:
-            nc.gpsimd.dma_start(out=fb[:], in_=freq_bias.partition_broadcast(P))
+            quantise(p_grouped, p_words[:], p_scales[:])
+            fill(8)
+            if not FB_PSUM:
+                nc.gpsimd.dma_start(out=fb[:], in_=freq_bias.partition_broadcast(P))
+            else:
+                nc.sync.dma_start(out=fb[0:1, :], in_=freq_bias.unsqueeze(0))
+
+
+        if STAGE_ONE_PINS:
+            with tc.manual_schedule(engines=STAGE_ONE_PINS):
+                stage_one()
         else:
-            nc.sync.dma_start(out=fb[0:1, :], in_=freq_bias.unsqueeze(0))
+            stage_one()
 
         z_tiles = {}
         a_tiles = {}
@@ -431,8 +443,9 @@ def tile_hyperbolicdistancedecoder_kernel(tc, v_tangent, code_points, W, b, freq
             a_tiles[u] = a
             z = z_tiles[u]
             for t in range(TILES):
+                nc.scalar.activation(out=a[:, t, :], in_=z[:, t, :], func=AF.Sqrt, scale=beta[:, u, t : t + 1], bias=neg_beta[:, u, t : t + 1])
+            for t in range(TILES):
                 scale = beta[:, u, t : t + 1]
-                nc.scalar.activation(out=a[:, t, :], in_=z[:, t, :], func=AF.Sqrt, scale=scale, bias=neg_beta[:, u, t : t + 1])
                 nc.scalar.activation(out=z[:, t, :], in_=z[:, t, :], func=AF.Sqrt, scale=scale, bias=one_minus_beta[:, u, t : t + 1])
 
         def add_roots(u):

@@ -31,30 +31,30 @@ GAP_MIN = 1e-8
 COLS = 5
 BCOL = 4
 
-RAW_BUFS = 10
+RAW_BUFS = 8
 WORD_BUFS = 6
 A_BUFS = max(GROUPS)
 LOG_BUFS = 4
 AHEAD = 4
 TURN_AT = 1
-ADV_ROOT = ((1, 1, 1, 1), (0, 1, 1, 0), (0, 1, 1, 0), (0, 1, 1, 0))
-ADV_LOG = ((0, 0, 1, 1), (0, 0, 1, 1), (0, 0, 1, 1), (0, 0, 0, 0))
-BATCHES = ((0, 1), (1, 2), (2, 3), (3, 4), (4, 5), (5, 6), (6, 8), (8, 10), (10, 12), (12, 14), (14, 16))
-ROOT_SUMS = ((3, 4, 4, 0), (0, 0, 0, 0), (0, 0, 0, 0), (0, 0, 0, 0))
-LOG_SUMS = (2, 2, 2, 0)
+ADV_ROOT = ((1, 1, 1, 1), (1, 1, 1, 0), (1, 1, 1, 0), (1, 1, 1, 0))
+ADV_LOG = ((0, 0, 1, 1), (0, 0, 1, 0), (0, 0, 1, 0), (0, 0, 0, 0))
+BATCHES = ((0, 2), (2, 4), (4, 6), (6, 8), (8, 12), (12, 16))
+ROOT_SUMS = ((4, 4, 0, 0), (0, 0, 0, 0), (0, 0, 0, 0), (0, 0, 0, 0))
+LOG_SUMS = (4, 3, 2, 0)
 Z_BUFS = max(GROUPS) + AHEAD
-CLIP_G = tuple(range(1, 16))
-SQUARE_G = tuple(range(14))
+CLIP_G = ()
+SQUARE_G = ()
 SQUARE_S = (14, 15)
-FB_PSUM = True
-SUM_V = (2, 3)
-VECTOR_ADDS = (2, 6, 10, 13, 14, 15)
+SUM_V = (3,)
+VECTOR_ADDS = (11, 13, 14, 15)
 GPSIMD_ADDS = ()
-KEEP = 1
+KEEP = 2
 SQUARE_STEP = 4
-VECTOR_SUMS = ((4, 4, 0, 0), (4, 4, 0, 0), (4, 0, 0, 0), (0, 0, 0, 0))
+VECTOR_SUMS = ((2, 2, 1, 0), (2, 2, 0, 0), (1, 0, 0, 0), (0, 0, 0, 0))
 FINISH_FROM = 0
 STAGE_ONE_PINS = {mybir.EngineType.Activation, mybir.EngineType.DVE, mybir.EngineType.PE}
+PIN_FIRST = True
 
 
 def tile_hyperbolicdistancedecoder_kernel(tc, v_tangent, code_points, W, b, freq_bias, temperature, out):
@@ -80,8 +80,6 @@ def tile_hyperbolicdistancedecoder_kernel(tc, v_tangent, code_points, W, b, freq
         neg2alpha = const.tile([P, ROWS], F32, name="neg2alpha")
         b_bc = const.tile([P, D], BF16, name="b_bc")
         t_bc = const.tile([P, 1], BF16, name="t_bc")
-        fb = const.tile([P, CODES], BF16, name="fb")
-        ones = const.tile([P, P], BF16, name="ones")
         x_words = const.tile([P, ROWS], U32, name="x_words", align_bytes=64)
         x_scales = const.tile([P, ROWS], U8, name="x_scales", align_bytes=64)
         w_words = const.tile([P, D], U32, name="w_words", align_bytes=64)
@@ -190,6 +188,14 @@ def tile_hyperbolicdistancedecoder_kernel(tc, v_tangent, code_points, W, b, freq
             def some(values):
                 return values[:, first:last, :].rearrange("p u t -> p (u t)")
 
+            def on_gpsimd():
+                def affine(out, in_, factor, term):
+                    nc.gpsimd.tensor_scalar(out=some(out), in0=some(in_), scalar1=factor, scalar2=term, op0=ALU.mult, op1=ALU.add)
+
+                affine(z_max, gap, T_MAX, 1.0)
+                affine(neg_beta, beta, -1.0, 0.0)
+                affine(one_minus_beta, beta, -1.0, 1.0)
+
             if SUM_V and first >= 6:
                 lo, hi = SUM_V[0], SUM_V[-1] + 1
                 even, odd = y2[:, first:last, lo:hi], moments[:, first:last, lo:hi]
@@ -205,10 +211,7 @@ def tile_hyperbolicdistancedecoder_kernel(tc, v_tangent, code_points, W, b, freq
             waiting.append(lambda: ts(some(gap), some(y2), -1.0, 1.0, ALU.mult, ALU.add))
             waiting.append(lambda: ts(some(shift), some(y2), -0.5, -0.5, ALU.mult, ALU.add))
             waiting.append(lambda: ts1(some(gap), some(gap), GAP_MIN, ALU.max))
-            waiting.append(lambda: nc.vector.reciprocal(out=some(beta), in_=some(gap)))
-            waiting.append(lambda: ts1(some(neg_beta), some(beta), -1.0, ALU.mult))
-            waiting.append(lambda: ts(some(one_minus_beta), some(beta), -1.0, 1.0, ALU.mult, ALU.add))
-            waiting.append(lambda: (ts(some(z_max), some(gap), T_MAX, 1.0, ALU.mult, ALU.add), ready.append(last)))
+            waiting.append(lambda: (nc.vector.reciprocal(out=some(beta), in_=some(gap)), on_gpsimd(), ready.append(last)))
 
         scaled = [0]
         ready = [0]
@@ -223,6 +226,8 @@ def tile_hyperbolicdistancedecoder_kernel(tc, v_tangent, code_points, W, b, freq
                 sum_scalar(u, t)
                 for first, last in BATCHES:
                     if u == last - 1 and (u + 1 == N_UNITS and not sums_todo or sums_todo and sums_todo[0][0] == last):
+                        while vector_sums and vector_sums[0][0] < last:
+                            sum_vector(*vector_sums.pop(0))
                         code_scalars(first, last)
                         scaled.append(last)
                         while len(loaded) < last + 6:
@@ -246,8 +251,6 @@ def tile_hyperbolicdistancedecoder_kernel(tc, v_tangent, code_points, W, b, freq
             tanh_m = small("tanh_m")
             warm = small("warm", 1)
             nc.vector.memset(warm[:], 0.0)
-            if FB_PSUM:
-                nc.vector.memset(fb[:].bitcast(mybir.dt.int32), 0)
             nc.vector.memset(norm2[:], 1.0)
             nc.vector.memset(mx2[:], 1.0)
             nc.vector.memset(mx_b[:], 0.0)
@@ -262,8 +265,6 @@ def tile_hyperbolicdistancedecoder_kernel(tc, v_tangent, code_points, W, b, freq
                 load_next_unit()
             make_identity(nc, ident[:])
             nc.scalar.activation(out=warm[:], in_=warm[:], func=AF.Sqrt)
-            if FB_PSUM:
-                nc.gpsimd.memset(ones[:], 1.0)
 
             sum_of_squares_scalar(raw_v[:, 0, :], norm2[:, 0:1])
             dot_vector(raw_v[:, 2, :], raw_v[:, 2, :], norm2[:, 2:3])
@@ -345,7 +346,7 @@ def tile_hyperbolicdistancedecoder_kernel(tc, v_tangent, code_points, W, b, freq
             nc.scalar.activation(out=warm_2[:], in_=tanh_m[:, 0:1], func=AF.Sqrt)
             stt(dot_unit[:], mx_b[:], scale_b, inv_mx_norm[:], ALU.mult, ALU.mult)
             quantise_words(0)
-            fill(2)
+            fill(1)
             m2 = small("m2")
             two_mbh = small("two_mbh")
             m_scale = small("m_scale")
@@ -374,7 +375,7 @@ def tile_hyperbolicdistancedecoder_kernel(tc, v_tangent, code_points, W, b, freq
             tt(coef_b[:], coef_b[:], inv_den[:], ALU.mult)
             tt(coef_mx[:], num_m[:], inv_den[:], ALU.mult)
             nc.vector.reciprocal(out=n2a[:], in_=n2a[:])
-            b_part = work.tile([P, TILES, D], F32, tag="a", bufs=A_BUFS, name="b_part")
+            b_part = work.tile([P, TILES, D], F32, tag="b_part", bufs=1, name="b_part")
             p_rows = work.tile([P, TILES, D], BF16, tag="a", bufs=A_BUFS, name="p_rows")
             p_grouped = grouped_tile("log", LOG_BUFS)
             p_banks = []
@@ -393,24 +394,13 @@ def tile_hyperbolicdistancedecoder_kernel(tc, v_tangent, code_points, W, b, freq
             word_copy("vector", p_banks[1], p_grouped, 1)
             trickle(2)
             quantise(p_grouped, p_words[:], p_scales[:])
-            fill(8)
-            if not FB_PSUM:
-                nc.gpsimd.dma_start(out=fb[:], in_=freq_bias.partition_broadcast(P))
-            else:
-                nc.sync.dma_start(out=fb[0:1, :], in_=freq_bias.unsqueeze(0))
+            fill(3)
 
-
-        if STAGE_ONE_PINS:
-            with tc.manual_schedule(engines=STAGE_ONE_PINS):
-                stage_one()
-        else:
-            stage_one()
 
         z_tiles = {}
         a_tiles = {}
         log_tiles = {}
         sum_banks = {}
-        bias_banks = {}
 
         def product_tile(u, t):
             if t == 0:
@@ -471,14 +461,17 @@ def tile_hyperbolicdistancedecoder_kernel(tc, v_tangent, code_points, W, b, freq
                 log_tiles[u] = work.tile([P, TILES, UNIT], F32, tag="log", bufs=LOG_BUFS, name="log", align_bytes=64)
             nc.scalar.activation(out=log_tiles[u][:, r, :], in_=sum_banks[(u, r)][:], func=AF.Ln)
 
+        lagging = []
+
+        def scalar_square(u, r):
+            square(u, r, r + 1)
+            if u == N_UNITS - 1:
+                finish(u, r, r + 1)
+            elif r == TILES - 1:
+                finish(u)
+
         def bias_of(u, pieces):
-            if FB_PSUM:
-                if u not in bias_banks:
-                    bias_banks[u] = psum.tile([P, UNIT], F32, tag="s", bufs=2, name="bias")
-                    nc.tensor.matmul(out=bias_banks[u][:], lhsT=ones[:], rhs=fb[:, u * UNIT : (u + 1) * UNIT], start=True, stop=True)
-                row = bias_banks[u][:]
-            else:
-                row = fb[:, u * UNIT : (u + 1) * UNIT]
+            row = fb[:, u * UNIT : (u + 1) * UNIT]
             return row if pieces == 1 else row.unsqueeze(1).to_broadcast([P, pieces, UNIT])
 
         def square(u, first=0, last=TILES):
@@ -521,20 +514,32 @@ def tile_hyperbolicdistancedecoder_kernel(tc, v_tangent, code_points, W, b, freq
             reached[0] = u + 1
             reached[1] = w + 1
 
-        ensure(0)
-        for t in range(TILES):
-            product_tile(0, t)
-            if t > 0:
-                clip(0, t - 1, t)
-        quantise_words(1)
-        clip(0, 3, 4)
-        reached[0] = 1
+        def first_unit():
+            ensure(0)
+            for t in range(TILES):
+                product_tile(0, t)
+                if t > 0:
+                    clip(0, t - 1, t)
+            quantise_words(1)
+            clip(0, 3, 4)
+            reached[0] = 1
+
+        if STAGE_ONE_PINS:
+            with tc.manual_schedule(engines=STAGE_ONE_PINS):
+                stage_one()
+                if PIN_FIRST:
+                    first_unit()
+        else:
+            stage_one()
+        if not PIN_FIRST:
+            first_unit()
         advance()
+        fb = work.tile([P, CODES], BF16, tag="b_part", bufs=1, name="fb")
+        nc.gpsimd.dma_start(out=fb[:], in_=freq_bias.partition_broadcast(P))
         first = 0
         pending = []
         for g in range(len(GROUPS)):
             last = first + GROUPS[g] - 1
-            final = g == len(GROUPS) - 1
             for u in range(first, last + 1):
                 roots(u)
                 if u == first + TURN_AT:
@@ -559,19 +564,19 @@ def tile_hyperbolicdistancedecoder_kernel(tc, v_tangent, code_points, W, b, freq
                         turn(u + 1, r)
                     if r < LOG_SUMS[g]:
                         fill(1)
-                    if u in SQUARE_S or (u in SQUARE_G and u == N_UNITS - 1):
-                        square(u, r, r + 1)
+                    if u in SQUARE_S:
+                        lagging.append((u, r))
+                        if len(lagging) > 1:
+                            scalar_square(*lagging.pop(0))
+                        if u == last and r == TILES - 1:
+                            scalar_square(*lagging.pop(0))
                     elif u in SQUARE_G and (r + 1) % SQUARE_STEP == 0:
                         square(u, r + 1 - SQUARE_STEP, r + 1)
-                    if u == N_UNITS - 1:
-                        if u not in SQUARE_S and u not in SQUARE_G:
-                            square(u, r, r + 1)
-                        finish(u, r, r + 1)
-                if u < N_UNITS - 1:
-                    if u not in SQUARE_S and u not in SQUARE_G:
+                if u not in SQUARE_S:
+                    if u not in SQUARE_G:
                         square(u)
                     pending.append(u)
-                    if len(pending) > (0 if final and u in SQUARE_S else 1 if final else KEEP):
+                    if len(pending) > KEEP:
                         finish(pending.pop(0))
                 for i in range(ADV_LOG[g][u - first]):
                     advance()

from contextlib import ExitStack
import math

import concourse.mybir as mybir
from concourse.masks import make_identity

F32 = mybir.dt.float32
BF16 = mybir.dt.bfloat16
U32 = mybir.dt.uint32
U8 = mybir.dt.uint8
FP8X4 = mybir.dt.float8_e4m3fn_x4
ALU = mybir.AluOpType
AF = mybir.ActivationFunctionType

P = 128
D = 512
ROWS = 512
CODES = 8192
TILES = 4
UNIT = TILES * P
N_UNITS = CODES // UNIT
GROUPS = (4, 4, 4, 4)
FLOPS = 2 * ROWS * D * D + 2 * ROWS * CODES * D

CLIP = 1.0 - 1e-5
ATANH_CLIP = 0.5 * math.log((1.0 + CLIP) / (1.0 - CLIP))
T_MAX = CLIP * CLIP / (1.0 - CLIP * CLIP)
TINY = 1e-15
GAP_MIN = 1e-8

COLS = 5
BCOL = 4

RAW_BUFS = 8
WORD_BUFS = 6
A_BUFS = max(GROUPS)
LOG_BUFS = 4
AHEAD = 4
TURN_AT = 1
ADV_ROOT = ((1, 1, 1, 1), (1, 1, 1, 0), (1, 1, 1, 0), (1, 1, 1, 0))
ADV_LOG = ((0, 0, 1, 1), (0, 0, 1, 0), (0, 0, 1, 0), (0, 0, 0, 0))
BATCHES = ((0, 2), (2, 4), (4, 6), (6, 8), (8, 12), (12, 16))
ROOT_SUMS = ((4, 4, 0, 0), (0, 0, 0, 0), (0, 0, 0, 0), (0, 0, 0, 0))
LOG_SUMS = (4, 3, 2, 0)
Z_BUFS = max(GROUPS) + AHEAD
CLIP_G = ()
SQUARE_G = ()
SQUARE_S = (14, 15)
SUM_V = (3,)
VECTOR_ADDS = (11, 13, 14, 15)
GPSIMD_ADDS = ()
KEEP = 2
SQUARE_STEP = 4
VECTOR_SUMS = ((2, 2, 1, 0), (2, 2, 0, 0), (1, 0, 0, 0), (0, 0, 0, 0))
FINISH_FROM = 0
STAGE_ONE_PINS = {mybir.EngineType.Activation, mybir.EngineType.DVE, mybir.EngineType.PE}
PIN_FIRST = True


def tile_hyperbolicdistancedecoder_kernel(tc, v_tangent, code_points, W, b, freq_bias, temperature, out):
    nc = tc.nc
    with ExitStack() as ctx:
        ctx.enter_context(tc.manual_schedule(engines={mybir.EngineType.Activation}))
        const = ctx.enter_context(tc.tile_pool(name="const", bufs=1))
        work = ctx.enter_context(tc.tile_pool(name="work", bufs=1))
        psum = ctx.enter_context(tc.psum_pool(name="psum", bufs=1))

        v_view = v_tangent.flatten_outer_dims().rearrange("(r p) d -> p r d", p=P)
        w_view = W.rearrange("(t p) d -> p t d", p=P)
        code_view = code_points.rearrange("(u t p) d -> u p t d", t=TILES, p=P)
        out_view = out.flatten_outer_dims().rearrange("(r p) (u n) -> u p r n", p=P, n=UNIT)

        def small(name, cols=COLS):
            return const.tile([P, cols], F32, name=name)

        def per_code(name):
            return const.tile([P, N_UNITS, TILES], F32, name=name)

        ident = const.tile([P, P], F32, name="ident")
        neg2alpha = const.tile([P, ROWS], F32, name="neg2alpha")
        b_bc = const.tile([P, D], BF16, name="b_bc")
        t_bc = const.tile([P, 1], BF16, name="t_bc")
        x_words = const.tile([P, ROWS], U32, name="x_words", align_bytes=64)
        x_scales = const.tile([P, ROWS], U8, name="x_scales", align_bytes=64)
        w_words = const.tile([P, D], U32, name="w_words", align_bytes=64)
        w_scales = const.tile([P, D], U8, name="w_scales", align_bytes=64)
        p_words = const.tile([P, ROWS], U32, name="p_words", align_bytes=64)
        p_scales = const.tile([P, ROWS], U8, name="p_scales", align_bytes=64)
        y2 = per_code("y2")
        stats = const.tile([P, N_UNITS, TILES, 6], F32, name="stats")
        moments = per_code("moments")
        shift = per_code("shift")
        gap = per_code("gap")
        beta = per_code("beta")
        neg_beta = per_code("neg_beta")
        one_minus_beta = per_code("one_minus_beta")
        z_max = per_code("z_max")

        def ts(o, i, s1, s2, op0, op1):
            nc.vector.tensor_scalar(out=o, in0=i, scalar1=s1, scalar2=s2, op0=op0, op1=op1)

        def ts1(o, i, s1, op0):
            nc.vector.tensor_scalar(out=o, in0=i, scalar1=s1, scalar2=None, op0=op0)

        def stt(o, i0, s, i1, op0, op1):
            nc.vector.scalar_tensor_tensor(out=o, in0=i0, scalar=s, in1=i1, op0=op0, op1=op1)

        def tt(o, i0, i1, op):
            nc.vector.tensor_tensor(out=o, in0=i0, in1=i1, op=op)

        def sum_of_squares_scalar(src, acc):
            unread = work.tile([P, D], BF16, tag="unread_a", bufs=4, name="unread")
            nc.scalar.activation(out=unread[:], in_=src, func=AF.Square, accum_out=acc)

        def dot_vector(src0, src1, acc):
            unread = work.tile([P, D], BF16, tag="unread_v", bufs=4, name="unread")
            nc.vector.scalar_tensor_tensor(out=unread[:], in0=src0, scalar=1.0, in1=src1, op0=ALU.mult, op1=ALU.mult, accum_out=acc)

        def copy(engine, o, i):
            if engine == "scalar":
                nc.scalar.copy(out=o, in_=i)
            else:
                nc.vector.tensor_copy(out=o, in_=i)

        def mx_pass(o, lhs_words, lhs_scales, rhs_words, rhs_scales):
            nc.tensor.matmul_mx(
                out=o, lhsT=lhs_words.bitcast(FP8X4), lhsT_scale=lhs_scales, rhs=rhs_words.bitcast(FP8X4), rhs_scale=rhs_scales,
                start=True, stop=True,
            )

        def quantise(grouped, words, scales):
            nc.vector.quantize_mx(out=words.bitcast(FP8X4), scales=scales, in_=grouped[:])

        def word_transposes(raw, half, tag):
            bank = psum.tile([P, 2, 2, P], F32, tag=tag, bufs=4 if tag == "sum" else 2, name="bank")
            raw_words = raw[:].rearrange("p t d -> p (t d)").bitcast(F32)
            for i in range(2):
                for h in range(2):
                    start = (2 * half + i) * (D // 2) + h * P
                    nc.tensor.transpose(bank[:, i, h, :], raw_words[:, start : start + P], ident[:])
            return bank

        def word_copy(engine, bank, grouped, half):
            dst = grouped[:].bitcast(F32).rearrange("p (c h) -> p c h", h=2)[:, half * 2 * P : (half + 1) * 2 * P, :]
            copy(engine, dst.rearrange("p (i c) h -> p i c h", i=2), bank[:].rearrange("p i h c -> p i c h"))

        def grouped_tile(tag, bufs):
            return work.tile([P, 4 * ROWS], BF16, tag=tag, bufs=bufs, name="grouped", align_bytes=64)

        raws = {}
        code_words = {}
        code_scales = {}
        banks = {}
        grouped = {}
        loaded = []

        def load_next_unit():
            u = len(loaded)
            if u < N_UNITS:
                raw = work.tile([P, TILES, D], BF16, tag="raw", bufs=RAW_BUFS, name="raw")
                nc.sync.dma_start(out=raw[:], in_=code_view[u])
                raws[u] = raw
                loaded.append(u)

        def turn_words(u):
            banks[u] = [word_transposes(raws[u], half, "words") for half in range(2)]
            grouped[u] = grouped_tile("grouped", 2)

        def quantise_words(u):
            code_words[u] = work.tile([P, UNIT], U32, tag="code_words", bufs=WORD_BUFS, name="words", align_bytes=64)
            code_scales[u] = work.tile([P, UNIT], U8, tag="code_scales", bufs=WORD_BUFS, name="scales", align_bytes=64)
            quantise(grouped[u], code_words[u][:], code_scales[u][:])

        def sum_scalar(u, t):
            sum_of_squares_scalar(raws[u][:, t, :], y2[:, u, t : t + 1])

        def sum_vector(u, t):
            nc.vector.bn_stats(out=stats[:, u, t, :], in_=raws[u][:, t, :])

        waiting = []

        def trickle(count=1):
            for i in range(count):
                if waiting:
                    waiting.pop(0)()

        def code_scalars(first, last):
            def some(values):
                return values[:, first:last, :].rearrange("p u t -> p (u t)")

            def on_gpsimd():
                def affine(out, in_, factor, term):
                    nc.gpsimd.tensor_scalar(out=some(out), in0=some(in_), scalar1=factor, scalar2=term, op0=ALU.mult, op1=ALU.add)

                affine(z_max, gap, T_MAX, 1.0)
                affine(neg_beta, beta, -1.0, 0.0)
                affine(one_minus_beta, beta, -1.0, 1.0)

            if SUM_V and first >= 6:
                lo, hi = SUM_V[0], SUM_V[-1] + 1
                even, odd = y2[:, first:last, lo:hi], moments[:, first:last, lo:hi]

                def stat(i):
                    return stats[:, first:last, lo:hi, i]

                waiting.append(lambda: tt(even, stat(1), stat(1), ALU.mult))
                waiting.append(lambda: tt(odd, stat(4), stat(4), ALU.mult))
                waiting.append(lambda: stt(even, even, D / 2.0, stat(2), ALU.mult, ALU.add))
                waiting.append(lambda: stt(odd, odd, D / 2.0, stat(5), ALU.mult, ALU.add))
                waiting.append(lambda: tt(even, even, odd, ALU.add))
            waiting.append(lambda: ts(some(gap), some(y2), -1.0, 1.0, ALU.mult, ALU.add))
            waiting.append(lambda: ts(some(shift), some(y2), -0.5, -0.5, ALU.mult, ALU.add))
            waiting.append(lambda: ts1(some(gap), some(gap), GAP_MIN, ALU.max))
            waiting.append(lambda: (nc.vector.reciprocal(out=some(beta), in_=some(gap)), on_gpsimd(), ready.append(last)))

        scaled = [0]
        ready = [0]
        vector_sums = [(u, t) for u in range(6, N_UNITS) for t in SUM_V]
        sums_todo = [(u, t) for u in range(N_UNITS) for t in range(TILES) if (u, t) not in vector_sums]

        def fill(count):
            for i in range(count):
                if not sums_todo:
                    break
                u, t = sums_todo.pop(0)
                sum_scalar(u, t)
                for first, last in BATCHES:
                    if u == last - 1 and (u + 1 == N_UNITS and not sums_todo or sums_todo and sums_todo[0][0] == last):
                        while vector_sums and vector_sums[0][0] < last:
                            sum_vector(*vector_sums.pop(0))
                        code_scalars(first, last)
                        scaled.append(last)
                        while len(loaded) < last + 6:
                            if len(loaded) == N_UNITS:
                                break
                            load_next_unit()

        def ensure(u):
            while scaled[-1] <= u:
                fill(1)
            while ready[-1] <= u:
                trickle()

        minus_four_over_t2 = small("minus_four_over_t2", 1)
        q_min = small("q_min", 1)

        def stage_one():
            norm2 = small("norm2")
            mx2 = small("mx2")
            mx_b = small("mx_b")
            tanh_m = small("tanh_m")
            warm = small("warm", 1)
            nc.vector.memset(warm[:], 0.0)
            nc.vector.memset(norm2[:], 1.0)
            nc.vector.memset(mx2[:], 1.0)
            nc.vector.memset(mx_b[:], 0.0)
            raw_v = work.tile([P, TILES, D], BF16, tag="raw", bufs=RAW_BUFS, name="raw_v")
            for r in (0, 2, 1, 3):
                nc.sync.dma_start(out=raw_v[:, r, :], in_=v_view[:, r, :])
            nc.scalar.dma_start(out=b_bc[:], in_=b.partition_broadcast(P))
            raw_w = work.tile([P, TILES, D], BF16, tag="raw", bufs=RAW_BUFS, name="raw_w")
            nc.sync.dma_start(out=raw_w[:], in_=w_view)
            nc.scalar.dma_start(out=t_bc[:], in_=temperature.partition_broadcast(P))
            for i in range(RAW_BUFS - 2):
                load_next_unit()
            make_identity(nc, ident[:])
            nc.scalar.activation(out=warm[:], in_=warm[:], func=AF.Sqrt)

            sum_of_squares_scalar(raw_v[:, 0, :], norm2[:, 0:1])
            dot_vector(raw_v[:, 2, :], raw_v[:, 2, :], norm2[:, 2:3])
            sum_of_squares_scalar(raw_v[:, 1, :], norm2[:, 1:2])
            dot_vector(raw_v[:, 3, :], raw_v[:, 3, :], norm2[:, 3:4])
            sum_of_squares_scalar(b_bc[:], norm2[:, BCOL : BCOL + 1])
            norm2_floor = small("norm2_floor")
            norm = small("norm")
            inv_norm = small("inv_norm")
            tanh_n = small("tanh_n")
            scale_x = small("scale_x")
            w_banks = [word_transposes(raw_w, i, "words") for i in range(2)]
            w_grouped = grouped_tile("log", LOG_BUFS)
            nc.scalar.activation(out=norm2_floor[:], in_=norm2[:], func=AF.Sqrt)
            nc.scalar.activation(out=tanh_n[:], in_=norm2_floor[:], func=AF.Tanh)
            ts1(norm[:], norm2_floor[:], TINY, ALU.max)
            word_copy("vector", w_banks[0], w_grouped, 0)
            nc.vector.reciprocal(out=inv_norm[:], in_=norm[:])
            tt(scale_x[:], tanh_n[:], inv_norm[:], ALU.mult)
            word_copy("scalar", w_banks[1], w_grouped, 1)
            fill(1)
            x_rows = work.tile([P, TILES, D], BF16, tag="a", bufs=A_BUFS, name="x_rows")
            for r in range(TILES):
                ts1(x_rows[:, r, :], raw_v[:, r, :], scale_x[:, r : r + 1], ALU.mult)
            x_banks = [word_transposes(x_rows, i, "sum") for i in range(2)]
            turn_words(0)
            x_grouped = grouped_tile("log", LOG_BUFS)
            quantise(w_grouped, w_words[:], w_scales[:])
            word_copy("scalar", x_banks[0], x_grouped, 0)
            warm_1 = small("warm_1", 1)
            nc.scalar.activation(out=warm_1[:], in_=tanh_n[:, 0:1], func=AF.Sqrt)
            rho = small("rho")
            inv_x = small("inv_x")
            bh2 = small("bh2", 1)
            bh2_plus_1 = small("bh2_plus_1", 1)
            ts1(inv_x[:], tanh_n[:], TINY, ALU.max)
            word_copy("vector", x_banks[1], x_grouped, 1)
            nc.vector.reciprocal(out=inv_x[:], in_=inv_x[:])
            quantise(x_grouped, x_words[:], x_scales[:])
            stt(rho[:], norm[:], ATANH_CLIP, inv_x[:], ALU.min, ALU.mult)
            tt(bh2[:], tanh_n[:, BCOL : BCOL + 1], tanh_n[:, BCOL : BCOL + 1], ALU.mult)
            ts1(bh2_plus_1[:], bh2[:], 1.0, ALU.add)
            tt(minus_four_over_t2[:], t_bc[:], t_bc[:], ALU.mult)
            nc.vector.reciprocal(out=minus_four_over_t2[:], in_=minus_four_over_t2[:])
            waiting.append(lambda: ts1(minus_four_over_t2[:], minus_four_over_t2[:], -4.0, ALU.mult))
            waiting.append(lambda: ts1(q_min[:], minus_four_over_t2[:], ATANH_CLIP * ATANH_CLIP, ALU.mult))
            fill(1)
            word_copy("scalar", banks[0][0], grouped[0], 0)
            word_copy("scalar", banks[0][1], grouped[0], 1)
            mx = {}
            for r in range(TILES):
                rows = slice(r * P, (r + 1) * P)
                mx[r] = psum.tile([P, D], F32, tag="sum", bufs=4, name="mx")
                mx_pass(mx[r][:], x_words[:, rows], x_scales[:, rows], w_words[:], w_scales[:])
                sum_of_squares_scalar(mx[r][:], mx2[:, r : r + 1])
                mx_again = psum.tile([P, D], F32, tag="s", bufs=2, name="mx_again")
                mx_pass(mx_again[:], x_words[:, rows], x_scales[:, rows], w_words[:], w_scales[:])
                dot_vector(mx_again[:], b_bc[:], mx_b[:, r : r + 1])
                trickle()
            fill(1)
            turn_words(1)
            load_next_unit()
            load_next_unit()
            scale_b = scale_x[:, BCOL : BCOL + 1]
            arg = small("arg")
            mx2_floor = small("mx2_floor")
            mx_norm = small("mx_norm")
            inv_mx_norm = small("inv_mx_norm")
            dot_unit = small("dot_unit")
            nc.scalar.activation(out=mx2_floor[:], in_=mx2[:], func=AF.Sqrt)
            warm_3 = small("warm_3", 1)
            nc.scalar.activation(out=warm_3[:], in_=mx2_floor[:, 0:1], func=AF.Tanh)
            ts1(mx_norm[:], mx2_floor[:], TINY, ALU.max)
            word_copy("vector", banks[1][0], grouped[1], 0)
            tt(arg[:], mx_norm[:], rho[:], ALU.mult)
            nc.scalar.activation(out=tanh_m[:], in_=arg[:], func=AF.Tanh)
            nc.vector.reciprocal(out=inv_mx_norm[:], in_=mx_norm[:])
            warm_2 = small("warm_2", 1)
            nc.scalar.activation(out=warm_2[:], in_=tanh_m[:, 0:1], func=AF.Sqrt)
            stt(dot_unit[:], mx_b[:], scale_b, inv_mx_norm[:], ALU.mult, ALU.mult)
            quantise_words(0)
            fill(1)
            m2 = small("m2")
            two_mbh = small("two_mbh")
            m_scale = small("m_scale")
            inv_den = small("inv_den")
            q2 = small("q2")
            shrink = small("shrink")
            num_m = small("num_m")
            coef_mx = small("coef_mx")
            coef_b = small("coef_b")
            tt(m2[:], tanh_m[:], tanh_m[:], ALU.mult)
            stt(two_mbh[:], tanh_m[:], 2.0, dot_unit[:], ALU.mult, ALU.mult)
            tt(m_scale[:], tanh_m[:], inv_mx_norm[:], ALU.mult)
            stt(inv_den[:], m2[:], bh2[:], two_mbh[:], ALU.mult, ALU.add)
            stt(q2[:], m2[:], bh2[:], two_mbh[:], ALU.add, ALU.add)
            ts(inv_den[:], inv_den[:], 1.0, TINY, ALU.add, ALU.max)
            stt(num_m[:], two_mbh[:], bh2_plus_1[:], m_scale[:], ALU.add, ALU.mult)
            nc.vector.reciprocal(out=inv_den[:], in_=inv_den[:])
            ts(coef_b[:], m2[:], -1.0, 1.0, ALU.mult, ALU.add)
            stt(q2[:], q2[:], 0.0, inv_den[:], ALU.max, ALU.mult)
            ts1(coef_b[:], coef_b[:], scale_b, ALU.mult)
            ts(shrink[:], q2[:], -0.5 * CLIP, 1.5 * CLIP, ALU.mult, ALU.add)
            n2a = small("n2a")
            ts(n2a[:], q2[:], CLIP * CLIP, -1.0, ALU.min, ALU.add)
            stt(inv_den[:], shrink[:], 1.0, inv_den[:], ALU.min, ALU.mult)
            ts1(n2a[:], n2a[:], 0.5, ALU.mult)
            tt(coef_b[:], coef_b[:], inv_den[:], ALU.mult)
            tt(coef_mx[:], num_m[:], inv_den[:], ALU.mult)
            nc.vector.reciprocal(out=n2a[:], in_=n2a[:])
            b_part = work.tile([P, TILES, D], F32, tag="b_part", bufs=1, name="b_part")
            p_rows = work.tile([P, TILES, D], BF16, tag="a", bufs=A_BUFS, name="p_rows")
            p_grouped = grouped_tile("log", LOG_BUFS)
            p_banks = []
            spread = psum.tile([P, ROWS], F32, tag="s", bufs=2, name="spread")
            for r in range(TILES):
                nc.tensor.matmul(out=spread[:, r * P : (r + 1) * P], lhsT=n2a[:, r : r + 1].to_broadcast([P, P]), rhs=ident[:], start=True, stop=True)
            for r in range(TILES):
                nc.scalar.activation(out=b_part[:, r, :], in_=b_bc[:], func=AF.Copy, scale=coef_b[:, r : r + 1])
                stt(p_rows[:, r, :], mx[r][:], coef_mx[:, r : r + 1], b_part[:, r, :], ALU.mult, ALU.add)
                trickle(2)
                if r % 2 == 1:
                    p_banks.append(word_transposes(p_rows, r // 2, "sum"))
            word_copy("scalar", p_banks[0], p_grouped, 0)
            copy("scalar", neg2alpha[:], spread[:])
            word_copy("vector", banks[1][1], grouped[1], 1)
            word_copy("vector", p_banks[1], p_grouped, 1)
            trickle(2)
            quantise(p_grouped, p_words[:], p_scales[:])
            fill(3)


        z_tiles = {}
        a_tiles = {}
        log_tiles = {}
        sum_banks = {}

        def product_tile(u, t):
            if t == 0:
                z_tiles[u] = work.tile([P, TILES, ROWS], F32, tag="z", bufs=Z_BUFS, name="z")
            codes = slice(t * P, (t + 1) * P)
            s = psum.tile([P, ROWS], F32, tag="s", bufs=2, name="s")
            mx_pass(s[:], code_words[u][:, codes], code_scales[u][:, codes], p_words[:], p_scales[:])
            stt(z_tiles[u][:, t, :], s[:], shift[:, u, t : t + 1], neg2alpha[:], ALU.add, ALU.mult)

        def clip(u, first=0, last=TILES):
            z = z_tiles[u][:, first:last, :]
            if u in CLIP_G or u in SQUARE_G or u in SQUARE_S:
                engine = nc.gpsimd if u in CLIP_G else nc.vector
                for t in range(first, last):
                    z = z_tiles[u][:, t, :]
                    engine.tensor_scalar(out=z, in0=z, scalar1=z_max[:, u, t : t + 1], scalar2=1.0, op0=ALU.min, op1=ALU.max)
            else:
                ts1(z, z, 1.0, ALU.max)

        def product(u):
            ensure(u)
            for t in range(TILES):
                product_tile(u, t)
                trickle()
                if u in CLIP_G:
                    clip(u, t, t + 1)

        def roots(u):
            a = work.tile([P, TILES, ROWS], F32, tag="a", bufs=A_BUFS, name="a")
            a_tiles[u] = a
            z = z_tiles[u]
            for t in range(TILES):
                nc.scalar.activation(out=a[:, t, :], in_=z[:, t, :], func=AF.Sqrt, scale=beta[:, u, t : t + 1], bias=neg_beta[:, u, t : t + 1])
            for t in range(TILES):
                scale = beta[:, u, t : t + 1]
                nc.scalar.activation(out=z[:, t, :], in_=z[:, t, :], func=AF.Sqrt, scale=scale, bias=one_minus_beta[:, u, t : t + 1])

        def add_roots(u):
            if u in GPSIMD_ADDS:
                nc.gpsimd.tensor_tensor(out=z_tiles[u][:], in0=a_tiles[u][:], in1=z_tiles[u][:], op=ALU.add)
            elif u in VECTOR_ADDS:
                tt(z_tiles[u][:], a_tiles[u][:], z_tiles[u][:], ALU.add)

        def turn(u, r):
            bank = psum.tile([P, UNIT], F32, tag="sum", bufs=4, name="bank")
            sum_banks[(u, r)] = bank
            rows = slice(r * P, (r + 1) * P)
            for t in range(TILES):
                block = bank[:, t * P : (t + 1) * P]
                if u in VECTOR_ADDS:
                    nc.tensor.transpose(block, z_tiles[u][:, t, rows], ident[:])
                else:
                    nc.tensor.matmul(out=block, lhsT=a_tiles[u][:, t, rows], rhs=ident[:], start=True, stop=False, is_transpose=True)
                    nc.tensor.matmul(out=block, lhsT=z_tiles[u][:, t, rows], rhs=ident[:], start=False, stop=True, is_transpose=True)

        def logarithm(u, r):
            if r == 0:
                log_tiles[u] = work.tile([P, TILES, UNIT], F32, tag="log", bufs=LOG_BUFS, name="log", align_bytes=64)
            nc.scalar.activation(out=log_tiles[u][:, r, :], in_=sum_banks[(u, r)][:], func=AF.Ln)

        lagging = []

        def scalar_square(u, r):
            square(u, r, r + 1)
            if u == N_UNITS - 1:
                finish(u, r, r + 1)
            elif r == TILES - 1:
                finish(u)

        def bias_of(u, pieces):
            row = fb[:, u * UNIT : (u + 1) * UNIT]
            return row if pieces == 1 else row.unsqueeze(1).to_broadcast([P, pieces, UNIT])

        def square(u, first=0, last=TILES):
            part = log_tiles[u][:, first:last, :]
            if u in SQUARE_G:
                for r in range(first, last, SQUARE_STEP):
                    piece = log_tiles[u][:, r : min(r + SQUARE_STEP, last), :]
                    nc.gpsimd.tensor_tensor(out=piece, in0=piece, in1=piece, op=ALU.mult)
            elif u in SQUARE_S:
                for r in range(first, last):
                    nc.scalar.activation(out=log_tiles[u][:, r, :], in_=log_tiles[u][:, r, :], func=AF.Square)
            else:
                stt(part, part, minus_four_over_t2[:], part, ALU.mult, ALU.mult)

        def finish(u, first=0, last=TILES):
            n = last - first
            part = log_tiles[u][:, first, :] if n == 1 else log_tiles[u][:, first:last, :]
            if u in SQUARE_G or u in SQUARE_S:
                stt(part, part, minus_four_over_t2[:], bias_of(u, n), ALU.mult, ALU.add)
            else:
                stt(part, part, q_min[:], bias_of(u, n), ALU.max, ALU.add)
            nc.sync.dma_start(out=out_view[u][:, first, :] if n == 1 else out_view[u][:, first:last, :], in_=part)

        reached = [0, 2]

        def advance():
            u, w = reached
            if w < N_UNITS:
                turn_words(w)
            if u < N_UNITS:
                product(u)
            if w < N_UNITS:
                for i in range(2):
                    word_copy("vector", banks[w][i], grouped[w], i)
                    trickle()
            if u < N_UNITS and u not in CLIP_G:
                clip(u)
            if w < N_UNITS:
                quantise_words(w)
            reached[0] = u + 1
            reached[1] = w + 1

        def first_unit():
            ensure(0)
            for t in range(TILES):
                product_tile(0, t)
                if t > 0:
                    clip(0, t - 1, t)
            quantise_words(1)
            clip(0, 3, 4)
            reached[0] = 1

        if STAGE_ONE_PINS:
            with tc.manual_schedule(engines=STAGE_ONE_PINS):
                stage_one()
                if PIN_FIRST:
                    first_unit()
        else:
            stage_one()
        if not PIN_FIRST:
            first_unit()
        advance()
        fb = work.tile([P, CODES], BF16, tag="b_part", bufs=1, name="fb")
        nc.gpsimd.dma_start(out=fb[:], in_=freq_bias.partition_broadcast(P))
        first = 0
        pending = []
        for g in range(len(GROUPS)):
            last = first + GROUPS[g] - 1
            for u in range(first, last + 1):
                roots(u)
                if u == first + TURN_AT:
                    for r in range(TILES):
                        turn(first, r)
                for i in range(ADV_ROOT[g][u - first]):
                    advance()
                if u > first:
                    add_roots(u - 1)
                fill(ROOT_SUMS[g][u - first])
                if pending and u - first >= FINISH_FROM:
                    finish(pending.pop(0))
            add_roots(last)
            for u in range(first, last + 1):
                for i in range(VECTOR_SUMS[g][u - first]):
                    if vector_sums:
                        sum_vector(*vector_sums.pop(0))
                        trickle()
                for r in range(TILES):
                    logarithm(u, r)
                    if u < last:
                        turn(u + 1, r)
                    if r < LOG_SUMS[g]:
                        fill(1)
                    if u in SQUARE_S:
                        lagging.append((u, r))
                        if len(lagging) > 1:
                            scalar_square(*lagging.pop(0))
                        if u == last and r == TILES - 1:
                            scalar_square(*lagging.pop(0))
                    elif u in SQUARE_G and (r + 1) % SQUARE_STEP == 0:
                        square(u, r + 1 - SQUARE_STEP, r + 1)
                if u not in SQUARE_S:
                    if u not in SQUARE_G:
                        square(u)
                    pending.append(u)
                    if len(pending) > KEEP:
                        finish(pending.pop(0))
                for i in range(ADV_LOG[g][u - first]):
                    advance()
            first = last + 1
        while pending:
            finish(pending.pop(0))
